import numpy as np
import ml_dtypes


def mxq(x, axis, fmt="e4m3"):
    dtype, down = {"e4m3": (ml_dtypes.float8_e4m3fn, 7), "e5m2": (ml_dtypes.float8_e5m2, 14)}[fmt]
    v = np.moveaxis(np.asarray(x, np.float32).astype(ml_dtypes.bfloat16).astype(np.float64), axis, -1)
    blocks = v.reshape(v.shape[:-1] + (-1, 32))
    amax = np.abs(blocks).max(-1, keepdims=True)
    byte = np.maximum(np.where(amax > 0, np.frexp(amax)[1] - 1 + 127, 0) - down, 1)
    scale = np.exp2(byte - 127.0)
    codes = (blocks / scale).astype(np.float32).astype(dtype).astype(np.float64)
    return np.moveaxis((codes * scale).reshape(v.shape), -1, axis)


WIDE = False


def mx_kscale(k):
    if not WIDE:
        return np.ones(k)
    levels = np.array([10, -10, 5, -5, 0])
    a = np.random.permutation(np.resize(levels, k // 512 * 4)).reshape(k // 512, 4)
    idx = np.arange(k)
    return np.exp2(a[idx // 512, idx % 128 // 32])


BF16 = ml_dtypes.bfloat16


def bf(x):
    return np.asarray(x, np.float32).astype(BF16)


def f64(x):
    return np.asarray(x).astype(np.float64)


B, F, P, T = 2, 1024, 512, 4096


def setup_inputs():
    s = np.asarray(mx_kscale(F), np.float64)
    u = np.random.uniform(size=(B, F, P))
    pe = u * 2.0 * T / F
    tm = np.random.uniform(-0.02, 1.02, size=(B, F, 1))
    cf = np.random.uniform(size=(B, F, 1))
    sg = (2.0 * T / F) * (1.0 + 0.1 * np.random.standard_normal(1))
    if np.any(s != 1.0):
        sg = np.array([2.0 ** -5])
        a = np.log2(s / s.min())[None, :, None]
        d = np.where(a > 0, sg[0] * np.sqrt(2.0 * np.log(np.maximum(2.0 ** a - 1.0, 1.0) * 1e10)), 0.0)
        tm = (np.random.randint(0, 4, size=(B, F, 1)) + d) / T
        c = f64(bf(tm)) * T
        gp = np.exp(-0.5 * ((c - np.round(c)) / sg[0]) ** 2)
        pe = u * (64.0 / F) * (gp + 1e-10) / gp
    return {"flashes_pe": bf(pe),
            "flashes_time": bf(tm),
            "flashes_confidence": bf(cf),
            "num_ticks": T,
            "sigma": bf(sg)}


def reference(flashes_pe, flashes_time, flashes_confidence, num_ticks, sigma):
    time_bins = np.clip(f64(flashes_time) * num_ticks, 0.0, num_ticks - 1)[..., 0]
    ticks = np.arange(num_ticks, dtype=np.float64)
    z = (ticks[None, None, :] - time_bins[..., None]) / f64(sigma)
    w = np.exp(-0.5 * z * z)
    w = w / (w.sum(axis=2, keepdims=True) + 1e-10)
    scaled_pe = f64(flashes_pe) * f64(flashes_confidence)
    return mxq(scaled_pe, 1, "e4m3").transpose(0, 2, 1) @ mxq(w, 1, "e4m3")

@@ -1,0 +1,180 @@
+from contextlib import ExitStack
+
+import concourse.mybir as mybir
+
+F32 = mybir.dt.float32
+BF16 = mybir.dt.bfloat16
+U32 = mybir.dt.uint32
+U8 = mybir.dt.uint8
+I32 = mybir.dt.int32
+FP8X4 = mybir.dt.float8_e4m3fn_x4
+ACT = mybir.ActivationFunctionType
+ALU = mybir.AluOpType
+
+P = 128
+PACK = 4
+EVENTS = 2
+FLASHES = 1024
+CHANNELS = 512
+TICKS = 4096
+K_PASS = P * PACK
+PASSES = FLASHES // K_PASS
+GROUPS = EVENTS * PASSES
+CHUNK = 1024
+N_CHUNKS = TICKS // CHUNK
+N_TILE = 512
+M_TILES = CHANNELS // P
+
+FLOPS = 2 * EVENTS * FLASHES * CHANNELS * TICKS
+
+
+def tile_flashrecomodel_t_kernel(tc, flashes_pe, flashes_time, flashes_confidence, num_ticks, sigma, out):
+    nc = tc.nc
+    assert num_ticks == TICKS
+    with ExitStack() as ctx:
+        const = ctx.enter_context(tc.tile_pool(name="const", bufs=1))
+        gpool = ctx.enter_context(tc.tile_pool(name="gpool", bufs=3))
+        wjpool = ctx.enter_context(tc.tile_pool(name="wjpool", bufs=2))
+        wchpool = ctx.enter_context(tc.tile_pool(name="wchpool", bufs=2))
+        c0pool = ctx.enter_context(tc.tile_pool(name="c0pool", bufs=1))
+        c1pool = ctx.enter_context(tc.tile_pool(name="c1pool", bufs=2))
+        spool = ctx.enter_context(tc.tile_pool(name="spool", bufs=2))
+        stpool = ctx.enter_context(tc.tile_pool(name="stpool", bufs=4))
+        psum = ctx.enter_context(tc.psum_pool(name="psum", bufs=8))
+
+        tm_bf = const.tile([P, GROUPS, PACK], BF16)
+        nc.sync.dma_start(
+            out=tm_bf[:], in_=flashes_time.rearrange("b (c p j) o -> p (b c) (j o)", p=P, j=PACK)
+        )
+        sig_bf = const.tile([P, 1], BF16)
+        nc.sync.dma_start(out=sig_bf[:], in_=sigma.partition_broadcast(P))
+        cf_bf = const.tile([P, GROUPS, PACK], BF16)
+        nc.sync.dma_start(
+            out=cf_bf[:], in_=flashes_confidence.rearrange("b (c p j) o -> p (b c) (j o)", p=P, j=PACK)
+        )
+        pe_raw = const.tile([P, GROUPS, PACK, CHANNELS], BF16)
+        nc.sync.dma_start(
+            out=pe_raw[:].rearrange("p g j w -> p g (j w)"),
+            in_=flashes_pe.rearrange("b (c p j) w -> p (b c) (j w)", p=P, j=PACK),
+        )
+
+        seed = 128
+        tick_i = const.tile([P, seed], I32)
+        nc.gpsimd.iota(tick_i[:], pattern=[[1, seed]], base=0, channel_multiplier=0)
+        ticks = const.tile([P, TICKS], F32)
+        nc.vector.tensor_copy(out=ticks[:, 0:seed], in_=tick_i[:])
+        have = seed
+        while have < TICKS:
+            nc.vector.tensor_scalar_add(out=ticks[:, have : 2 * have], in0=ticks[:, 0:have], scalar1=float(have))
+            have *= 2
+
+        negc = const.tile([P, GROUPS * PACK], F32)
+        nc.vector.tensor_scalar(
+            out=negc[:], in0=tm_bf[:].rearrange("p g j -> p (g j)"), scalar1=-float(TICKS), scalar2=0.0,
+            op0=ALU.mult, op1=ALU.min,
+        )
+        nc.vector.tensor_scalar_max(out=negc[:], in0=negc[:], scalar1=-float(TICKS - 1))
+        sig2 = const.tile([P, 1], F32)
+        nc.vector.tensor_tensor(out=sig2[:], in0=sig_bf[:], in1=sig_bf[:], op=ALU.mult)
+        inv2 = const.tile([P, 1], F32)
+        nc.vector.reciprocal(out=inv2[:], in_=sig2[:])
+        neg_h = const.tile([P, 1], F32)
+        nc.vector.tensor_scalar_mul(out=neg_h[:], in0=inv2[:], scalar1=-0.5)
+
+        sums = const.tile([P, GROUPS * PACK], F32)
+        sums_eps = const.tile([P, GROUPS * PACK], F32)
+        recip = const.tile([P, GROUPS * PACK], F32)
+
+        cf32 = const.tile([P, GROUPS, PACK], F32)
+        nc.vector.tensor_copy(out=cf32[:], in_=cf_bf[:])
+        pe_codes = []
+        pe_scales = []
+        for g in range(GROUPS):
+            spe = spool.tile([P, CHANNELS, PACK], BF16, align_bytes=64)
+            nc.gpsimd.tensor_tensor(
+                out=spe[:],
+                in0=pe_raw[:, g].rearrange("p j w -> p w j"),
+                in1=cf32[:, g].unsqueeze(1).to_broadcast([P, CHANNELS, PACK]),
+                op=ALU.mult,
+            )
+            codes = const.tile([P, CHANNELS], U32, name="pe_codes%d" % g, align_bytes=64)
+            scales = const.tile([P, CHANNELS], U8, name="pe_scales%d" % g, align_bytes=64)
+            nc.vector.quantize_mx(
+                out=codes[:].bitcast(FP8X4), scales=scales[:], in_=spe[:].rearrange("p w j -> p (w j)")
+            )
+            pe_codes.append(codes)
+            pe_scales.append(scales)
+
+        c0_codes = {}
+        c0_scales = {}
+
+        def quantise(g, n, wch):
+            if g % PASSES == 0:
+                codes = c0pool.tile([P, CHUNK], U32, name="c0_codes%d" % n, align_bytes=64)
+                scales = c0pool.tile([P, CHUNK], U8, name="c0_scales%d" % n, align_bytes=64)
+                c0_codes[n] = codes
+                c0_scales[n] = scales
+            else:
+                codes = c1pool.tile([P, CHUNK], U32, name="c1_codes", align_bytes=64)
+                scales = c1pool.tile([P, CHUNK], U8, name="c1_scales", align_bytes=64)
+            nc.vector.quantize_mx(
+                out=codes[:].bitcast(FP8X4), scales=scales[:], in_=wch[:].rearrange("p t j -> p (t j)")
+            )
+            return codes, scales
+
+        def multiply(b, n, codes, scales):
+            for m in range(M_TILES):
+                m_cols = slice(m * P, (m + 1) * P)
+                stage = stpool.tile([P, CHUNK], F32, name="stage")
+                for h in range(CHUNK // N_TILE):
+                    n_cols = slice(h * N_TILE, (h + 1) * N_TILE)
+                    acc = psum.tile([P, N_TILE], F32, name="acc")
+                    nc.tensor.matmul_mx(
+                        out=acc[:],
+                        lhsT=pe_codes[b * PASSES][:, m_cols].bitcast(FP8X4),
+                        lhsT_scale=pe_scales[b * PASSES][:, m_cols],
+                        rhs=c0_codes[n][:, n_cols].bitcast(FP8X4),
+                        rhs_scale=c0_scales[n][:, n_cols],
+                        start=True,
+                        stop=False,
+                    )
+                    nc.tensor.matmul_mx(
+                        out=acc[:],
+                        lhsT=pe_codes[b * PASSES + 1][:, m_cols].bitcast(FP8X4),
+                        lhsT_scale=pe_scales[b * PASSES + 1][:, m_cols],
+                        rhs=codes[:, n_cols].bitcast(FP8X4),
+                        rhs_scale=scales[:, n_cols],
+                        start=False,
+                        stop=True,
+                    )
+                    if b == 0:
+                        nc.vector.tensor_copy(out=stage[:, n_cols], in_=acc[:])
+                    else:
+                        nc.scalar.copy(out=stage[:, n_cols], in_=acc[:])
+                nc.sync.dma_start(out=out[b, m_cols, n * CHUNK : (n + 1) * CHUNK], in_=stage[:])
+
+        for g in range(GROUPS):
+            b = g // PASSES
+            wj = wjpool.tile([P, PACK, TICKS], BF16, name="wj")
+            for j in range(PACK):
+                col = slice(g * PACK + j, g * PACK + j + 1)
+                gt = gpool.tile([P, TICKS], F32, name="gt")
+                nc.scalar.activation(out=gt[:], in_=ticks[:], func=ACT.Square, bias=negc[:, col], scale=1.0)
+                nc.scalar.activation(out=gt[:], in_=gt[:], func=ACT.Exp, scale=neg_h[:, 0:1], accum_out=sums[:, col])
+                nc.vector.tensor_scalar_add(out=sums_eps[:, col], in0=sums[:, col], scalar1=1e-10)
+                nc.vector.reciprocal(out=recip[:, col], in_=sums_eps[:, col])
+                nc.vector.tensor_scalar_mul(out=wj[:, j, :], in0=gt[:], scalar1=recip[:, col])
+            pending = None
+            for n in range(N_CHUNKS + 1):
+                wch = None
+                if n < N_CHUNKS:
+                    wch = wchpool.tile([P, CHUNK, PACK], BF16, name="wch", align_bytes=64)
+                    nc.vector.tensor_copy(
+                        out=wch[:].rearrange("p (c i) j -> p c j i", i=4),
+                        in_=wj[:, :, n * CHUNK : (n + 1) * CHUNK].rearrange("p j (c i) -> p c j i", i=4),
+                    )
+                if pending is not None:
+                    codes, scales = quantise(g, n - 1, pending)
+                    if g % PASSES == PASSES - 1:
+                        multiply(b, n - 1, codes, scales)
+                pending = wch

@@ -1,6 +1,7 @@
 from contextlib import ExitStack
 
 import concourse.mybir as mybir
+from concourse.masks import make_identity
 
 F32 = mybir.dt.float32
 BF16 = mybir.dt.bfloat16
@@ -10,6 +11,7 @@ I32 = mybir.dt.int32
 FP8X4 = mybir.dt.float8_e4m3fn_x4
 ACT = mybir.ActivationFunctionType
 ALU = mybir.AluOpType
+AX = mybir.AxisListType
 
 P = 128
 PACK = 4
@@ -20,10 +22,16 @@ TICKS = 4096
 K_PASS = P * PACK
 PASSES = FLASHES // K_PASS
 GROUPS = EVENTS * PASSES
+TILES = GROUPS * PACK
 CHUNK = 1024
 N_CHUNKS = TICKS // CHUNK
 N_TILE = 512
-M_TILES = CHANNELS // P
+WINDOW = 1536
+W_BANKS = WINDOW // N_TILE
+W_BLOCKS = WINDOW // P
+PARTS = W_BANKS + 1
+VECTOR_SQUARES = (2, 3)
+UNIT_PERIODS = {9: (0,), 10: (1,), 11: (2,), 12: (3, 4), 13: (5,), 14: (6,), 15: (7,)}
 
 FLOPS = 2 * EVENTS * FLASHES * CHANNELS * TICKS
 
@@ -32,149 +40,350 @@ def tile_flashrecomodel_t_kernel(tc, flashes_pe, flashes_time, flashes_confidenc
     nc = tc.nc
     assert num_ticks == TICKS
     with ExitStack() as ctx:
+        ctx.enter_context(tc.manual_schedule())
         const = ctx.enter_context(tc.tile_pool(name="const", bufs=1))
         gpool = ctx.enter_context(tc.tile_pool(name="gpool", bufs=3))
         wjpool = ctx.enter_context(tc.tile_pool(name="wjpool", bufs=2))
         wchpool = ctx.enter_context(tc.tile_pool(name="wchpool", bufs=2))
         c0pool = ctx.enter_context(tc.tile_pool(name="c0pool", bufs=1))
-        c1pool = ctx.enter_context(tc.tile_pool(name="c1pool", bufs=2))
-        spool = ctx.enter_context(tc.tile_pool(name="spool", bufs=2))
-        stpool = ctx.enter_context(tc.tile_pool(name="stpool", bufs=4))
-        psum = ctx.enter_context(tc.psum_pool(name="psum", bufs=8))
+        dqpool = ctx.enter_context(tc.psum_pool(name="dqpool", bufs=1))
+        accpool = ctx.enter_context(tc.psum_pool(name="accpool", bufs=5))
 
-        tm_bf = const.tile([P, GROUPS, PACK], BF16)
-        nc.sync.dma_start(
-            out=tm_bf[:], in_=flashes_time.rearrange("b (c p j) o -> p (b c) (j o)", p=P, j=PACK)
-        )
-        sig_bf = const.tile([P, 1], BF16)
-        nc.sync.dma_start(out=sig_bf[:], in_=sigma.partition_broadcast(P))
-        cf_bf = const.tile([P, GROUPS, PACK], BF16)
-        nc.sync.dma_start(
-            out=cf_bf[:], in_=flashes_confidence.rearrange("b (c p j) o -> p (b c) (j o)", p=P, j=PACK)
-        )
-        pe_raw = const.tile([P, GROUPS, PACK, CHANNELS], BF16)
-        nc.sync.dma_start(
-            out=pe_raw[:].rearrange("p g j w -> p g (j w)"),
-            in_=flashes_pe.rearrange("b (c p j) w -> p (b c) (j w)", p=P, j=PACK),
-        )
-
-        seed = 128
-        tick_i = const.tile([P, seed], I32)
-        nc.gpsimd.iota(tick_i[:], pattern=[[1, seed]], base=0, channel_multiplier=0)
         ticks = const.tile([P, TICKS], F32)
-        nc.vector.tensor_copy(out=ticks[:, 0:seed], in_=tick_i[:])
-        have = seed
-        while have < TICKS:
-            nc.vector.tensor_scalar_add(out=ticks[:, have : 2 * have], in0=ticks[:, 0:have], scalar1=float(have))
-            have *= 2
-
-        negc = const.tile([P, GROUPS * PACK], F32)
-        nc.vector.tensor_scalar(
-            out=negc[:], in0=tm_bf[:].rearrange("p g j -> p (g j)"), scalar1=-float(TICKS), scalar2=0.0,
-            op0=ALU.mult, op1=ALU.min,
-        )
-        nc.vector.tensor_scalar_max(out=negc[:], in0=negc[:], scalar1=-float(TICKS - 1))
-        sig2 = const.tile([P, 1], F32)
-        nc.vector.tensor_tensor(out=sig2[:], in0=sig_bf[:], in1=sig_bf[:], op=ALU.mult)
-        inv2 = const.tile([P, 1], F32)
-        nc.vector.reciprocal(out=inv2[:], in_=sig2[:])
+        negc = const.tile([P, TILES], F32)
         neg_h = const.tile([P, 1], F32)
-        nc.vector.tensor_scalar_mul(out=neg_h[:], in0=inv2[:], scalar1=-0.5)
-
-        sums = const.tile([P, GROUPS * PACK], F32)
-        sums_eps = const.tile([P, GROUPS * PACK], F32)
-        recip = const.tile([P, GROUPS * PACK], F32)
-
-        cf32 = const.tile([P, GROUPS, PACK], F32)
-        nc.vector.tensor_copy(out=cf32[:], in_=cf_bf[:])
+        parts = []
+        sums = []
+        sums_eps = []
+        recip = []
+        for i in range(TILES):
+            parts.append(const.tile([P, PARTS], F32, name="parts%d" % i))
+            sums.append(const.tile([P, 1], F32, name="sums%d" % i))
+            sums_eps.append(const.tile([P, 1], F32, name="sums_eps%d" % i))
+            recip.append(const.tile([P, 1], F32, name="recip%d" % i))
+        ident = const.tile([P, P], BF16)
+        tick_rows = const.tile([P, WINDOW], BF16)
+        flash_rows = const.tile([P, TILES * P], BF16)
         pe_codes = []
         pe_scales = []
         for g in range(GROUPS):
-            spe = spool.tile([P, CHANNELS, PACK], BF16, align_bytes=64)
-            nc.gpsimd.tensor_tensor(
-                out=spe[:],
-                in0=pe_raw[:, g].rearrange("p j w -> p w j"),
-                in1=cf32[:, g].unsqueeze(1).to_broadcast([P, CHANNELS, PACK]),
-                op=ALU.mult,
+            pe_codes.append(const.tile([P, CHANNELS], U32, name="pe_codes%d" % g, align_bytes=64))
+            pe_scales.append(const.tile([P, CHANNELS], U8, name="pe_scales%d" % g, align_bytes=64))
+
+        gts = {}
+        dqs = {}
+        wjs = {}
+        wchs = {}
+        w_codes = {}
+        w_scales = {}
+        late = {}
+        rest = slice(WINDOW, TICKS)
+
+        def g_tile(i):
+            if i not in gts:
+                gts[i] = gpool.tile([P, TICKS], F32, name="gt")
+            return gts[i]
+
+        def square_scalar(i):
+            nc.scalar.activation(
+                out=g_tile(i)[:, rest], in_=ticks[:, rest], func=ACT.Square, bias=negc[:, i : i + 1], scale=1.0
             )
-            codes = const.tile([P, CHANNELS], U32, name="pe_codes%d" % g, align_bytes=64)
-            scales = const.tile([P, CHANNELS], U8, name="pe_scales%d" % g, align_bytes=64)
+
+        def square_vector(i):
+            gt = g_tile(i)
+            nc.vector.tensor_scalar_add(out=gt[:, rest], in0=ticks[:, rest], scalar1=negc[:, i : i + 1])
+            nc.vector.tensor_tensor(out=gt[:, rest], in0=gt[:, rest], in1=gt[:, rest], op=ALU.mult)
+
+        def exp_rest(i):
+            gt = g_tile(i)
+            nc.scalar.activation(
+                out=gt[:, rest], in_=gt[:, rest], func=ACT.Exp, scale=neg_h[:, 0:1],
+                accum_out=parts[i][:, W_BANKS : W_BANKS + 1],
+            )
+
+        def square_tensor(i, u):
+            dq = dqpool.tile([P, N_TILE], F32, name="dq%d" % u)
+            dqs[u] = dq
+            nc.tensor.matmul(
+                out=dq[:],
+                lhsT=flash_rows[:, i * P : (i + 1) * P],
+                rhs=tick_rows[:, u * N_TILE : (u + 1) * N_TILE],
+                start=True,
+                stop=True,
+            )
+
+        def exp_window(i):
+            gt = g_tile(i)
+            for u in range(W_BANKS):
+                nc.scalar.activation(
+                    out=gt[:, u * N_TILE : (u + 1) * N_TILE], in_=dqs[u][:], func=ACT.Exp, scale=neg_h[:, 0:1],
+                    accum_out=parts[i][:, u : u + 1],
+                )
+                if i + 1 < TILES:
+                    square_tensor(i + 1, u)
+
+        def reciprocal_of_sum(i):
+            nc.vector.reduce_sum(out=sums[i][:], in_=parts[i][:], axis=AX.X)
+            nc.vector.tensor_scalar_add(out=sums_eps[i][:], in0=sums[i][:], scalar1=1e-10)
+            nc.vector.reciprocal(out=recip[i][:], in_=sums_eps[i][:])
+
+        def normalise(i, cols):
+            g, j = divmod(i, PACK)
+            if g not in wjs:
+                wjs[g] = wjpool.tile([P, PACK, TICKS], BF16, name="wj")
+            nc.vector.tensor_scalar_mul(out=wjs[g][:, j, cols], in0=gts[i][:, cols], scalar1=recip[i][:, 0:1])
+
+        def finish_tile(i):
+            reciprocal_of_sum(i)
+            normalise(i, slice(0, TICKS))
+
+        def regroup(k):
+            g, n = divmod(k, N_CHUNKS)
+            wch = wchpool.tile([P, CHUNK, PACK], BF16, name="wch", align_bytes=64)
+            wchs[k] = wch
+            nc.vector.tensor_copy(
+                out=wch[:].rearrange("p (c i) j -> p c j i", i=4),
+                in_=wjs[g][:, :, n * CHUNK : (n + 1) * CHUNK].rearrange("p j (c i) -> p c j i", i=4),
+            )
+
+        def quantise(k):
+            g, n = divmod(k, N_CHUNKS)
+            c = g % PASSES
+            pool = c0pool if c == 0 else late["c1pool"]
+            codes = pool.tile([P, CHUNK], U32, name="w_codes%d_%d" % (c, n), align_bytes=64)
+            scales = pool.tile([P, CHUNK], U8, name="w_scales%d_%d" % (c, n), align_bytes=64)
+            w_codes[(c, n)] = codes
+            w_scales[(c, n)] = scales
             nc.vector.quantize_mx(
-                out=codes[:].bitcast(FP8X4), scales=scales[:], in_=spe[:].rearrange("p w j -> p (w j)")
+                out=codes[:].bitcast(FP8X4), scales=scales[:], in_=wchs[k][:].rearrange("p t j -> p (t j)")
             )
-            pe_codes.append(codes)
-            pe_scales.append(scales)
 
-        c0_codes = {}
-        c0_scales = {}
+        banks = [0]
 
-        def quantise(g, n, wch):
-            if g % PASSES == 0:
-                codes = c0pool.tile([P, CHUNK], U32, name="c0_codes%d" % n, align_bytes=64)
-                scales = c0pool.tile([P, CHUNK], U8, name="c0_scales%d" % n, align_bytes=64)
-                c0_codes[n] = codes
-                c0_scales[n] = scales
-            else:
-                codes = c1pool.tile([P, CHUNK], U32, name="c1_codes", align_bytes=64)
-                scales = c1pool.tile([P, CHUNK], U8, name="c1_scales", align_bytes=64)
-            nc.vector.quantize_mx(
-                out=codes[:].bitcast(FP8X4), scales=scales[:], in_=wch[:].rearrange("p t j -> p (t j)")
-            )
-            return codes, scales
+        def bank(all_eight):
+            q = banks[0] % 8
+            banks[0] += 1
+            if all_eight and q >= 5:
+                return dqpool.tile([P, N_TILE], F32, name="acc_dq", tag="dq%d" % (q - 5))
+            return accpool.tile([P, N_TILE], F32, name="acc")
 
-        def multiply(b, n, codes, scales):
-            for m in range(M_TILES):
+        def unit(b, v, engines, all_eight):
+            n, half = divmod(v, 2)
+            for mm in range(2):
+                m = 2 * half + mm
                 m_cols = slice(m * P, (m + 1) * P)
-                stage = stpool.tile([P, CHUNK], F32, name="stage")
-                for h in range(CHUNK // N_TILE):
+                stage = late["stpool"].tile([P, CHUNK], F32, name="stage")
+                for h in range(2):
                     n_cols = slice(h * N_TILE, (h + 1) * N_TILE)
-                    acc = psum.tile([P, N_TILE], F32, name="acc")
-                    nc.tensor.matmul_mx(
-                        out=acc[:],
-                        lhsT=pe_codes[b * PASSES][:, m_cols].bitcast(FP8X4),
-                        lhsT_scale=pe_scales[b * PASSES][:, m_cols],
-                        rhs=c0_codes[n][:, n_cols].bitcast(FP8X4),
-                        rhs_scale=c0_scales[n][:, n_cols],
-                        start=True,
-                        stop=False,
-                    )
-                    nc.tensor.matmul_mx(
-                        out=acc[:],
-                        lhsT=pe_codes[b * PASSES + 1][:, m_cols].bitcast(FP8X4),
-                        lhsT_scale=pe_scales[b * PASSES + 1][:, m_cols],
-                        rhs=codes[:, n_cols].bitcast(FP8X4),
-                        rhs_scale=scales[:, n_cols],
-                        start=False,
-                        stop=True,
-                    )
-                    if b == 0:
+                    acc = bank(all_eight)
+                    for c in range(PASSES):
+                        nc.tensor.matmul_mx(
+                            out=acc[:],
+                            lhsT=pe_codes[b * PASSES + c][:, m_cols].bitcast(FP8X4),
+                            lhsT_scale=pe_scales[b * PASSES + c][:, m_cols],
+                            rhs=w_codes[(c, n)][:, n_cols].bitcast(FP8X4),
+                            rhs_scale=w_scales[(c, n)][:, n_cols],
+                            start=(c == 0),
+                            stop=(c == PASSES - 1),
+                        )
+                    if engines[2 * mm + h] == "V":
                         nc.vector.tensor_copy(out=stage[:, n_cols], in_=acc[:])
                     else:
                         nc.scalar.copy(out=stage[:, n_cols], in_=acc[:])
                 nc.sync.dma_start(out=out[b, m_cols, n * CHUNK : (n + 1) * CHUNK], in_=stage[:])
 
-        for g in range(GROUPS):
-            b = g // PASSES
-            wj = wjpool.tile([P, PACK, TICKS], BF16, name="wj")
-            for j in range(PACK):
-                col = slice(g * PACK + j, g * PACK + j + 1)
-                gt = gpool.tile([P, TICKS], F32, name="gt")
-                nc.scalar.activation(out=gt[:], in_=ticks[:], func=ACT.Square, bias=negc[:, col], scale=1.0)
-                nc.scalar.activation(out=gt[:], in_=gt[:], func=ACT.Exp, scale=neg_h[:, 0:1], accum_out=sums[:, col])
-                nc.vector.tensor_scalar_add(out=sums_eps[:, col], in0=sums[:, col], scalar1=1e-10)
-                nc.vector.reciprocal(out=recip[:, col], in_=sums_eps[:, col])
-                nc.vector.tensor_scalar_mul(out=wj[:, j, :], in0=gt[:], scalar1=recip[:, col])
-            pending = None
-            for n in range(N_CHUNKS + 1):
-                wch = None
-                if n < N_CHUNKS:
-                    wch = wchpool.tile([P, CHUNK, PACK], BF16, name="wch", align_bytes=64)
-                    nc.vector.tensor_copy(
-                        out=wch[:].rearrange("p (c i) j -> p c j i", i=4),
-                        in_=wj[:, :, n * CHUNK : (n + 1) * CHUNK].rearrange("p j (c i) -> p c j i", i=4),
-                    )
-                if pending is not None:
-                    codes, scales = quantise(g, n - 1, pending)
-                    if g % PASSES == PASSES - 1:
-                        multiply(b, n - 1, codes, scales)
-                pending = wch
+        def period(i, extra):
+            exp_window(i)
+            square_scalar(i)
+            exp_rest(i)
+            k = i - PACK
+            if k >= 1:
+                quantise(k - 1)
+            regroup(k)
+            extra(i)
+            for v in UNIT_PERIODS.get(i, ()):
+                unit(0, v, "VVVA", False)
+
+        with tc.tile_pool(name="prep", bufs=1) as prep:
+            tm_bf = prep.tile([P, GROUPS, PACK], BF16)
+            nc.sync.dma_start(
+                out=tm_bf[:], in_=flashes_time.rearrange("b (c p j) o -> p (b c) (j o)", p=P, j=PACK)
+            )
+            sig_bf = prep.tile([P, 1], BF16)
+            nc.sync.dma_start(out=sig_bf[:], in_=sigma.partition_broadcast(P))
+            cf_bf = prep.tile([P, GROUPS, PACK], BF16)
+            nc.sync.dma_start(
+                out=cf_bf[:], in_=flashes_confidence.rearrange("b (c p j) o -> p (b c) (j o)", p=P, j=PACK)
+            )
+            pe_raw = prep.tile([P, GROUPS, PACK, CHANNELS], BF16)
+            pe_view = flashes_pe.rearrange("b (c p j) w -> p (b c) (j w)", p=P, j=PACK)
+            for g in range(GROUPS):
+                nc.sync.dma_start(out=pe_raw[:, g].rearrange("p j w -> p (j w)"), in_=pe_view[:, g])
+
+            seed = 128
+            tick_i = prep.tile([P, seed], I32)
+            nc.gpsimd.iota(tick_i[:], pattern=[[1, seed]], base=0, channel_multiplier=0)
+            warm = prep.tile([P, 1], F32)
+            nc.gpsimd.memset(warm[:], 0.0)
+            tcol_i = prep.tile([P, W_BLOCKS], I32)
+            nc.gpsimd.iota(tcol_i[:], pattern=[[P, W_BLOCKS]], base=0, channel_multiplier=1)
+            tick_cols = prep.tile([P, W_BLOCKS, P], BF16)
+            nc.gpsimd.memset(tick_cols[:].rearrange("p a k -> p (a k)").bitcast(F32), 0.0)
+            flash_cols = prep.tile([P, TILES, P], BF16)
+            nc.gpsimd.memset(flash_cols[:].rearrange("p a k -> p (a k)").bitcast(F32), 0.0)
+            make_identity(nc, ident[:])
+
+            warm_out = prep.tile([P, 1], F32)
+            nc.scalar.activation(out=warm_out[:], in_=warm[:], func=ACT.Exp)
+
+            nc.vector.tensor_copy(out=ticks[:, 0:seed], in_=tick_i[:])
+            have = seed
+            while have < TICKS:
+                nc.vector.tensor_scalar_add(out=ticks[:, have : 2 * have], in0=ticks[:, 0:have], scalar1=float(have))
+                have *= 2
+
+            nc.vector.tensor_scalar(
+                out=negc[:], in0=tm_bf[:].rearrange("p g j -> p (g j)"), scalar1=-float(TICKS), scalar2=0.0,
+                op0=ALU.mult, op1=ALU.min,
+            )
+            nc.vector.tensor_scalar_max(out=negc[:], in0=negc[:], scalar1=-float(TICKS - 1))
+            sig2 = prep.tile([P, 1], F32)
+            nc.vector.tensor_tensor(out=sig2[:], in0=sig_bf[:], in1=sig_bf[:], op=ALU.mult)
+            inv2 = prep.tile([P, 1], F32)
+            nc.vector.reciprocal(out=inv2[:], in_=sig2[:])
+            nc.vector.tensor_scalar_mul(out=neg_h[:], in0=inv2[:], scalar1=-0.5)
+
+            square_scalar(0)
+            exp_rest(0)
+            square_scalar(1)
+            exp_rest(1)
+
+            spes = []
+            for g in range(GROUPS):
+                spe = prep.tile([P, CHANNELS, PACK], BF16, name="spe%d" % g, align_bytes=64)
+                nc.gpsimd.tensor_tensor(
+                    out=spe[:],
+                    in0=pe_raw[:, g].rearrange("p j w -> p w j"),
+                    in1=cf_bf[:, g].unsqueeze(1).to_broadcast([P, CHANNELS, PACK]),
+                    op=ALU.mult,
+                )
+                spes.append(spe)
+
+            tcol = prep.tile([P, W_BLOCKS], F32)
+            nc.vector.tensor_copy(out=tcol[:], in_=tcol_i[:])
+            t_sq = prep.tile([P, W_BLOCKS], F32)
+            nc.vector.tensor_tensor(out=t_sq[:], in0=tcol[:], in1=tcol[:], op=ALU.mult)
+            nc.vector.tensor_copy(out=tick_cols[:, :, 0], in_=t_sq[:])
+            t_rem1 = prep.tile([P, W_BLOCKS], F32)
+            nc.vector.tensor_tensor(out=t_rem1[:], in0=t_sq[:], in1=tick_cols[:, :, 0], op=ALU.subtract)
+            nc.vector.tensor_copy(out=tick_cols[:, :, 1], in_=t_rem1[:])
+            t_rem2 = prep.tile([P, W_BLOCKS], F32)
+            nc.vector.tensor_tensor(out=t_rem2[:], in0=t_rem1[:], in1=tick_cols[:, :, 1], op=ALU.subtract)
+            nc.vector.tensor_copy(out=tick_cols[:, :, 2], in_=t_rem2[:])
+            nc.vector.tensor_copy(
+                out=tick_cols[:, :, 3:6:2], in_=tcol[:].unsqueeze(2).to_broadcast([P, W_BLOCKS, 2])
+            )
+            t_lo = prep.tile([P, W_BLOCKS], F32)
+            nc.vector.tensor_tensor(out=t_lo[:], in0=tcol[:], in1=tick_cols[:, :, 3], op=ALU.subtract)
+            nc.vector.tensor_copy(
+                out=tick_cols[:, :, 4:7:2], in_=t_lo[:].unsqueeze(2).to_broadcast([P, W_BLOCKS, 2])
+            )
+            nc.vector.memset(tick_cols[:, :, 7:10], 1.0)
+            tab0 = accpool.tile([P, 8 * P], BF16, name="tab0", tag="acc")
+            tab1 = accpool.tile([P, 8 * P], BF16, name="tab1", tag="acc")
+            for a in range(W_BLOCKS):
+                tab = tab0 if a < 8 else tab1
+                nc.tensor.transpose(tab[:, (a % 8) * P : (a % 8 + 1) * P], tick_cols[:, a, :], ident[:])
+
+            a_full = prep.tile([P, TILES], F32)
+            nc.vector.tensor_scalar_mul(out=a_full[:], in0=negc[:], scalar1=2.0)
+            nc.vector.tensor_copy(
+                out=flash_cols[:, :, 3:5], in_=a_full[:].unsqueeze(2).to_broadcast([P, TILES, 2])
+            )
+            a_lo = prep.tile([P, TILES], F32)
+            nc.vector.tensor_tensor(out=a_lo[:], in0=a_full[:], in1=flash_cols[:, :, 3], op=ALU.subtract)
+            nc.vector.tensor_copy(
+                out=flash_cols[:, :, 5:7], in_=a_lo[:].unsqueeze(2).to_broadcast([P, TILES, 2])
+            )
+            c_sq = prep.tile([P, TILES], F32)
+            nc.vector.tensor_tensor(out=c_sq[:], in0=negc[:], in1=negc[:], op=ALU.mult)
+            nc.vector.tensor_copy(out=flash_cols[:, :, 7], in_=c_sq[:])
+            c_rem1 = prep.tile([P, TILES], F32)
+            nc.vector.tensor_tensor(out=c_rem1[:], in0=c_sq[:], in1=flash_cols[:, :, 7], op=ALU.subtract)
+            nc.vector.tensor_copy(out=flash_cols[:, :, 8], in_=c_rem1[:])
+            c_rem2 = prep.tile([P, TILES], F32)
+            nc.vector.tensor_tensor(out=c_rem2[:], in0=c_rem1[:], in1=flash_cols[:, :, 8], op=ALU.subtract)
+            nc.vector.tensor_copy(out=flash_cols[:, :, 9], in_=c_rem2[:])
+            nc.vector.memset(flash_cols[:, :, 0:3], 1.0)
+            tab2 = accpool.tile([P, 8 * P], BF16, name="tab2", tag="acc")
+            tab3 = accpool.tile([P, 8 * P], BF16, name="tab3", tag="acc")
+            for a in range(TILES):
+                tab = tab2 if a < 8 else tab3
+                nc.tensor.transpose(tab[:, (a % 8) * P : (a % 8 + 1) * P], flash_cols[:, a, :], ident[:])
+
+            nc.vector.tensor_copy(out=tick_rows[:, 0 : 8 * P], in_=tab0[:])
+            nc.vector.tensor_copy(out=tick_rows[:, 8 * P : WINDOW], in_=tab1[:, 0 : WINDOW - 8 * P])
+            nc.vector.tensor_copy(out=flash_rows[:, 0 : 8 * P], in_=tab2[:])
+            nc.vector.tensor_copy(out=flash_rows[:, 8 * P : TILES * P], in_=tab3[:])
+
+            for u in range(W_BANKS):
+                square_tensor(0, u)
+            square_vector(2)
+            exp_window(0)
+            finish_tile(0)
+            square_vector(3)
+            exp_window(1)
+            finish_tile(1)
+            exp_window(2)
+            exp_rest(2)
+            finish_tile(2)
+            exp_window(3)
+            exp_rest(3)
+            finish_tile(3)
+
+            def quantise_pe(i):
+                g = i - PACK
+                nc.vector.quantize_mx(
+                    out=pe_codes[g][:].bitcast(FP8X4), scales=pe_scales[g][:],
+                    in_=spes[g][:].rearrange("p w j -> p (w j)"),
+                )
+
+            for i in range(PACK, 2 * PACK):
+                period(i, quantise_pe)
+                finish_tile(i)
+
+        with tc.tile_pool(name="c1pool", bufs=1) as c1pool, tc.tile_pool(name="stpool", bufs=4) as stpool:
+            late["c1pool"] = c1pool
+            late["stpool"] = stpool
+
+            def nothing(i):
+                return None
+
+            for i in range(2 * PACK, TILES):
+                period(i, nothing)
+                if i < TILES - 1:
+                    finish_tile(i)
+            last = TILES - 1
+            first_k = (GROUPS - 1) * N_CHUNKS
+            quantise(first_k - 1)
+            reciprocal_of_sum(last)
+            normalise(last, slice(0, CHUNK))
+            regroup(first_k)
+            quantise(first_k)
+            unit(1, 0, "AAAA", True)
+            normalise(last, slice(CHUNK, 2 * CHUNK))
+            regroup(first_k + 1)
+            unit(1, 1, "AAAA", True)
+            quantise(first_k + 1)
+            normalise(last, slice(2 * CHUNK, 3 * CHUNK))
+            regroup(first_k + 2)
+            unit(1, 2, "AAAA", True)
+            quantise(first_k + 2)
+            normalise(last, slice(3 * CHUNK, 4 * CHUNK))
+            regroup(first_k + 3)
+            unit(1, 3, "AAAA", True)
+            quantise(first_k + 3)
+            unit(1, 4, "AVAV", True)
+            unit(1, 5, "AVAV", True)
+            unit(1, 6, "AVAV", True)
+            unit(1, 7, "AVAV", True)

@@ -29,9 +29,9 @@ N_TILE = 512
 WINDOW = 1536
 W_BANKS = WINDOW // N_TILE
 W_BLOCKS = WINDOW // P
-PARTS = W_BANKS + 1
-VECTOR_SQUARES = (2, 3)
-UNIT_PERIODS = {9: (0,), 10: (1,), 11: (2,), 12: (3, 4), 13: (5,), 14: (6,), 15: (7,)}
+VECTOR_SQUARES = (2, 3, 6)
+UNIT_SLOTS = {10: (0, 1), 11: (2,), 12: (3,), 13: (4, 5), 14: (6,), 15: (7,)}
+LAST_BLOCKS = ((0, 256), (256, 256), (512, 512), (1024, 1024), (2048, 1024), (3072, 1024))
 
 FLOPS = 2 * EVENTS * FLASHES * CHANNELS * TICKS
 
@@ -53,13 +53,13 @@ def tile_flashrecomodel_t_kernel(tc, flashes_pe, flashes_time, flashes_confidenc
         negc = const.tile([P, TILES], F32)
         neg_h = const.tile([P, 1], F32)
         parts = []
-        sums = []
-        sums_eps = []
+        sum_win = []
+        sum_eps = []
         recip = []
         for i in range(TILES):
-            parts.append(const.tile([P, PARTS], F32, name="parts%d" % i))
-            sums.append(const.tile([P, 1], F32, name="sums%d" % i))
-            sums_eps.append(const.tile([P, 1], F32, name="sums_eps%d" % i))
+            parts.append(const.tile([P, W_BANKS + 1], F32, name="parts%d" % i))
+            sum_win.append(const.tile([P, 1], F32, name="sum_win%d" % i))
+            sum_eps.append(const.tile([P, 1], F32, name="sum_eps%d" % i))
             recip.append(const.tile([P, 1], F32, name="recip%d" % i))
         ident = const.tile([P, P], BF16)
         tick_rows = const.tile([P, WINDOW], BF16)
@@ -89,9 +89,11 @@ def tile_flashrecomodel_t_kernel(tc, flashes_pe, flashes_time, flashes_confidenc
                 out=g_tile(i)[:, rest], in_=ticks[:, rest], func=ACT.Square, bias=negc[:, i : i + 1], scale=1.0
             )
 
+        def distance_vector(i):
+            nc.vector.tensor_scalar_add(out=g_tile(i)[:, rest], in0=ticks[:, rest], scalar1=negc[:, i : i + 1])
+
         def square_vector(i):
             gt = g_tile(i)
-            nc.vector.tensor_scalar_add(out=gt[:, rest], in0=ticks[:, rest], scalar1=negc[:, i : i + 1])
             nc.vector.tensor_tensor(out=gt[:, rest], in0=gt[:, rest], in1=gt[:, rest], op=ALU.mult)
 
         def exp_rest(i):
@@ -122,40 +124,46 @@ def tile_flashrecomodel_t_kernel(tc, flashes_pe, flashes_time, flashes_confidenc
                 if i + 1 < TILES:
                     square_tensor(i + 1, u)
 
-        def reciprocal_of_sum(i):
-            nc.vector.reduce_sum(out=sums[i][:], in_=parts[i][:], axis=AX.X)
-            nc.vector.tensor_scalar_add(out=sums_eps[i][:], in0=sums[i][:], scalar1=1e-10)
-            nc.vector.reciprocal(out=recip[i][:], in_=sums_eps[i][:])
+        def sum_window(i):
+            nc.vector.reduce_sum(out=sum_win[i][:], in_=parts[i][:, 0:W_BANKS], axis=AX.X)
 
-        def normalise(i, cols):
+        def sum_all(i):
+            nc.vector.scalar_tensor_tensor(
+                out=sum_eps[i][:], in0=parts[i][:, W_BANKS : W_BANKS + 1], scalar=1e-10, in1=sum_win[i][:],
+                op0=ALU.add, op1=ALU.add,
+            )
+
+        def invert(i):
+            nc.vector.reciprocal(out=recip[i][:], in_=sum_eps[i][:])
+
+        def normalise(i, t0, width):
             g, j = divmod(i, PACK)
             if g not in wjs:
                 wjs[g] = wjpool.tile([P, PACK, TICKS], BF16, name="wj")
-            nc.vector.tensor_scalar_mul(out=wjs[g][:, j, cols], in0=gts[i][:, cols], scalar1=recip[i][:, 0:1])
-
-        def finish_tile(i):
-            reciprocal_of_sum(i)
-            normalise(i, slice(0, TICKS))
-
-        def regroup(k):
-            g, n = divmod(k, N_CHUNKS)
-            wch = wchpool.tile([P, CHUNK, PACK], BF16, name="wch", align_bytes=64)
-            wchs[k] = wch
-            nc.vector.tensor_copy(
-                out=wch[:].rearrange("p (c i) j -> p c j i", i=4),
-                in_=wjs[g][:, :, n * CHUNK : (n + 1) * CHUNK].rearrange("p j (c i) -> p c j i", i=4),
+            nc.vector.tensor_scalar_mul(
+                out=wjs[g][:, j, t0 : t0 + width], in0=gts[i][:, t0 : t0 + width], scalar1=recip[i][:, 0:1]
             )
 
-        def quantise(k):
-            g, n = divmod(k, N_CHUNKS)
+        def regroup(g, t0, width):
+            n, off = divmod(t0, CHUNK)
+            if off == 0:
+                wchs[(g, n)] = wchpool.tile([P, CHUNK, PACK], BF16, name="wch", align_bytes=64)
+            nc.vector.tensor_copy(
+                out=wchs[(g, n)][:, off : off + width, :].rearrange("p (c i) j -> p c j i", i=4),
+                in_=wjs[g][:, :, t0 : t0 + width].rearrange("p j (c i) -> p c j i", i=4),
+            )
+
+        def quantise(g, t0, width):
+            n, off = divmod(t0, CHUNK)
             c = g % PASSES
-            pool = c0pool if c == 0 else late["c1pool"]
-            codes = pool.tile([P, CHUNK], U32, name="w_codes%d_%d" % (c, n), align_bytes=64)
-            scales = pool.tile([P, CHUNK], U8, name="w_scales%d_%d" % (c, n), align_bytes=64)
-            w_codes[(c, n)] = codes
-            w_scales[(c, n)] = scales
+            if off == 0:
+                pool = c0pool if c == 0 else late["c1pool"]
+                w_codes[(c, n)] = pool.tile([P, CHUNK], U32, name="w_codes%d_%d" % (c, n), align_bytes=64)
+                w_scales[(c, n)] = pool.tile([P, CHUNK], U8, name="w_scales%d_%d" % (c, n), align_bytes=64)
             nc.vector.quantize_mx(
-                out=codes[:].bitcast(FP8X4), scales=scales[:], in_=wchs[k][:].rearrange("p t j -> p (t j)")
+                out=w_codes[(c, n)][:, off : off + width].bitcast(FP8X4),
+                scales=w_scales[(c, n)][:, off : off + width],
+                in_=wchs[(g, n)][:, off : off + width, :].rearrange("p t j -> p (t j)"),
             )
 
         banks = [0]
@@ -167,18 +175,19 @@ def tile_flashrecomodel_t_kernel(tc, flashes_pe, flashes_time, flashes_confidenc
                 return dqpool.tile([P, N_TILE], F32, name="acc_dq", tag="dq%d" % (q - 5))
             return accpool.tile([P, N_TILE], F32, name="acc")
 
-        def unit(b, v, engines, all_eight):
-            n, half = divmod(v, 2)
-            for mm in range(2):
-                m = 2 * half + mm
+        def multiply(b, t0, width, ms, all_eight):
+            n, off = divmod(t0, CHUNK)
+            todo = []
+            for m in ms:
                 m_cols = slice(m * P, (m + 1) * P)
-                stage = late["stpool"].tile([P, CHUNK], F32, name="stage")
-                for h in range(2):
-                    n_cols = slice(h * N_TILE, (h + 1) * N_TILE)
+                pieces = []
+                for x0 in range(0, width, N_TILE):
+                    nw = min(N_TILE, width - x0)
+                    n_cols = slice(off + x0, off + x0 + nw)
                     acc = bank(all_eight)
                     for c in range(PASSES):
                         nc.tensor.matmul_mx(
-                            out=acc[:],
+                            out=acc[:, 0:nw],
                             lhsT=pe_codes[b * PASSES + c][:, m_cols].bitcast(FP8X4),
                             lhsT_scale=pe_scales[b * PASSES + c][:, m_cols],
                             rhs=w_codes[(c, n)][:, n_cols].bitcast(FP8X4),
@@ -186,23 +195,50 @@ def tile_flashrecomodel_t_kernel(tc, flashes_pe, flashes_time, flashes_confidenc
                             start=(c == 0),
                             stop=(c == PASSES - 1),
                         )
-                    if engines[2 * mm + h] == "V":
-                        nc.vector.tensor_copy(out=stage[:, n_cols], in_=acc[:])
-                    else:
-                        nc.scalar.copy(out=stage[:, n_cols], in_=acc[:])
-                nc.sync.dma_start(out=out[b, m_cols, n * CHUNK : (n + 1) * CHUNK], in_=stage[:])
+                    pieces.append((acc, x0, nw))
+                todo.append((b, m_cols, t0, width, pieces))
+            return todo
 
-        def period(i, extra):
+        def copy_out(item, engines):
+            b, m_cols, t0, width, pieces = item
+            stage = late["stpool"].tile([P, CHUNK], F32, name="stage")
+            for e, (acc, x0, nw) in zip(engines, pieces):
+                if e == "V":
+                    nc.vector.tensor_copy(out=stage[:, x0 : x0 + nw], in_=acc[:, 0:nw])
+                else:
+                    nc.scalar.copy(out=stage[:, x0 : x0 + nw], in_=acc[:, 0:nw])
+            nc.sync.dma_start(out=out[b, m_cols, t0 : t0 + width], in_=stage[:, 0:width])
+
+        def slot(i, filler):
+            if i not in VECTOR_SQUARES:
+                square_scalar(i)
             exp_window(i)
-            square_scalar(i)
             exp_rest(i)
+            units = UNIT_SLOTS.get(i, ())
+            todo = []
+            if units:
+                todo = multiply(0, (units[0] // 2) * CHUNK, CHUNK, (2 * (units[0] % 2), 2 * (units[0] % 2) + 1), False)
             k = i - PACK
+            sum_all(i - 1)
             if k >= 1:
-                quantise(k - 1)
-            regroup(k)
-            extra(i)
-            for v in UNIT_PERIODS.get(i, ()):
-                unit(0, v, "VVVA", False)
+                quantise((k - 1) // N_CHUNKS, ((k - 1) % N_CHUNKS) * CHUNK, CHUNK)
+            invert(i - 1)
+            filler(i)
+            if todo:
+                copy_out(todo[0], "VV")
+            normalise(i - 1, 0, TICKS)
+            if i + 1 in VECTOR_SQUARES:
+                distance_vector(i + 1)
+            regroup(k // N_CHUNKS, (k % N_CHUNKS) * CHUNK, CHUNK)
+            if i + 1 in VECTOR_SQUARES:
+                square_vector(i + 1)
+            if todo:
+                copy_out(todo[1], "VA")
+            for v in units[1:]:
+                todo = multiply(0, (v // 2) * CHUNK, CHUNK, (2 * (v % 2), 2 * (v % 2) + 1), False)
+                copy_out(todo[0], "VV")
+                copy_out(todo[1], "VA")
+            sum_window(i)
 
         with tc.tile_pool(name="prep", bufs=1) as prep:
             tm_bf = prep.tile([P, GROUPS, PACK], BF16)
@@ -242,15 +278,17 @@ def tile_flashrecomodel_t_kernel(tc, flashes_pe, flashes_time, flashes_confidenc
                 nc.vector.tensor_scalar_add(out=ticks[:, have : 2 * have], in0=ticks[:, 0:have], scalar1=float(have))
                 have *= 2
 
+            sig2 = prep.tile([P, 1], F32)
+            inv2 = prep.tile([P, 1], F32)
             nc.vector.tensor_scalar(
                 out=negc[:], in0=tm_bf[:].rearrange("p g j -> p (g j)"), scalar1=-float(TICKS), scalar2=0.0,
                 op0=ALU.mult, op1=ALU.min,
             )
-            nc.vector.tensor_scalar_max(out=negc[:], in0=negc[:], scalar1=-float(TICKS - 1))
-            sig2 = prep.tile([P, 1], F32)
             nc.vector.tensor_tensor(out=sig2[:], in0=sig_bf[:], in1=sig_bf[:], op=ALU.mult)
-            inv2 = prep.tile([P, 1], F32)
+            nc.vector.tensor_scalar_max(out=negc[:], in0=negc[:], scalar1=-float(TICKS - 1))
             nc.vector.reciprocal(out=inv2[:], in_=sig2[:])
+            tcol = prep.tile([P, W_BLOCKS], F32)
+            nc.vector.tensor_copy(out=tcol[:], in_=tcol_i[:])
             nc.vector.tensor_scalar_mul(out=neg_h[:], in0=inv2[:], scalar1=-0.5)
 
             square_scalar(0)
@@ -269,77 +307,98 @@ def tile_flashrecomodel_t_kernel(tc, flashes_pe, flashes_time, flashes_confidenc
                 )
                 spes.append(spe)
 
-            tcol = prep.tile([P, W_BLOCKS], F32)
-            nc.vector.tensor_copy(out=tcol[:], in_=tcol_i[:])
             t_sq = prep.tile([P, W_BLOCKS], F32)
-            nc.vector.tensor_tensor(out=t_sq[:], in0=tcol[:], in1=tcol[:], op=ALU.mult)
-            nc.vector.tensor_copy(out=tick_cols[:, :, 0], in_=t_sq[:])
             t_rem1 = prep.tile([P, W_BLOCKS], F32)
-            nc.vector.tensor_tensor(out=t_rem1[:], in0=t_sq[:], in1=tick_cols[:, :, 0], op=ALU.subtract)
-            nc.vector.tensor_copy(out=tick_cols[:, :, 1], in_=t_rem1[:])
             t_rem2 = prep.tile([P, W_BLOCKS], F32)
-            nc.vector.tensor_tensor(out=t_rem2[:], in0=t_rem1[:], in1=tick_cols[:, :, 1], op=ALU.subtract)
-            nc.vector.tensor_copy(out=tick_cols[:, :, 2], in_=t_rem2[:])
-            nc.vector.tensor_copy(
-                out=tick_cols[:, :, 3:6:2], in_=tcol[:].unsqueeze(2).to_broadcast([P, W_BLOCKS, 2])
-            )
             t_lo = prep.tile([P, W_BLOCKS], F32)
-            nc.vector.tensor_tensor(out=t_lo[:], in0=tcol[:], in1=tick_cols[:, :, 3], op=ALU.subtract)
-            nc.vector.tensor_copy(
-                out=tick_cols[:, :, 4:7:2], in_=t_lo[:].unsqueeze(2).to_broadcast([P, W_BLOCKS, 2])
-            )
-            nc.vector.memset(tick_cols[:, :, 7:10], 1.0)
-            tab0 = accpool.tile([P, 8 * P], BF16, name="tab0", tag="acc")
-            tab1 = accpool.tile([P, 8 * P], BF16, name="tab1", tag="acc")
-            for a in range(W_BLOCKS):
-                tab = tab0 if a < 8 else tab1
-                nc.tensor.transpose(tab[:, (a % 8) * P : (a % 8 + 1) * P], tick_cols[:, a, :], ident[:])
-
             a_full = prep.tile([P, TILES], F32)
-            nc.vector.tensor_scalar_mul(out=a_full[:], in0=negc[:], scalar1=2.0)
-            nc.vector.tensor_copy(
-                out=flash_cols[:, :, 3:5], in_=a_full[:].unsqueeze(2).to_broadcast([P, TILES, 2])
-            )
             a_lo = prep.tile([P, TILES], F32)
-            nc.vector.tensor_tensor(out=a_lo[:], in0=a_full[:], in1=flash_cols[:, :, 3], op=ALU.subtract)
-            nc.vector.tensor_copy(
-                out=flash_cols[:, :, 5:7], in_=a_lo[:].unsqueeze(2).to_broadcast([P, TILES, 2])
-            )
             c_sq = prep.tile([P, TILES], F32)
-            nc.vector.tensor_tensor(out=c_sq[:], in0=negc[:], in1=negc[:], op=ALU.mult)
-            nc.vector.tensor_copy(out=flash_cols[:, :, 7], in_=c_sq[:])
             c_rem1 = prep.tile([P, TILES], F32)
-            nc.vector.tensor_tensor(out=c_rem1[:], in0=c_sq[:], in1=flash_cols[:, :, 7], op=ALU.subtract)
-            nc.vector.tensor_copy(out=flash_cols[:, :, 8], in_=c_rem1[:])
             c_rem2 = prep.tile([P, TILES], F32)
-            nc.vector.tensor_tensor(out=c_rem2[:], in0=c_rem1[:], in1=flash_cols[:, :, 8], op=ALU.subtract)
-            nc.vector.tensor_copy(out=flash_cols[:, :, 9], in_=c_rem2[:])
-            nc.vector.memset(flash_cols[:, :, 0:3], 1.0)
-            tab2 = accpool.tile([P, 8 * P], BF16, name="tab2", tag="acc")
-            tab3 = accpool.tile([P, 8 * P], BF16, name="tab3", tag="acc")
-            for a in range(TILES):
-                tab = tab2 if a < 8 else tab3
-                nc.tensor.transpose(tab[:, (a % 8) * P : (a % 8 + 1) * P], flash_cols[:, a, :], ident[:])
 
-            nc.vector.tensor_copy(out=tick_rows[:, 0 : 8 * P], in_=tab0[:])
-            nc.vector.tensor_copy(out=tick_rows[:, 8 * P : WINDOW], in_=tab1[:, 0 : WINDOW - 8 * P])
-            nc.vector.tensor_copy(out=flash_rows[:, 0 : 8 * P], in_=tab2[:])
-            nc.vector.tensor_copy(out=flash_rows[:, 8 * P : TILES * P], in_=tab3[:])
+            def cast(dst, src):
+                return lambda: nc.vector.tensor_copy(out=dst, in_=src)
+
+            def twice(src, count):
+                return src.unsqueeze(2).to_broadcast([P, count, 2])
+
+            def combine(dst, in0, in1, op):
+                return lambda: nc.vector.tensor_tensor(out=dst, in0=in0, in1=in1, op=op)
+
+            chains = [
+                [
+                    combine(t_sq[:], tcol[:], tcol[:], ALU.mult),
+                    cast(tick_cols[:, :, 0], t_sq[:]),
+                    combine(t_rem1[:], t_sq[:], tick_cols[:, :, 0], ALU.subtract),
+                    cast(tick_cols[:, :, 1], t_rem1[:]),
+                    combine(t_rem2[:], t_rem1[:], tick_cols[:, :, 1], ALU.subtract),
+                    cast(tick_cols[:, :, 2], t_rem2[:]),
+                ],
+                [
+                    combine(c_sq[:], negc[:], negc[:], ALU.mult),
+                    cast(flash_cols[:, :, 7], c_sq[:]),
+                    combine(c_rem1[:], c_sq[:], flash_cols[:, :, 7], ALU.subtract),
+                    cast(flash_cols[:, :, 8], c_rem1[:]),
+                    combine(c_rem2[:], c_rem1[:], flash_cols[:, :, 8], ALU.subtract),
+                    cast(flash_cols[:, :, 9], c_rem2[:]),
+                ],
+                [
+                    cast(tick_cols[:, :, 3:6:2], twice(tcol[:], W_BLOCKS)),
+                    combine(t_lo[:], tcol[:], tick_cols[:, :, 3], ALU.subtract),
+                    cast(tick_cols[:, :, 4:7:2], twice(t_lo[:], W_BLOCKS)),
+                    lambda: nc.vector.memset(tick_cols[:, :, 7:10], 1.0),
+                ],
+                [
+                    lambda: nc.vector.tensor_scalar_mul(out=a_full[:], in0=negc[:], scalar1=2.0),
+                    cast(flash_cols[:, :, 3:5], twice(a_full[:], TILES)),
+                    combine(a_lo[:], a_full[:], flash_cols[:, :, 3], ALU.subtract),
+                    cast(flash_cols[:, :, 5:7], twice(a_lo[:], TILES)),
+                    lambda: nc.vector.memset(flash_cols[:, :, 0:3], 1.0),
+                ],
+            ]
+            for step in range(6):
+                for chain in chains:
+                    if step < len(chain):
+                        chain[step]()
+
+            tabs = []
+            for a in range(4):
+                tabs.append(accpool.tile([P, 8 * P], BF16, name="tab%d" % a, tag="acc"))
+            for a in range(W_BLOCKS):
+                nc.tensor.transpose(tabs[a // 8][:, (a % 8) * P : (a % 8 + 1) * P], tick_cols[:, a, :], ident[:])
+            for a in range(TILES):
+                nc.tensor.transpose(tabs[2 + a // 8][:, (a % 8) * P : (a % 8 + 1) * P], flash_cols[:, a, :], ident[:])
+            distance_vector(2)
+            nc.vector.tensor_copy(out=tick_rows[:, 0 : 8 * P], in_=tabs[0][:])
+            nc.vector.tensor_copy(out=tick_rows[:, 8 * P : WINDOW], in_=tabs[1][:, 0 : WINDOW - 8 * P])
+            nc.vector.tensor_copy(out=flash_rows[:, 0 : 8 * P], in_=tabs[2][:])
+            nc.vector.tensor_copy(out=flash_rows[:, 8 * P : TILES * P], in_=tabs[3][:])
 
             for u in range(W_BANKS):
                 square_tensor(0, u)
             square_vector(2)
             exp_window(0)
-            finish_tile(0)
-            square_vector(3)
+            sum_window(0)
+            sum_all(0)
+            invert(0)
+            normalise(0, 0, TICKS)
+            distance_vector(3)
             exp_window(1)
-            finish_tile(1)
+            sum_window(1)
+            square_vector(3)
+            sum_all(1)
+            invert(1)
+            normalise(1, 0, TICKS)
             exp_window(2)
             exp_rest(2)
-            finish_tile(2)
+            sum_window(2)
+            sum_all(2)
+            invert(2)
+            normalise(2, 0, TICKS)
             exp_window(3)
             exp_rest(3)
-            finish_tile(3)
+            sum_window(3)
 
             def quantise_pe(i):
                 g = i - PACK
@@ -349,8 +408,7 @@ def tile_flashrecomodel_t_kernel(tc, flashes_pe, flashes_time, flashes_confidenc
                 )
 
             for i in range(PACK, 2 * PACK):
-                period(i, quantise_pe)
-                finish_tile(i)
+                slot(i, quantise_pe)
 
         with tc.tile_pool(name="c1pool", bufs=1) as c1pool, tc.tile_pool(name="stpool", bufs=4) as stpool:
             late["c1pool"] = c1pool
@@ -360,30 +418,23 @@ def tile_flashrecomodel_t_kernel(tc, flashes_pe, flashes_time, flashes_confidenc
                 return None
 
             for i in range(2 * PACK, TILES):
-                period(i, nothing)
-                if i < TILES - 1:
-                    finish_tile(i)
+                slot(i, nothing)
+
             last = TILES - 1
-            first_k = (GROUPS - 1) * N_CHUNKS
-            quantise(first_k - 1)
-            reciprocal_of_sum(last)
-            normalise(last, slice(0, CHUNK))
-            regroup(first_k)
-            quantise(first_k)
-            unit(1, 0, "AAAA", True)
-            normalise(last, slice(CHUNK, 2 * CHUNK))
-            regroup(first_k + 1)
-            unit(1, 1, "AAAA", True)
-            quantise(first_k + 1)
-            normalise(last, slice(2 * CHUNK, 3 * CHUNK))
-            regroup(first_k + 2)
-            unit(1, 2, "AAAA", True)
-            quantise(first_k + 2)
-            normalise(last, slice(3 * CHUNK, 4 * CHUNK))
-            regroup(first_k + 3)
-            unit(1, 3, "AAAA", True)
-            quantise(first_k + 3)
-            unit(1, 4, "AVAV", True)
-            unit(1, 5, "AVAV", True)
-            unit(1, 6, "AVAV", True)
-            unit(1, 7, "AVAV", True)
+            g_last = GROUPS - 1
+            sum_all(last)
+            quantise(g_last - 1, TICKS - CHUNK, CHUNK)
+            invert(last)
+            normalise(last, LAST_BLOCKS[0][0], LAST_BLOCKS[0][1])
+            regroup(g_last, LAST_BLOCKS[0][0], LAST_BLOCKS[0][1])
+            for x in range(len(LAST_BLOCKS)):
+                t0, width = LAST_BLOCKS[x]
+                more = x + 1 < len(LAST_BLOCKS)
+                if more:
+                    normalise(last, LAST_BLOCKS[x + 1][0], LAST_BLOCKS[x + 1][1])
+                quantise(g_last, t0, width)
+                todo = multiply(1, t0, width, (0, 1, 2, 3), True)
+                if more:
+                    regroup(g_last, LAST_BLOCKS[x + 1][0], LAST_BLOCKS[x + 1][1])
+                for item in todo:
+                    copy_out(item, "AA" if more else "AV")

@@ -29,7 +29,7 @@ N_TILE = 512
 WINDOW = 1536
 W_BANKS = WINDOW // N_TILE
 W_BLOCKS = WINDOW // P
-VECTOR_SQUARES = (2, 3, 6)
+VECTOR_SQUARES = (2, 3)
 UNIT_SLOTS = {10: (0, 1), 11: (2,), 12: (3,), 13: (4, 5), 14: (6,), 15: (7,)}
 LAST_BLOCKS = ((0, 256), (256, 256), (512, 512), (1024, 1024), (2048, 1024), (3072, 1024))
 
@@ -296,16 +296,16 @@ def tile_flashrecomodel_t_kernel(tc, flashes_pe, flashes_time, flashes_confidenc
             square_scalar(1)
             exp_rest(1)
 
-            spes = []
-            for g in range(GROUPS):
-                spe = prep.tile([P, CHANNELS, PACK], BF16, name="spe%d" % g, align_bytes=64)
-                nc.gpsimd.tensor_tensor(
-                    out=spe[:],
+            spes = {}
+
+            def scale_pe(g):
+                spes[g] = prep.tile([P, CHANNELS, PACK], BF16, name="spe%d" % g, align_bytes=64)
+                nc.vector.tensor_tensor(
+                    out=spes[g][:],
                     in0=pe_raw[:, g].rearrange("p j w -> p w j"),
                     in1=cf_bf[:, g].unsqueeze(1).to_broadcast([P, CHANNELS, PACK]),
                     op=ALU.mult,
                 )
-                spes.append(spe)
 
             t_sq = prep.tile([P, W_BLOCKS], F32)
             t_rem1 = prep.tile([P, W_BLOCKS], F32)
@@ -370,6 +370,7 @@ def tile_flashrecomodel_t_kernel(tc, flashes_pe, flashes_time, flashes_confidenc
             for a in range(TILES):
                 nc.tensor.transpose(tabs[2 + a // 8][:, (a % 8) * P : (a % 8 + 1) * P], flash_cols[:, a, :], ident[:])
             distance_vector(2)
+            scale_pe(0)
             nc.vector.tensor_copy(out=tick_rows[:, 0 : 8 * P], in_=tabs[0][:])
             nc.vector.tensor_copy(out=tick_rows[:, 8 * P : WINDOW], in_=tabs[1][:, 0 : WINDOW - 8 * P])
             nc.vector.tensor_copy(out=flash_rows[:, 0 : 8 * P], in_=tabs[2][:])
@@ -378,6 +379,7 @@ def tile_flashrecomodel_t_kernel(tc, flashes_pe, flashes_time, flashes_confidenc
             for u in range(W_BANKS):
                 square_tensor(0, u)
             square_vector(2)
+            scale_pe(1)
             exp_window(0)
             sum_window(0)
             sum_all(0)
@@ -402,6 +404,8 @@ def tile_flashrecomodel_t_kernel(tc, flashes_pe, flashes_time, flashes_confidenc
 
             def quantise_pe(i):
                 g = i - PACK
+                if g + 1 in (2, 3):
+                    scale_pe(g + 1)
                 nc.vector.quantize_mx(
                     out=pe_codes[g][:].bitcast(FP8X4), scales=pe_scales[g][:],
                     in_=spes[g][:].rearrange("p w j -> p (w j)"),

@@ -31,7 +31,7 @@ W_BANKS = WINDOW // N_TILE
 W_BLOCKS = WINDOW // P
 VECTOR_SQUARES = (2, 3)
 UNIT_SLOTS = {10: (0, 1), 11: (2,), 12: (3,), 13: (4, 5), 14: (6,), 15: (7,)}
-LAST_BLOCKS = ((0, 256), (256, 256), (512, 512), (1024, 1024), (2048, 1024), (3072, 1024))
+LAST_WIDTHS = (256, 256, 512, 512, 512, 512, 512, 1024)
 
 FLOPS = 2 * EVENTS * FLASHES * CHANNELS * TICKS
 
@@ -49,7 +49,7 @@ def tile_flashrecomodel_t_kernel(tc, flashes_pe, flashes_time, flashes_confidenc
         dqpool = ctx.enter_context(tc.psum_pool(name="dqpool", bufs=1))
         accpool = ctx.enter_context(tc.psum_pool(name="accpool", bufs=5))
 
-        ticks = const.tile([P, TICKS], F32)
+        ticks = const.tile([P, TICKS - WINDOW], F32)
         negc = const.tile([P, TILES], F32)
         neg_h = const.tile([P, 1], F32)
         parts = []
@@ -86,11 +86,11 @@ def tile_flashrecomodel_t_kernel(tc, flashes_pe, flashes_time, flashes_confidenc
 
         def square_scalar(i):
             nc.scalar.activation(
-                out=g_tile(i)[:, rest], in_=ticks[:, rest], func=ACT.Square, bias=negc[:, i : i + 1], scale=1.0
+                out=g_tile(i)[:, rest], in_=ticks[:], func=ACT.Square, bias=negc[:, i : i + 1], scale=1.0
             )
 
         def distance_vector(i):
-            nc.vector.tensor_scalar_add(out=g_tile(i)[:, rest], in0=ticks[:, rest], scalar1=negc[:, i : i + 1])
+            nc.vector.tensor_scalar_add(out=g_tile(i)[:, rest], in0=ticks[:], scalar1=negc[:, i : i + 1])
 
         def square_vector(i):
             gt = g_tile(i)
@@ -196,28 +196,36 @@ def tile_flashrecomodel_t_kernel(tc, flashes_pe, flashes_time, flashes_confidenc
                             stop=(c == PASSES - 1),
                         )
                     pieces.append((acc, x0, nw))
-                todo.append((b, m_cols, t0, width, pieces))
+                todo.append((b, m, t0, width, pieces))
             return todo
 
-        def copy_out(item, engines):
-            b, m_cols, t0, width, pieces = item
+        def copy_out(items, engines):
+            b, m_first, t0, width, unused = items[0]
             stage = late["stpool"].tile([P, CHUNK], F32, name="stage")
-            for e, (acc, x0, nw) in zip(engines, pieces):
-                if e == "V":
-                    nc.vector.tensor_copy(out=stage[:, x0 : x0 + nw], in_=acc[:, 0:nw])
-                else:
-                    nc.scalar.copy(out=stage[:, x0 : x0 + nw], in_=acc[:, 0:nw])
-            nc.sync.dma_start(out=out[b, m_cols, t0 : t0 + width], in_=stage[:, 0:width])
+            e = 0
+            for a, item in enumerate(items):
+                for acc, x0, nw in item[4]:
+                    dst = stage[:, a * width + x0 : a * width + x0 + nw]
+                    if engines[e % len(engines)] == "V":
+                        nc.vector.tensor_copy(out=dst, in_=acc[:, 0:nw])
+                    else:
+                        nc.scalar.copy(out=dst, in_=acc[:, 0:nw])
+                    e += 1
+            count = len(items)
+            nc.sync.dma_start(
+                out=out[b, m_first * P : (m_first + count) * P, t0 : t0 + width].rearrange("(m p) t -> p m t", p=P),
+                in_=stage[:, 0 : count * width].rearrange("p (m t) -> p m t", m=count),
+            )
 
         def slot(i, filler):
-            if i not in VECTOR_SQUARES:
-                square_scalar(i)
-            exp_window(i)
-            exp_rest(i)
             units = UNIT_SLOTS.get(i, ())
             todo = []
             if units:
                 todo = multiply(0, (units[0] // 2) * CHUNK, CHUNK, (2 * (units[0] % 2), 2 * (units[0] % 2) + 1), False)
+            if i not in VECTOR_SQUARES:
+                square_scalar(i)
+            exp_window(i)
+            exp_rest(i)
             k = i - PACK
             sum_all(i - 1)
             if k >= 1:
@@ -225,7 +233,7 @@ def tile_flashrecomodel_t_kernel(tc, flashes_pe, flashes_time, flashes_confidenc
             invert(i - 1)
             filler(i)
             if todo:
-                copy_out(todo[0], "VV")
+                copy_out(todo[0:1], "VV")
             normalise(i - 1, 0, TICKS)
             if i + 1 in VECTOR_SQUARES:
                 distance_vector(i + 1)
@@ -233,11 +241,11 @@ def tile_flashrecomodel_t_kernel(tc, flashes_pe, flashes_time, flashes_confidenc
             if i + 1 in VECTOR_SQUARES:
                 square_vector(i + 1)
             if todo:
-                copy_out(todo[1], "VA")
+                copy_out(todo[1:2], "VA")
             for v in units[1:]:
                 todo = multiply(0, (v // 2) * CHUNK, CHUNK, (2 * (v % 2), 2 * (v % 2) + 1), False)
-                copy_out(todo[0], "VV")
-                copy_out(todo[1], "VA")
+                copy_out(todo[0:1], "VV")
+                copy_out(todo[1:2], "VA")
             sum_window(i)
 
         with tc.tile_pool(name="prep", bufs=1) as prep:
@@ -258,7 +266,7 @@ def tile_flashrecomodel_t_kernel(tc, flashes_pe, flashes_time, flashes_confidenc
 
             seed = 128
             tick_i = prep.tile([P, seed], I32)
-            nc.gpsimd.iota(tick_i[:], pattern=[[1, seed]], base=0, channel_multiplier=0)
+            nc.gpsimd.iota(tick_i[:], pattern=[[1, seed]], base=WINDOW, channel_multiplier=0)
             warm = prep.tile([P, 1], F32)
             nc.gpsimd.memset(warm[:], 0.0)
             tcol_i = prep.tile([P, W_BLOCKS], I32)
@@ -274,9 +282,10 @@ def tile_flashrecomodel_t_kernel(tc, flashes_pe, flashes_time, flashes_confidenc
 
             nc.vector.tensor_copy(out=ticks[:, 0:seed], in_=tick_i[:])
             have = seed
-            while have < TICKS:
-                nc.vector.tensor_scalar_add(out=ticks[:, have : 2 * have], in0=ticks[:, 0:have], scalar1=float(have))
-                have *= 2
+            while have < TICKS - WINDOW:
+                more = min(have, TICKS - WINDOW - have)
+                nc.vector.tensor_scalar_add(out=ticks[:, have : have + more], in0=ticks[:, 0:more], scalar1=float(have))
+                have += more
 
             sig2 = prep.tile([P, 1], F32)
             inv2 = prep.tile([P, 1], F32)
@@ -426,19 +435,25 @@ def tile_flashrecomodel_t_kernel(tc, flashes_pe, flashes_time, flashes_confidenc
 
             last = TILES - 1
             g_last = GROUPS - 1
+            blocks = []
+            begin = 0
+            for width in LAST_WIDTHS:
+                blocks.append((begin, width))
+                begin += width
             sum_all(last)
             quantise(g_last - 1, TICKS - CHUNK, CHUNK)
             invert(last)
-            normalise(last, LAST_BLOCKS[0][0], LAST_BLOCKS[0][1])
-            regroup(g_last, LAST_BLOCKS[0][0], LAST_BLOCKS[0][1])
-            for x in range(len(LAST_BLOCKS)):
-                t0, width = LAST_BLOCKS[x]
-                more = x + 1 < len(LAST_BLOCKS)
+            normalise(last, blocks[0][0], blocks[0][1])
+            regroup(g_last, blocks[0][0], blocks[0][1])
+            for x in range(len(blocks)):
+                t0, width = blocks[x]
+                more = x + 1 < len(blocks)
                 if more:
-                    normalise(last, LAST_BLOCKS[x + 1][0], LAST_BLOCKS[x + 1][1])
+                    normalise(last, blocks[x + 1][0], blocks[x + 1][1])
                 quantise(g_last, t0, width)
                 todo = multiply(1, t0, width, (0, 1, 2, 3), True)
                 if more:
-                    regroup(g_last, LAST_BLOCKS[x + 1][0], LAST_BLOCKS[x + 1][1])
-                for item in todo:
-                    copy_out(item, "AA" if more else "AV")
+                    regroup(g_last, blocks[x + 1][0], blocks[x + 1][1])
+                together = CHUNK // width
+                for a in range(0, len(todo), together):
+                    copy_out(todo[a : a + together], "A" if more else "AV")

@@ -42,7 +42,7 @@ def tile_flashrecomodel_t_kernel(tc, flashes_pe, flashes_time, flashes_confidenc
     with ExitStack() as ctx:
         ctx.enter_context(tc.manual_schedule())
         const = ctx.enter_context(tc.tile_pool(name="const", bufs=1))
-        gpool = ctx.enter_context(tc.tile_pool(name="gpool", bufs=3))
+        gpool = ctx.enter_context(tc.tile_pool(name="gpool", bufs=4))
         wjpool = ctx.enter_context(tc.tile_pool(name="wjpool", bufs=2))
         wchpool = ctx.enter_context(tc.tile_pool(name="wchpool", bufs=2))
         c0pool = ctx.enter_context(tc.tile_pool(name="c0pool", bufs=1))
@@ -63,7 +63,7 @@ def tile_flashrecomodel_t_kernel(tc, flashes_pe, flashes_time, flashes_confidenc
             recip.append(const.tile([P, 1], F32, name="recip%d" % i))
         ident = const.tile([P, P], BF16)
         tick_rows = const.tile([P, WINDOW], BF16)
-        flash_rows = const.tile([P, TILES * P], BF16)
+        flash_rows = [const.tile([P, 8 * P], BF16, name="flash_rows%d" % a) for a in range(2)]
         pe_codes = []
         pe_scales = []
         for g in range(GROUPS):
@@ -108,7 +108,7 @@ def tile_flashrecomodel_t_kernel(tc, flashes_pe, flashes_time, flashes_confidenc
             dqs[u] = dq
             nc.tensor.matmul(
                 out=dq[:],
-                lhsT=flash_rows[:, i * P : (i + 1) * P],
+                lhsT=flash_rows[i // 8][:, (i % 8) * P : (i % 8 + 1) * P],
                 rhs=tick_rows[:, u * N_TILE : (u + 1) * N_TILE],
                 start=True,
                 stop=True,
@@ -272,9 +272,7 @@ def tile_flashrecomodel_t_kernel(tc, flashes_pe, flashes_time, flashes_confidenc
             tcol_i = prep.tile([P, W_BLOCKS], I32)
             nc.gpsimd.iota(tcol_i[:], pattern=[[P, W_BLOCKS]], base=0, channel_multiplier=1)
             tick_cols = prep.tile([P, W_BLOCKS, P], BF16)
-            nc.gpsimd.memset(tick_cols[:].rearrange("p a k -> p (a k)").bitcast(F32), 0.0)
             flash_cols = prep.tile([P, TILES, P], BF16)
-            nc.gpsimd.memset(flash_cols[:].rearrange("p a k -> p (a k)").bitcast(F32), 0.0)
             make_identity(nc, ident[:])
 
             warm_out = prep.tile([P, 1], F32)
@@ -286,6 +284,9 @@ def tile_flashrecomodel_t_kernel(tc, flashes_pe, flashes_time, flashes_confidenc
                 more = min(have, TICKS - WINDOW - have)
                 nc.vector.tensor_scalar_add(out=ticks[:, have : have + more], in0=ticks[:, 0:more], scalar1=float(have))
                 have += more
+
+            nc.vector.memset(tick_cols[:].rearrange("p a k -> p (a k)").bitcast(I32), 0)
+            nc.vector.memset(flash_cols[:].rearrange("p a k -> p (a k)").bitcast(I32), 0)
 
             sig2 = prep.tile([P, 1], F32)
             inv2 = prep.tile([P, 1], F32)
@@ -376,28 +377,30 @@ def tile_flashrecomodel_t_kernel(tc, flashes_pe, flashes_time, flashes_confidenc
                 tabs.append(accpool.tile([P, 8 * P], BF16, name="tab%d" % a, tag="acc"))
             for a in range(W_BLOCKS):
                 nc.tensor.transpose(tabs[a // 8][:, (a % 8) * P : (a % 8 + 1) * P], tick_cols[:, a, :], ident[:])
-            for a in range(TILES):
-                nc.tensor.transpose(tabs[2 + a // 8][:, (a % 8) * P : (a % 8 + 1) * P], flash_cols[:, a, :], ident[:])
+            for a in range(8):
+                nc.tensor.transpose(tabs[2][:, a * P : (a + 1) * P], flash_cols[:, a, :], ident[:])
             distance_vector(2)
             scale_pe(0)
             nc.vector.tensor_copy(out=tick_rows[:, 0 : 8 * P], in_=tabs[0][:])
             nc.vector.tensor_copy(out=tick_rows[:, 8 * P : WINDOW], in_=tabs[1][:, 0 : WINDOW - 8 * P])
-            nc.vector.tensor_copy(out=flash_rows[:, 0 : 8 * P], in_=tabs[2][:])
-            nc.vector.tensor_copy(out=flash_rows[:, 8 * P : TILES * P], in_=tabs[3][:])
+            nc.vector.tensor_copy(out=flash_rows[0][:], in_=tabs[2][:])
 
             for u in range(W_BANKS):
                 square_tensor(0, u)
+            for a in range(8):
+                nc.tensor.transpose(tabs[3][:, a * P : (a + 1) * P], flash_cols[:, 8 + a, :], ident[:])
+            distance_vector(3)
             square_vector(2)
-            scale_pe(1)
+            square_vector(3)
             exp_window(0)
             sum_window(0)
             sum_all(0)
+            nc.vector.tensor_copy(out=flash_rows[1][:], in_=tabs[3][:])
             invert(0)
             normalise(0, 0, TICKS)
-            distance_vector(3)
             exp_window(1)
             sum_window(1)
-            square_vector(3)
+            scale_pe(1)
             sum_all(1)
             invert(1)
             normalise(1, 0, TICKS)

@@ -29,7 +29,8 @@ N_TILE = 512
 WINDOW = 1536
 W_BANKS = WINDOW // N_TILE
 W_BLOCKS = WINDOW // P
-VECTOR_SQUARES = (2, 3)
+REST = TICKS - WINDOW
+VECTOR_SQUARES = {2: REST, 3: REST, 4: 512, 5: 512, 6: 512, 7: 512}
 UNIT_SLOTS = {10: (0, 1), 11: (2,), 12: (3,), 13: (4, 5), 14: (6,), 15: (7,)}
 LAST_WIDTHS = (256, 256, 512, 512, 512, 512, 512, 1024)
 
@@ -42,26 +43,24 @@ def tile_flashrecomodel_t_kernel(tc, flashes_pe, flashes_time, flashes_confidenc
     with ExitStack() as ctx:
         ctx.enter_context(tc.manual_schedule())
         const = ctx.enter_context(tc.tile_pool(name="const", bufs=1))
-        gpool = ctx.enter_context(tc.tile_pool(name="gpool", bufs=4))
-        wjpool = ctx.enter_context(tc.tile_pool(name="wjpool", bufs=2))
+        gpool = ctx.enter_context(tc.tile_pool(name="gpool", bufs=2))
         wchpool = ctx.enter_context(tc.tile_pool(name="wchpool", bufs=2))
         c0pool = ctx.enter_context(tc.tile_pool(name="c0pool", bufs=1))
         dqpool = ctx.enter_context(tc.psum_pool(name="dqpool", bufs=1))
-        accpool = ctx.enter_context(tc.psum_pool(name="accpool", bufs=5))
+        accpool = ctx.enter_context(tc.psum_pool(name="accpool", bufs=4))
 
         ticks = const.tile([P, TICKS - WINDOW], F32)
         negc = const.tile([P, TILES], F32)
         neg_h = const.tile([P, 1], F32)
-        parts = []
-        sum_win = []
-        sum_eps = []
-        recip = []
-        for i in range(TILES):
-            parts.append(const.tile([P, W_BANKS + 1], F32, name="parts%d" % i))
-            sum_win.append(const.tile([P, 1], F32, name="sum_win%d" % i))
-            sum_eps.append(const.tile([P, 1], F32, name="sum_eps%d" % i))
-            recip.append(const.tile([P, 1], F32, name="recip%d" % i))
+        parts = const.tile([P, TILES, W_BANKS + 1], F32)
+        sums = const.tile([P, TILES], F32)
+        sums_eps = const.tile([P, TILES], F32)
+        recip = const.tile([P, TILES], F32)
+        recip_ps = dqpool.tile([P, TILES], F32, name="recip_ps")
         ident = const.tile([P, P], BF16)
+        ident_f = const.tile([P, P], F32)
+        tokens = const.tile([P, 32 * PACK], F32)
+        tokens_used = [0]
         tick_rows = const.tile([P, WINDOW], BF16)
         flash_rows = [const.tile([P, 8 * P], BF16, name="flash_rows%d" % a) for a in range(2)]
         pe_codes = []
@@ -72,7 +71,6 @@ def tile_flashrecomodel_t_kernel(tc, flashes_pe, flashes_time, flashes_confidenc
 
         gts = {}
         dqs = {}
-        wjs = {}
         wchs = {}
         w_codes = {}
         w_scales = {}
@@ -80,27 +78,37 @@ def tile_flashrecomodel_t_kernel(tc, flashes_pe, flashes_time, flashes_confidenc
         rest = slice(WINDOW, TICKS)
 
         def g_tile(i):
-            if i not in gts:
-                gts[i] = gpool.tile([P, TICKS], F32, name="gt")
-            return gts[i]
+            g, j = divmod(i, PACK)
+            if g not in gts:
+                gts[g] = gpool.tile([P, PACK, TICKS], F32, name="gg")
+            return gts[g][:, j, :]
 
         def square_scalar(i):
-            nc.scalar.activation(
-                out=g_tile(i)[:, rest], in_=ticks[:], func=ACT.Square, bias=negc[:, i : i + 1], scale=1.0
-            )
+            lo = VECTOR_SQUARES.get(i, 0)
+            if lo < REST:
+                nc.scalar.activation(
+                    out=g_tile(i)[:, WINDOW + lo : TICKS], in_=ticks[:, lo:REST], func=ACT.Square,
+                    bias=negc[:, i : i + 1], scale=1.0,
+                )
 
         def distance_vector(i):
-            nc.vector.tensor_scalar_add(out=g_tile(i)[:, rest], in0=ticks[:], scalar1=negc[:, i : i + 1])
+            hi = VECTOR_SQUARES.get(i, 0)
+            if hi > 0:
+                nc.vector.tensor_scalar_add(
+                    out=g_tile(i)[:, WINDOW : WINDOW + hi], in0=ticks[:, 0:hi], scalar1=negc[:, i : i + 1]
+                )
 
         def square_vector(i):
-            gt = g_tile(i)
-            nc.vector.tensor_tensor(out=gt[:, rest], in0=gt[:, rest], in1=gt[:, rest], op=ALU.mult)
+            hi = VECTOR_SQUARES.get(i, 0)
+            if hi > 0:
+                gt = g_tile(i)[:, WINDOW : WINDOW + hi]
+                nc.vector.tensor_tensor(out=gt, in0=gt, in1=gt, op=ALU.mult)
 
         def exp_rest(i):
             gt = g_tile(i)
             nc.scalar.activation(
                 out=gt[:, rest], in_=gt[:, rest], func=ACT.Exp, scale=neg_h[:, 0:1],
-                accum_out=parts[i][:, W_BANKS : W_BANKS + 1],
+                accum_out=parts[:, i, W_BANKS : W_BANKS + 1],
             )
 
         def square_tensor(i, u):
@@ -119,38 +127,43 @@ def tile_flashrecomodel_t_kernel(tc, flashes_pe, flashes_time, flashes_confidenc
             for u in range(W_BANKS):
                 nc.scalar.activation(
                     out=gt[:, u * N_TILE : (u + 1) * N_TILE], in_=dqs[u][:], func=ACT.Exp, scale=neg_h[:, 0:1],
-                    accum_out=parts[i][:, u : u + 1],
+                    accum_out=parts[:, i, u : u + 1],
                 )
                 if i + 1 < TILES:
                     square_tensor(i + 1, u)
 
-        def sum_window(i):
-            nc.vector.reduce_sum(out=sum_win[i][:], in_=parts[i][:, 0:W_BANKS], axis=AX.X)
+        def sum_group(g):
+            four = slice(g * PACK, (g + 1) * PACK)
+            nc.vector.reduce_sum(out=sums[:, four], in_=parts[:, four, :], axis=AX.X)
 
-        def sum_all(i):
-            nc.vector.scalar_tensor_tensor(
-                out=sum_eps[i][:], in0=parts[i][:, W_BANKS : W_BANKS + 1], scalar=1e-10, in1=sum_win[i][:],
-                op0=ALU.add, op1=ALU.add,
-            )
+        def invert_group(g):
+            four = slice(g * PACK, (g + 1) * PACK)
+            nc.vector.tensor_scalar_add(out=sums_eps[:, four], in0=sums[:, four], scalar1=1e-10)
+            nc.vector.reciprocal(out=recip[:, four], in_=sums_eps[:, four])
+            nc.tensor.matmul(out=recip_ps[:, four], lhsT=ident_f[:], rhs=recip[:, four], start=True, stop=True)
 
-        def invert(i):
-            nc.vector.reciprocal(out=recip[i][:], in_=sum_eps[i][:])
-
-        def normalise(i, t0, width):
-            g, j = divmod(i, PACK)
-            if g not in wjs:
-                wjs[g] = wjpool.tile([P, PACK, TICKS], BF16, name="wj")
-            nc.vector.tensor_scalar_mul(
-                out=wjs[g][:, j, t0 : t0 + width], in0=gts[i][:, t0 : t0 + width], scalar1=recip[i][:, 0:1]
-            )
-
-        def regroup(g, t0, width):
+        def weigh(g, t0, width):
             n, off = divmod(t0, CHUNK)
             if off == 0:
                 wchs[(g, n)] = wchpool.tile([P, CHUNK, PACK], BF16, name="wch", align_bytes=64)
-            nc.vector.tensor_copy(
-                out=wchs[(g, n)][:, off : off + width, :].rearrange("p (c i) j -> p c j i", i=4),
-                in_=wjs[g][:, :, t0 : t0 + width].rearrange("p j (c i) -> p c j i", i=4),
+            four = slice(g * PACK, (g + 1) * PACK)
+            helper = width // 4 if width >= 512 else 0
+            mine = width - helper
+            if helper:
+                token = tokens[:, tokens_used[0] * PACK : (tokens_used[0] + 1) * PACK]
+                tokens_used[0] += 1
+                nc.vector.tensor_copy(out=token, in_=recip_ps[:, four])
+                nc.gpsimd.tensor_tensor(
+                    out=wchs[(g, n)][:, off + mine : off + width, :].rearrange("p (c i) j -> p c j i", i=4),
+                    in0=gts[g][:, :, t0 + mine : t0 + width].rearrange("p j (c i) -> p c j i", i=4),
+                    in1=token.unsqueeze(1).unsqueeze(3).to_broadcast([P, helper // 4, PACK, 4]),
+                    op=ALU.mult,
+                )
+            nc.vector.tensor_tensor(
+                out=wchs[(g, n)][:, off : off + mine, :].rearrange("p (c i) j -> p c j i", i=4),
+                in0=gts[g][:, :, t0 : t0 + mine].rearrange("p j (c i) -> p c j i", i=4),
+                in1=recip_ps[:, four].unsqueeze(1).unsqueeze(3).to_broadcast([P, mine // 4, PACK, 4]),
+                op=ALU.mult,
             )
 
         def quantise(g, t0, width):
@@ -169,10 +182,10 @@ def tile_flashrecomodel_t_kernel(tc, flashes_pe, flashes_time, flashes_confidenc
         banks = [0]
 
         def bank(all_eight):
-            q = banks[0] % 8
+            q = banks[0] % 7
             banks[0] += 1
-            if all_eight and q >= 5:
-                return dqpool.tile([P, N_TILE], F32, name="acc_dq", tag="dq%d" % (q - 5))
+            if all_eight and q >= 4:
+                return dqpool.tile([P, N_TILE], F32, name="acc_dq", tag="dq%d" % (q - 4))
             return accpool.tile([P, N_TILE], F32, name="acc")
 
         def multiply(b, t0, width, ms, all_eight):
@@ -217,36 +230,32 @@ def tile_flashrecomodel_t_kernel(tc, flashes_pe, flashes_time, flashes_confidenc
                 in_=stage[:, 0 : count * width].rearrange("p (m t) -> p m t", m=count),
             )
 
-        def slot(i, filler):
+        def slot(i):
+            k = i - PACK
+            g, n = divmod(k, N_CHUNKS)
+            if n == 0:
+                sum_group(g)
+            if k >= 1:
+                quantise((k - 1) // N_CHUNKS, ((k - 1) % N_CHUNKS) * CHUNK, CHUNK)
+            if n == 0:
+                invert_group(g)
             units = UNIT_SLOTS.get(i, ())
             todo = []
             if units:
                 todo = multiply(0, (units[0] // 2) * CHUNK, CHUNK, (2 * (units[0] % 2), 2 * (units[0] % 2) + 1), False)
-            if i not in VECTOR_SQUARES:
-                square_scalar(i)
+            square_scalar(i)
             exp_window(i)
             exp_rest(i)
-            k = i - PACK
-            sum_all(i - 1)
-            if k >= 1:
-                quantise((k - 1) // N_CHUNKS, ((k - 1) % N_CHUNKS) * CHUNK, CHUNK)
-            invert(i - 1)
-            filler(i)
+            distance_vector(i + 1)
+            weigh(g, n * CHUNK, CHUNK)
+            square_vector(i + 1)
             if todo:
                 copy_out(todo[0:1], "VV")
-            normalise(i - 1, 0, TICKS)
-            if i + 1 in VECTOR_SQUARES:
-                distance_vector(i + 1)
-            regroup(k // N_CHUNKS, (k % N_CHUNKS) * CHUNK, CHUNK)
-            if i + 1 in VECTOR_SQUARES:
-                square_vector(i + 1)
-            if todo:
                 copy_out(todo[1:2], "VA")
             for v in units[1:]:
                 todo = multiply(0, (v // 2) * CHUNK, CHUNK, (2 * (v % 2), 2 * (v % 2) + 1), False)
                 copy_out(todo[0:1], "VV")
                 copy_out(todo[1:2], "VA")
-            sum_window(i)
 
         with tc.tile_pool(name="prep", bufs=1) as prep:
             tm_bf = prep.tile([P, GROUPS, PACK], BF16)
@@ -274,6 +283,7 @@ def tile_flashrecomodel_t_kernel(tc, flashes_pe, flashes_time, flashes_confidenc
             tick_cols = prep.tile([P, W_BLOCKS, P], BF16)
             flash_cols = prep.tile([P, TILES, P], BF16)
             make_identity(nc, ident[:])
+            make_identity(nc, ident_f[:])
 
             warm_out = prep.tile([P, 1], F32)
             nc.scalar.activation(out=warm_out[:], in_=warm[:], func=ACT.Exp)
@@ -392,71 +402,53 @@ def tile_flashrecomodel_t_kernel(tc, flashes_pe, flashes_time, flashes_confidenc
             distance_vector(3)
             square_vector(2)
             square_vector(3)
-            exp_window(0)
-            sum_window(0)
-            sum_all(0)
-            nc.vector.tensor_copy(out=flash_rows[1][:], in_=tabs[3][:])
-            invert(0)
-            normalise(0, 0, TICKS)
-            exp_window(1)
-            sum_window(1)
-            scale_pe(1)
-            sum_all(1)
-            invert(1)
-            normalise(1, 0, TICKS)
-            exp_window(2)
-            exp_rest(2)
-            sum_window(2)
-            sum_all(2)
-            invert(2)
-            normalise(2, 0, TICKS)
-            exp_window(3)
-            exp_rest(3)
-            sum_window(3)
-
-            def quantise_pe(i):
-                g = i - PACK
-                if g + 1 in (2, 3):
-                    scale_pe(g + 1)
+            def quantise_pe(g):
                 nc.vector.quantize_mx(
                     out=pe_codes[g][:].bitcast(FP8X4), scales=pe_scales[g][:],
                     in_=spes[g][:].rearrange("p w j -> p (w j)"),
                 )
 
-            for i in range(PACK, 2 * PACK):
-                slot(i, quantise_pe)
+            exp_window(0)
+            nc.vector.tensor_copy(out=flash_rows[1][:], in_=tabs[3][:])
+            scale_pe(1)
+            quantise_pe(0)
+            exp_window(1)
+            scale_pe(2)
+            quantise_pe(1)
+            exp_window(2)
+            exp_rest(2)
+            scale_pe(3)
+            quantise_pe(2)
+            exp_window(3)
+            exp_rest(3)
+            distance_vector(4)
+            quantise_pe(3)
+            square_vector(4)
 
         with tc.tile_pool(name="c1pool", bufs=1) as c1pool, tc.tile_pool(name="stpool", bufs=4) as stpool:
             late["c1pool"] = c1pool
             late["stpool"] = stpool
 
-            def nothing(i):
-                return None
+            for i in range(PACK, TILES):
+                slot(i)
 
-            for i in range(2 * PACK, TILES):
-                slot(i, nothing)
-
-            last = TILES - 1
             g_last = GROUPS - 1
             blocks = []
             begin = 0
             for width in LAST_WIDTHS:
                 blocks.append((begin, width))
                 begin += width
-            sum_all(last)
+            sum_group(g_last)
             quantise(g_last - 1, TICKS - CHUNK, CHUNK)
-            invert(last)
-            normalise(last, blocks[0][0], blocks[0][1])
-            regroup(g_last, blocks[0][0], blocks[0][1])
+            invert_group(g_last)
+            weigh(g_last, blocks[0][0], blocks[0][1])
             for x in range(len(blocks)):
                 t0, width = blocks[x]
                 more = x + 1 < len(blocks)
                 if more:
-                    normalise(last, blocks[x + 1][0], blocks[x + 1][1])
+                    weigh(g_last, blocks[x + 1][0], blocks[x + 1][1])
                 quantise(g_last, t0, width)
                 todo = multiply(1, t0, width, (0, 1, 2, 3), True)
-                if more:
-                    regroup(g_last, blocks[x + 1][0], blocks[x + 1][1])
                 together = CHUNK // width
                 for a in range(0, len(todo), together):
                     copy_out(todo[a : a + together], "A" if more else "AV")

@@ -30,9 +30,10 @@ WINDOW = 1536
 W_BANKS = WINDOW // N_TILE
 W_BLOCKS = WINDOW // P
 REST = TICKS - WINDOW
-VECTOR_SQUARES = {2: REST, 3: REST, 4: 512, 5: 512, 6: 512, 7: 512}
-UNIT_SLOTS = {10: (0, 1), 11: (2,), 12: (3,), 13: (4, 5), 14: (6,), 15: (7,)}
-LAST_WIDTHS = (256, 256, 512, 512, 512, 512, 512, 1024)
+VECTOR_SQUARES = {1: 2560, 2: 2560, 3: 2560, 4: 512, 5: 512, 6: 512, 7: 512, 8: 512, 9: 512, 10: 512, 11: 512}
+LAST_WIDTHS = (512, 512, 512, 512, 512, 512, 512, 256, 256)
+LAST_HELP = (160, 160, 160, 160, 160, 160, 160, 64, 0)
+LAST_ENGINES = ("AAAA", "AAAA", "AAAA", "AAAA", "AAAA", "AAAV", "AVAV", "AV", "AV")
 
 FLOPS = 2 * EVENTS * FLASHES * CHANNELS * TICKS
 
@@ -142,12 +143,11 @@ def tile_flashrecomodel_t_kernel(tc, flashes_pe, flashes_time, flashes_confidenc
             nc.vector.reciprocal(out=recip[:, four], in_=sums_eps[:, four])
             nc.tensor.matmul(out=recip_ps[:, four], lhsT=ident_f[:], rhs=recip[:, four], start=True, stop=True)
 
-        def weigh(g, t0, width):
+        def weigh(g, t0, width, helper):
             n, off = divmod(t0, CHUNK)
             if off == 0:
                 wchs[(g, n)] = wchpool.tile([P, CHUNK, PACK], BF16, name="wch", align_bytes=64)
             four = slice(g * PACK, (g + 1) * PACK)
-            helper = width // 4 if width >= 512 else 0
             mine = width - helper
             if helper:
                 token = tokens[:, tokens_used[0] * PACK : (tokens_used[0] + 1) * PACK]
@@ -230,32 +230,29 @@ def tile_flashrecomodel_t_kernel(tc, flashes_pe, flashes_time, flashes_confidenc
                 in_=stage[:, 0 : count * width].rearrange("p (m t) -> p m t", m=count),
             )
 
-        def slot(i):
-            k = i - PACK
-            g, n = divmod(k, N_CHUNKS)
-            if n == 0:
-                sum_group(g)
-            if k >= 1:
-                quantise((k - 1) // N_CHUNKS, ((k - 1) % N_CHUNKS) * CHUNK, CHUNK)
-            if n == 0:
-                invert_group(g)
-            units = UNIT_SLOTS.get(i, ())
-            todo = []
-            if units:
-                todo = multiply(0, (units[0] // 2) * CHUNK, CHUNK, (2 * (units[0] % 2), 2 * (units[0] % 2) + 1), False)
+        def make_tile(i):
             square_scalar(i)
             exp_window(i)
             exp_rest(i)
-            distance_vector(i + 1)
-            weigh(g, n * CHUNK, CHUNK)
-            square_vector(i + 1)
-            if todo:
-                copy_out(todo[0:1], "VV")
-                copy_out(todo[1:2], "VA")
-            for v in units[1:]:
-                todo = multiply(0, (v // 2) * CHUNK, CHUNK, (2 * (v % 2), 2 * (v % 2) + 1), False)
-                copy_out(todo[0:1], "VV")
-                copy_out(todo[1:2], "VA")
+
+        def chunk(g, n, helper):
+            weigh(g, n * CHUNK, CHUNK, helper)
+
+        def codes(g, n):
+            quantise(g, n * CHUNK, CHUNK)
+
+        def unit(v):
+            return multiply(0, (v // 2) * CHUNK, CHUNK, (2 * (v % 2), 2 * (v % 2) + 1), False)
+
+        def empty(todo, engines):
+            copy_out(todo[0:1], engines[0:2])
+            copy_out(todo[1:2], engines[2:4])
+
+        def start_group(g):
+            sum_group(g)
+            invert_group(g)
+            if g >= 1:
+                codes(g - 1, N_CHUNKS - 1)
 
         with tc.tile_pool(name="prep", bufs=1) as prep:
             tm_bf = prep.tile([P, GROUPS, PACK], BF16)
@@ -313,8 +310,6 @@ def tile_flashrecomodel_t_kernel(tc, flashes_pe, flashes_time, flashes_confidenc
 
             square_scalar(0)
             exp_rest(0)
-            square_scalar(1)
-            exp_rest(1)
 
             spes = {}
 
@@ -389,48 +384,128 @@ def tile_flashrecomodel_t_kernel(tc, flashes_pe, flashes_time, flashes_confidenc
                 nc.tensor.transpose(tabs[a // 8][:, (a % 8) * P : (a % 8 + 1) * P], tick_cols[:, a, :], ident[:])
             for a in range(8):
                 nc.tensor.transpose(tabs[2][:, a * P : (a + 1) * P], flash_cols[:, a, :], ident[:])
-            distance_vector(2)
-            scale_pe(0)
-            nc.vector.tensor_copy(out=tick_rows[:, 0 : 8 * P], in_=tabs[0][:])
-            nc.vector.tensor_copy(out=tick_rows[:, 8 * P : WINDOW], in_=tabs[1][:, 0 : WINDOW - 8 * P])
-            nc.vector.tensor_copy(out=flash_rows[0][:], in_=tabs[2][:])
-
-            for u in range(W_BANKS):
-                square_tensor(0, u)
-            for a in range(8):
-                nc.tensor.transpose(tabs[3][:, a * P : (a + 1) * P], flash_cols[:, 8 + a, :], ident[:])
-            distance_vector(3)
-            square_vector(2)
-            square_vector(3)
             def quantise_pe(g):
                 nc.vector.quantize_mx(
                     out=pe_codes[g][:].bitcast(FP8X4), scales=pe_scales[g][:],
                     in_=spes[g][:].rearrange("p w j -> p (w j)"),
                 )
 
+            todos = {}
+            distance_vector(1)
+            nc.vector.tensor_copy(out=tick_rows[:, 0 : 8 * P], in_=tabs[0][:])
+            square_vector(1)
+            exp_rest(1)
+            nc.vector.tensor_copy(out=tick_rows[:, 8 * P : WINDOW], in_=tabs[1][:, 0 : WINDOW - 8 * P])
+            nc.vector.tensor_copy(out=flash_rows[0][:], in_=tabs[2][:])
+            for u in range(W_BANKS):
+                square_tensor(0, u)
+            for a in range(8):
+                nc.tensor.transpose(tabs[3][:, a * P : (a + 1) * P], flash_cols[:, 8 + a, :], ident[:])
+            distance_vector(2)
+            distance_vector(3)
+            square_vector(2)
+            square_vector(3)
             exp_window(0)
             nc.vector.tensor_copy(out=flash_rows[1][:], in_=tabs[3][:])
+            scale_pe(0)
             scale_pe(1)
             quantise_pe(0)
             exp_window(1)
-            scale_pe(2)
-            quantise_pe(1)
             exp_window(2)
             exp_rest(2)
-            scale_pe(3)
-            quantise_pe(2)
             exp_window(3)
             exp_rest(3)
             distance_vector(4)
-            quantise_pe(3)
+            quantise_pe(1)
             square_vector(4)
+            distance_vector(5)
+            sum_group(0)
+            square_vector(5)
+            invert_group(0)
+            make_tile(4)
+            chunk(0, 0, 320)
+            chunk(0, 1, 320)
+            codes(0, 0)
+            make_tile(5)
+            distance_vector(6)
+            chunk(0, 2, 320)
+            square_vector(6)
+            codes(0, 1)
+            distance_vector(7)
+            chunk(0, 3, 320)
+            square_vector(7)
+            make_tile(6)
+            scale_pe(2)
+            codes(0, 2)
+            scale_pe(3)
+            quantise_pe(2)
+            make_tile(7)
+            distance_vector(8)
+            quantise_pe(3)
+            distance_vector(9)
+            square_vector(8)
+            distance_vector(10)
+            square_vector(9)
+            distance_vector(11)
+            square_vector(10)
 
         with tc.tile_pool(name="c1pool", bufs=1) as c1pool, tc.tile_pool(name="stpool", bufs=4) as stpool:
             late["c1pool"] = c1pool
             late["stpool"] = stpool
-
-            for i in range(PACK, TILES):
-                slot(i)
+            sum_group(1)
+            invert_group(1)
+            codes(0, 3)
+            square_vector(11)
+            make_tile(8)
+            chunk(1, 0, 320)
+            chunk(1, 1, 320)
+            codes(1, 0)
+            todos[0] = unit(0)
+            make_tile(9)
+            chunk(1, 2, 320)
+            codes(1, 1)
+            chunk(1, 3, 320)
+            make_tile(10)
+            empty(todos[0], "VVVV")
+            codes(1, 2)
+            todos[1] = unit(1)
+            empty(todos[1], "VVVV")
+            todos[2] = unit(2)
+            empty(todos[2], "VVVV")
+            make_tile(11)
+            todos[3] = unit(3)
+            empty(todos[3], "VVVV")
+            distance_vector(12)
+            distance_vector(13)
+            square_vector(12)
+            square_vector(13)
+            sum_group(2)
+            invert_group(2)
+            codes(1, 3)
+            todos[4] = unit(4)
+            make_tile(12)
+            chunk(2, 0, 448)
+            empty(todos[4], "VVVV")
+            distance_vector(14)
+            todos[5] = unit(5)
+            make_tile(13)
+            codes(2, 0)
+            square_vector(14)
+            chunk(2, 1, 448)
+            empty(todos[5], "VVVV")
+            distance_vector(15)
+            todos[6] = unit(6)
+            make_tile(14)
+            codes(2, 1)
+            square_vector(15)
+            chunk(2, 2, 448)
+            empty(todos[6], "VVVV")
+            todos[7] = unit(7)
+            make_tile(15)
+            codes(2, 2)
+            chunk(2, 3, 448)
+            empty(todos[7], "AAAA")
+            codes(2, 3)
 
             g_last = GROUPS - 1
             blocks = []
@@ -438,17 +513,48 @@ def tile_flashrecomodel_t_kernel(tc, flashes_pe, flashes_time, flashes_confidenc
             for width in LAST_WIDTHS:
                 blocks.append((begin, width))
                 begin += width
-            sum_group(g_last)
-            quantise(g_last - 1, TICKS - CHUNK, CHUNK)
-            invert_group(g_last)
-            weigh(g_last, blocks[0][0], blocks[0][1])
-            for x in range(len(blocks)):
-                t0, width = blocks[x]
-                more = x + 1 < len(blocks)
-                if more:
-                    weigh(g_last, blocks[x + 1][0], blocks[x + 1][1])
-                quantise(g_last, t0, width)
-                todo = multiply(1, t0, width, (0, 1, 2, 3), True)
-                together = CHUNK // width
-                for a in range(0, len(todo), together):
-                    copy_out(todo[a : a + together], "A" if more else "AV")
+            lasts = {}
+
+            def empty_last(x):
+                together = CHUNK // blocks[x][1]
+                for a in range(0, len(lasts[x]), together):
+                    copy_out(lasts[x][a : a + together], LAST_ENGINES[x][a:] + LAST_ENGINES[x][:a])
+
+            sum_group(3)
+            invert_group(3)
+            weigh(g_last, blocks[0][0], blocks[0][1], LAST_HELP[0])
+            quantise(g_last, blocks[0][0], blocks[0][1])
+            lasts[0] = multiply(1, blocks[0][0], blocks[0][1], (0, 1, 2, 3), True)
+            weigh(g_last, blocks[1][0], blocks[1][1], LAST_HELP[1])
+            weigh(g_last, blocks[2][0], blocks[2][1], LAST_HELP[2])
+            quantise(g_last, blocks[1][0], blocks[1][1])
+            lasts[1] = multiply(1, blocks[1][0], blocks[1][1], (0, 1, 2, 3), True)
+            empty_last(0)
+            weigh(g_last, blocks[3][0], blocks[3][1], LAST_HELP[3])
+            quantise(g_last, blocks[2][0], blocks[2][1])
+            lasts[2] = multiply(1, blocks[2][0], blocks[2][1], (0, 1, 2, 3), True)
+            empty_last(1)
+            weigh(g_last, blocks[4][0], blocks[4][1], LAST_HELP[4])
+            quantise(g_last, blocks[3][0], blocks[3][1])
+            lasts[3] = multiply(1, blocks[3][0], blocks[3][1], (0, 1, 2, 3), True)
+            empty_last(2)
+            weigh(g_last, blocks[5][0], blocks[5][1], LAST_HELP[5])
+            quantise(g_last, blocks[4][0], blocks[4][1])
+            lasts[4] = multiply(1, blocks[4][0], blocks[4][1], (0, 1, 2, 3), True)
+            empty_last(3)
+            weigh(g_last, blocks[6][0], blocks[6][1], LAST_HELP[6])
+            quantise(g_last, blocks[5][0], blocks[5][1])
+            lasts[5] = multiply(1, blocks[5][0], blocks[5][1], (0, 1, 2, 3), True)
+            empty_last(4)
+            weigh(g_last, blocks[7][0], blocks[7][1], LAST_HELP[7])
+            quantise(g_last, blocks[6][0], blocks[6][1])
+            lasts[6] = multiply(1, blocks[6][0], blocks[6][1], (0, 1, 2, 3), True)
+            empty_last(5)
+            weigh(g_last, blocks[8][0], blocks[8][1], LAST_HELP[8])
+            quantise(g_last, blocks[7][0], blocks[7][1])
+            lasts[7] = multiply(1, blocks[7][0], blocks[7][1], (0, 1, 2, 3), True)
+            empty_last(6)
+            quantise(g_last, blocks[8][0], blocks[8][1])
+            lasts[8] = multiply(1, blocks[8][0], blocks[8][1], (0, 1, 2, 3), True)
+            empty_last(7)
+            empty_last(8)

@@ -28,12 +28,15 @@ N_CHUNKS = TICKS // CHUNK
 N_TILE = 512
 WINDOW = 1536
 W_BANKS = WINDOW // N_TILE
-W_BLOCKS = WINDOW // P
+TABLE = WINDOW + N_TILE
+T_BLOCKS = TABLE // P
 REST = TICKS - WINDOW
-VECTOR_SQUARES = {1: 2560, 2: 2560, 3: 2560, 4: 512, 5: 512, 6: 512, 7: 512, 8: 512, 9: 512, 10: 512, 11: 512}
-LAST_WIDTHS = (512, 512, 512, 512, 512, 512, 512, 256, 256)
-LAST_HELP = (160, 160, 160, 160, 160, 160, 160, 64, 0)
-LAST_ENGINES = ("AAAA", "AAAA", "AAAA", "AAAA", "AAAA", "AAAV", "AVAV", "AV", "AV")
+WIDER = (1, 2, 3)
+VECTOR_SQUARES = {1: 2048, 2: 2048, 3: 2048, 4: 512, 5: 512, 6: 512, 7: 512, 8: 512, 9: 512, 10: 512, 11: 512}
+GPSIMD_SQUARES = {4: 1024, 8: 1024, 12: 1792}
+LAST_WIDTHS = (512, 512, 512, 512, 512, 512, 512, 512)
+LAST_HELP = (160, 160, 160, 160, 160, 160, 160, 160)
+LAST_ENGINES = ("AAAA", "AAAA", "AAAA", "AAAA", "AAAA", "AAAV", "AVAV", "AVAV")
 
 FLOPS = 2 * EVENTS * FLASHES * CHANNELS * TICKS
 
@@ -50,19 +53,21 @@ def tile_flashrecomodel_t_kernel(tc, flashes_pe, flashes_time, flashes_confidenc
         dqpool = ctx.enter_context(tc.psum_pool(name="dqpool", bufs=1))
         accpool = ctx.enter_context(tc.psum_pool(name="accpool", bufs=4))
 
-        ticks = const.tile([P, TICKS - WINDOW], F32)
+        ticks = const.tile([P, REST], F32)
         negc = const.tile([P, TILES], F32)
         neg_h = const.tile([P, 1], F32)
-        parts = const.tile([P, TILES, W_BANKS + 1], F32)
+        parts = const.tile([P, TILES, W_BANKS + 2], F32)
         sums = const.tile([P, TILES], F32)
         sums_eps = const.tile([P, TILES], F32)
         recip = const.tile([P, TILES], F32)
-        recip_ps = dqpool.tile([P, TILES], F32, name="recip_ps")
+        factors_ps = dqpool.tile([P, 2 * TILES], F32, name="factors_ps")
+        recip_ps = factors_ps[:, 0:TILES]
+        cf_ps = factors_ps[:, TILES : 2 * TILES]
         ident = const.tile([P, P], BF16)
         ident_f = const.tile([P, P], F32)
         tokens = const.tile([P, 32 * PACK], F32)
         tokens_used = [0]
-        tick_rows = const.tile([P, WINDOW], BF16)
+        tick_rows = const.tile([P, TABLE], BF16)
         flash_rows = [const.tile([P, 8 * P], BF16, name="flash_rows%d" % a) for a in range(2)]
         pe_codes = []
         pe_scales = []
@@ -76,7 +81,7 @@ def tile_flashrecomodel_t_kernel(tc, flashes_pe, flashes_time, flashes_confidenc
         w_codes = {}
         w_scales = {}
         late = {}
-        rest = slice(WINDOW, TICKS)
+        todos = {}
 
         def g_tile(i):
             g, j = divmod(i, PACK)
@@ -84,37 +89,62 @@ def tile_flashrecomodel_t_kernel(tc, flashes_pe, flashes_time, flashes_confidenc
                 gts[g] = gpool.tile([P, PACK, TICKS], F32, name="gg")
             return gts[g][:, j, :]
 
-        def square_scalar(i):
-            lo = VECTOR_SQUARES.get(i, 0)
-            if lo < REST:
-                nc.scalar.activation(
-                    out=g_tile(i)[:, WINDOW + lo : TICKS], in_=ticks[:, lo:REST], func=ACT.Square,
-                    bias=negc[:, i : i + 1], scale=1.0,
-                )
+        def first_rest(i):
+            return TABLE if i in WIDER else WINDOW
+
+        def token(src):
+            width = src.shape[1]
+            dst = tokens[:, tokens_used[0] * PACK : tokens_used[0] * PACK + width]
+            tokens_used[0] += 1
+            nc.vector.tensor_copy(out=dst, in_=src)
+            return dst
 
         def distance_vector(i):
-            hi = VECTOR_SQUARES.get(i, 0)
-            if hi > 0:
+            lo = first_rest(i)
+            hi = lo + VECTOR_SQUARES.get(i, 0)
+            if hi > lo:
                 nc.vector.tensor_scalar_add(
-                    out=g_tile(i)[:, WINDOW : WINDOW + hi], in0=ticks[:, 0:hi], scalar1=negc[:, i : i + 1]
+                    out=g_tile(i)[:, lo:hi], in0=ticks[:, lo - WINDOW : hi - WINDOW], scalar1=negc[:, i : i + 1]
                 )
 
         def square_vector(i):
-            hi = VECTOR_SQUARES.get(i, 0)
-            if hi > 0:
-                gt = g_tile(i)[:, WINDOW : WINDOW + hi]
+            lo = first_rest(i)
+            hi = lo + VECTOR_SQUARES.get(i, 0)
+            if hi > lo:
+                gt = g_tile(i)[:, lo:hi]
                 nc.vector.tensor_tensor(out=gt, in0=gt, in1=gt, op=ALU.mult)
 
+        def square_gpsimd(i):
+            lo = first_rest(i) + VECTOR_SQUARES.get(i, 0)
+            hi = lo + GPSIMD_SQUARES.get(i, 0)
+            if hi > lo:
+                gt = g_tile(i)[:, lo:hi]
+                nc.gpsimd.tensor_scalar(
+                    out=gt, in0=ticks[:, lo - WINDOW : hi - WINDOW], scalar1=token(negc[:, i : i + 1]), scalar2=1.0,
+                    op0=ALU.add, op1=ALU.mult,
+                )
+                nc.gpsimd.tensor_tensor(out=gt, in0=gt, in1=gt, op=ALU.mult)
+
+        def square_scalar(i):
+            lo = first_rest(i) + VECTOR_SQUARES.get(i, 0) + GPSIMD_SQUARES.get(i, 0)
+            if lo < TICKS:
+                nc.scalar.activation(
+                    out=g_tile(i)[:, lo:TICKS], in_=ticks[:, lo - WINDOW : REST], func=ACT.Square,
+                    bias=negc[:, i : i + 1], scale=1.0,
+                )
+
         def exp_rest(i):
-            gt = g_tile(i)
+            gt = g_tile(i)[:, first_rest(i) : TICKS]
             nc.scalar.activation(
-                out=gt[:, rest], in_=gt[:, rest], func=ACT.Exp, scale=neg_h[:, 0:1],
-                accum_out=parts[:, i, W_BANKS : W_BANKS + 1],
+                out=gt, in_=gt, func=ACT.Exp, scale=neg_h[:, 0:1], accum_out=parts[:, i, W_BANKS : W_BANKS + 1],
             )
 
         def square_tensor(i, u):
-            dq = dqpool.tile([P, N_TILE], F32, name="dq%d" % u)
-            dqs[u] = dq
+            if u < W_BANKS:
+                dq = dqpool.tile([P, N_TILE], F32, name="dq%d" % u)
+            else:
+                dq = accpool.tile([P, N_TILE], F32, name="dq_wider", tag="acc")
+            dqs[(i, u)] = dq
             nc.tensor.matmul(
                 out=dq[:],
                 lhsT=flash_rows[i // 8][:, (i % 8) * P : (i % 8 + 1) * P],
@@ -123,13 +153,16 @@ def tile_flashrecomodel_t_kernel(tc, flashes_pe, flashes_time, flashes_confidenc
                 stop=True,
             )
 
+        def exp_bank(i, u):
+            column = u if u < W_BANKS else W_BANKS + 1
+            nc.scalar.activation(
+                out=g_tile(i)[:, u * N_TILE : (u + 1) * N_TILE], in_=dqs[(i, u)][:], func=ACT.Exp, scale=neg_h[:, 0:1],
+                accum_out=parts[:, i, column : column + 1],
+            )
+
         def exp_window(i):
-            gt = g_tile(i)
             for u in range(W_BANKS):
-                nc.scalar.activation(
-                    out=gt[:, u * N_TILE : (u + 1) * N_TILE], in_=dqs[u][:], func=ACT.Exp, scale=neg_h[:, 0:1],
-                    accum_out=parts[:, i, u : u + 1],
-                )
+                exp_bank(i, u)
                 if i + 1 < TILES:
                     square_tensor(i + 1, u)
 
@@ -150,13 +183,10 @@ def tile_flashrecomodel_t_kernel(tc, flashes_pe, flashes_time, flashes_confidenc
             four = slice(g * PACK, (g + 1) * PACK)
             mine = width - helper
             if helper:
-                token = tokens[:, tokens_used[0] * PACK : (tokens_used[0] + 1) * PACK]
-                tokens_used[0] += 1
-                nc.vector.tensor_copy(out=token, in_=recip_ps[:, four])
                 nc.gpsimd.tensor_tensor(
                     out=wchs[(g, n)][:, off + mine : off + width, :].rearrange("p (c i) j -> p c j i", i=4),
                     in0=gts[g][:, :, t0 + mine : t0 + width].rearrange("p j (c i) -> p c j i", i=4),
-                    in1=token.unsqueeze(1).unsqueeze(3).to_broadcast([P, helper // 4, PACK, 4]),
+                    in1=token(recip_ps[:, four]).unsqueeze(1).unsqueeze(3).to_broadcast([P, helper // 4, PACK, 4]),
                     op=ALU.mult,
                 )
             nc.vector.tensor_tensor(
@@ -181,14 +211,14 @@ def tile_flashrecomodel_t_kernel(tc, flashes_pe, flashes_time, flashes_confidenc
 
         banks = [0]
 
-        def bank(all_eight):
+        def bank(all_seven):
             q = banks[0] % 7
             banks[0] += 1
-            if all_eight and q >= 4:
+            if all_seven and q >= 4:
                 return dqpool.tile([P, N_TILE], F32, name="acc_dq", tag="dq%d" % (q - 4))
             return accpool.tile([P, N_TILE], F32, name="acc")
 
-        def multiply(b, t0, width, ms, all_eight):
+        def multiply(b, t0, width, ms, all_seven):
             n, off = divmod(t0, CHUNK)
             todo = []
             for m in ms:
@@ -197,7 +227,7 @@ def tile_flashrecomodel_t_kernel(tc, flashes_pe, flashes_time, flashes_confidenc
                 for x0 in range(0, width, N_TILE):
                     nw = min(N_TILE, width - x0)
                     n_cols = slice(off + x0, off + x0 + nw)
-                    acc = bank(all_eight)
+                    acc = bank(all_seven)
                     for c in range(PASSES):
                         nc.tensor.matmul_mx(
                             out=acc[:, 0:nw],
@@ -210,6 +240,29 @@ def tile_flashrecomodel_t_kernel(tc, flashes_pe, flashes_time, flashes_confidenc
                         )
                     pieces.append((acc, x0, nw))
                 todo.append((b, m, t0, width, pieces))
+            return todo
+
+        def pass_of(b, c, t0, width, todo):
+            n, off = divmod(t0, CHUNK)
+            for unused_b, m, unused_t, unused_w, pieces in todo:
+                m_cols = slice(m * P, (m + 1) * P)
+                for acc, x0, nw in pieces:
+                    n_cols = slice(off + x0, off + x0 + nw)
+                    nc.tensor.matmul_mx(
+                        out=acc[:, 0:nw],
+                        lhsT=pe_codes[b * PASSES + c][:, m_cols].bitcast(FP8X4),
+                        lhsT_scale=pe_scales[b * PASSES + c][:, m_cols],
+                        rhs=w_codes[(c, n)][:, n_cols].bitcast(FP8X4),
+                        rhs_scale=w_scales[(c, n)][:, n_cols],
+                        start=(c == 0),
+                        stop=(c == PASSES - 1),
+                    )
+
+        def open_block(b, t0, width):
+            todo = []
+            for m in range(CHANNELS // P):
+                todo.append((b, m, t0, width, [(bank(True), 0, width)]))
+            pass_of(b, 0, t0, width, todo)
             return todo
 
         def copy_out(items, engines):
@@ -248,12 +301,6 @@ def tile_flashrecomodel_t_kernel(tc, flashes_pe, flashes_time, flashes_confidenc
             copy_out(todo[0:1], engines[0:2])
             copy_out(todo[1:2], engines[2:4])
 
-        def start_group(g):
-            sum_group(g)
-            invert_group(g)
-            if g >= 1:
-                codes(g - 1, N_CHUNKS - 1)
-
         with tc.tile_pool(name="prep", bufs=1) as prep:
             tm_bf = prep.tile([P, GROUPS, PACK], BF16)
             nc.sync.dma_start(
@@ -275,25 +322,26 @@ def tile_flashrecomodel_t_kernel(tc, flashes_pe, flashes_time, flashes_confidenc
             nc.gpsimd.iota(tick_i[:], pattern=[[1, seed]], base=WINDOW, channel_multiplier=0)
             warm = prep.tile([P, 1], F32)
             nc.gpsimd.memset(warm[:], 0.0)
-            tcol_i = prep.tile([P, W_BLOCKS], I32)
-            nc.gpsimd.iota(tcol_i[:], pattern=[[P, W_BLOCKS]], base=0, channel_multiplier=1)
-            tick_cols = prep.tile([P, W_BLOCKS, P], BF16)
+            tcol_i = prep.tile([P, T_BLOCKS], I32)
+            nc.gpsimd.iota(tcol_i[:], pattern=[[P, T_BLOCKS]], base=0, channel_multiplier=1)
+            tick_cols = prep.tile([P, T_BLOCKS, P], BF16)
             flash_cols = prep.tile([P, TILES, P], BF16)
             make_identity(nc, ident[:])
-            make_identity(nc, ident_f[:])
 
             warm_out = prep.tile([P, 1], F32)
             nc.scalar.activation(out=warm_out[:], in_=warm[:], func=ACT.Exp)
+            nc.scalar.copy(out=ident_f[:], in_=ident[:])
 
             nc.vector.tensor_copy(out=ticks[:, 0:seed], in_=tick_i[:])
             have = seed
-            while have < TICKS - WINDOW:
-                more = min(have, TICKS - WINDOW - have)
+            while have < REST:
+                more = min(have, REST - have)
                 nc.vector.tensor_scalar_add(out=ticks[:, have : have + more], in0=ticks[:, 0:more], scalar1=float(have))
                 have += more
 
             nc.vector.memset(tick_cols[:].rearrange("p a k -> p (a k)").bitcast(I32), 0)
             nc.vector.memset(flash_cols[:].rearrange("p a k -> p (a k)").bitcast(I32), 0)
+            nc.vector.memset(parts[:].rearrange("p a k -> p (a k)"), 0.0)
 
             sig2 = prep.tile([P, 1], F32)
             inv2 = prep.tile([P, 1], F32)
@@ -304,9 +352,12 @@ def tile_flashrecomodel_t_kernel(tc, flashes_pe, flashes_time, flashes_confidenc
             nc.vector.tensor_tensor(out=sig2[:], in0=sig_bf[:], in1=sig_bf[:], op=ALU.mult)
             nc.vector.tensor_scalar_max(out=negc[:], in0=negc[:], scalar1=-float(TICKS - 1))
             nc.vector.reciprocal(out=inv2[:], in_=sig2[:])
-            tcol = prep.tile([P, W_BLOCKS], F32)
+            tcol = prep.tile([P, T_BLOCKS], F32)
             nc.vector.tensor_copy(out=tcol[:], in_=tcol_i[:])
             nc.vector.tensor_scalar_mul(out=neg_h[:], in0=inv2[:], scalar1=-0.5)
+            cf_f = prep.tile([P, TILES], F32)
+            nc.vector.tensor_copy(out=cf_f[:], in_=cf_bf[:].rearrange("p g j -> p (g j)"))
+            nc.tensor.matmul(out=cf_ps, lhsT=ident_f[:], rhs=cf_f[:], start=True, stop=True)
 
             square_scalar(0)
             exp_rest(0)
@@ -318,14 +369,20 @@ def tile_flashrecomodel_t_kernel(tc, flashes_pe, flashes_time, flashes_confidenc
                 nc.vector.tensor_tensor(
                     out=spes[g][:],
                     in0=pe_raw[:, g].rearrange("p j w -> p w j"),
-                    in1=cf_bf[:, g].unsqueeze(1).to_broadcast([P, CHANNELS, PACK]),
+                    in1=cf_ps[:, g * PACK : (g + 1) * PACK].unsqueeze(1).to_broadcast([P, CHANNELS, PACK]),
                     op=ALU.mult,
                 )
 
-            t_sq = prep.tile([P, W_BLOCKS], F32)
-            t_rem1 = prep.tile([P, W_BLOCKS], F32)
-            t_rem2 = prep.tile([P, W_BLOCKS], F32)
-            t_lo = prep.tile([P, W_BLOCKS], F32)
+            def quantise_pe(g):
+                nc.vector.quantize_mx(
+                    out=pe_codes[g][:].bitcast(FP8X4), scales=pe_scales[g][:],
+                    in_=spes[g][:].rearrange("p w j -> p (w j)"),
+                )
+
+            t_sq = prep.tile([P, T_BLOCKS], F32)
+            t_rem1 = prep.tile([P, T_BLOCKS], F32)
+            t_rem2 = prep.tile([P, T_BLOCKS], F32)
+            t_lo = prep.tile([P, T_BLOCKS], F32)
             a_full = prep.tile([P, TILES], F32)
             a_lo = prep.tile([P, TILES], F32)
             c_sq = prep.tile([P, TILES], F32)
@@ -359,9 +416,9 @@ def tile_flashrecomodel_t_kernel(tc, flashes_pe, flashes_time, flashes_confidenc
                     cast(flash_cols[:, :, 9], c_rem2[:]),
                 ],
                 [
-                    cast(tick_cols[:, :, 3:6:2], twice(tcol[:], W_BLOCKS)),
+                    cast(tick_cols[:, :, 3:6:2], twice(tcol[:], T_BLOCKS)),
                     combine(t_lo[:], tcol[:], tick_cols[:, :, 3], ALU.subtract),
-                    cast(tick_cols[:, :, 4:7:2], twice(t_lo[:], W_BLOCKS)),
+                    cast(tick_cols[:, :, 4:7:2], twice(t_lo[:], T_BLOCKS)),
                     lambda: nc.vector.memset(tick_cols[:, :, 7:10], 1.0),
                 ],
                 [
@@ -380,40 +437,40 @@ def tile_flashrecomodel_t_kernel(tc, flashes_pe, flashes_time, flashes_confidenc
             tabs = []
             for a in range(4):
                 tabs.append(accpool.tile([P, 8 * P], BF16, name="tab%d" % a, tag="acc"))
-            for a in range(W_BLOCKS):
+            for a in range(T_BLOCKS):
                 nc.tensor.transpose(tabs[a // 8][:, (a % 8) * P : (a % 8 + 1) * P], tick_cols[:, a, :], ident[:])
             for a in range(8):
                 nc.tensor.transpose(tabs[2][:, a * P : (a + 1) * P], flash_cols[:, a, :], ident[:])
-            def quantise_pe(g):
-                nc.vector.quantize_mx(
-                    out=pe_codes[g][:].bitcast(FP8X4), scales=pe_scales[g][:],
-                    in_=spes[g][:].rearrange("p w j -> p (w j)"),
-                )
-
-            todos = {}
             distance_vector(1)
             nc.vector.tensor_copy(out=tick_rows[:, 0 : 8 * P], in_=tabs[0][:])
             square_vector(1)
             exp_rest(1)
-            nc.vector.tensor_copy(out=tick_rows[:, 8 * P : WINDOW], in_=tabs[1][:, 0 : WINDOW - 8 * P])
+            nc.vector.tensor_copy(out=tick_rows[:, 8 * P : TABLE], in_=tabs[1][:])
             nc.vector.tensor_copy(out=flash_rows[0][:], in_=tabs[2][:])
             for u in range(W_BANKS):
                 square_tensor(0, u)
             for a in range(8):
                 nc.tensor.transpose(tabs[3][:, a * P : (a + 1) * P], flash_cols[:, 8 + a, :], ident[:])
+            square_tensor(1, W_BANKS)
             distance_vector(2)
             distance_vector(3)
             square_vector(2)
             square_vector(3)
             exp_window(0)
+            exp_bank(1, W_BANKS)
+            square_tensor(2, W_BANKS)
             nc.vector.tensor_copy(out=flash_rows[1][:], in_=tabs[3][:])
+            square_gpsimd(4)
             scale_pe(0)
             scale_pe(1)
             quantise_pe(0)
             exp_window(1)
+            exp_bank(2, W_BANKS)
+            square_tensor(3, W_BANKS)
             exp_window(2)
             exp_rest(2)
             exp_window(3)
+            exp_bank(3, W_BANKS)
             exp_rest(3)
             distance_vector(4)
             quantise_pe(1)
@@ -435,9 +492,10 @@ def tile_flashrecomodel_t_kernel(tc, flashes_pe, flashes_time, flashes_confidenc
             chunk(0, 3, 320)
             square_vector(7)
             make_tile(6)
+            square_gpsimd(8)
             scale_pe(2)
-            codes(0, 2)
             scale_pe(3)
+            codes(0, 2)
             quantise_pe(2)
             make_tile(7)
             distance_vector(8)
@@ -469,16 +527,13 @@ def tile_flashrecomodel_t_kernel(tc, flashes_pe, flashes_time, flashes_confidenc
             empty(todos[0], "VVVV")
             codes(1, 2)
             todos[1] = unit(1)
+            square_gpsimd(12)
             empty(todos[1], "VVVV")
             todos[2] = unit(2)
             empty(todos[2], "VVVV")
             make_tile(11)
             todos[3] = unit(3)
             empty(todos[3], "VVVV")
-            distance_vector(12)
-            distance_vector(13)
-            square_vector(12)
-            square_vector(13)
             sum_group(2)
             invert_group(2)
             codes(1, 3)
@@ -486,18 +541,14 @@ def tile_flashrecomodel_t_kernel(tc, flashes_pe, flashes_time, flashes_confidenc
             make_tile(12)
             chunk(2, 0, 448)
             empty(todos[4], "VVVV")
-            distance_vector(14)
             todos[5] = unit(5)
             make_tile(13)
             codes(2, 0)
-            square_vector(14)
             chunk(2, 1, 448)
             empty(todos[5], "VVVV")
-            distance_vector(15)
             todos[6] = unit(6)
             make_tile(14)
             codes(2, 1)
-            square_vector(15)
             chunk(2, 2, 448)
             empty(todos[6], "VVVV")
             todos[7] = unit(7)
@@ -522,39 +573,43 @@ def tile_flashrecomodel_t_kernel(tc, flashes_pe, flashes_time, flashes_confidenc
 
             sum_group(3)
             invert_group(3)
+            lasts[0] = open_block(1, blocks[0][0], blocks[0][1])
             weigh(g_last, blocks[0][0], blocks[0][1], LAST_HELP[0])
             quantise(g_last, blocks[0][0], blocks[0][1])
-            lasts[0] = multiply(1, blocks[0][0], blocks[0][1], (0, 1, 2, 3), True)
+            pass_of(1, 1, blocks[0][0], blocks[0][1], lasts[0])
+            lasts[1] = open_block(1, blocks[1][0], blocks[1][1])
             weigh(g_last, blocks[1][0], blocks[1][1], LAST_HELP[1])
             weigh(g_last, blocks[2][0], blocks[2][1], LAST_HELP[2])
             quantise(g_last, blocks[1][0], blocks[1][1])
-            lasts[1] = multiply(1, blocks[1][0], blocks[1][1], (0, 1, 2, 3), True)
+            pass_of(1, 1, blocks[1][0], blocks[1][1], lasts[1])
+            lasts[2] = open_block(1, blocks[2][0], blocks[2][1])
             empty_last(0)
             weigh(g_last, blocks[3][0], blocks[3][1], LAST_HELP[3])
             quantise(g_last, blocks[2][0], blocks[2][1])
-            lasts[2] = multiply(1, blocks[2][0], blocks[2][1], (0, 1, 2, 3), True)
+            pass_of(1, 1, blocks[2][0], blocks[2][1], lasts[2])
+            lasts[3] = open_block(1, blocks[3][0], blocks[3][1])
             empty_last(1)
             weigh(g_last, blocks[4][0], blocks[4][1], LAST_HELP[4])
             quantise(g_last, blocks[3][0], blocks[3][1])
-            lasts[3] = multiply(1, blocks[3][0], blocks[3][1], (0, 1, 2, 3), True)
+            pass_of(1, 1, blocks[3][0], blocks[3][1], lasts[3])
+            lasts[4] = open_block(1, blocks[4][0], blocks[4][1])
             empty_last(2)
             weigh(g_last, blocks[5][0], blocks[5][1], LAST_HELP[5])
             quantise(g_last, blocks[4][0], blocks[4][1])
-            lasts[4] = multiply(1, blocks[4][0], blocks[4][1], (0, 1, 2, 3), True)
+            pass_of(1, 1, blocks[4][0], blocks[4][1], lasts[4])
+            lasts[5] = open_block(1, blocks[5][0], blocks[5][1])
             empty_last(3)
             weigh(g_last, blocks[6][0], blocks[6][1], LAST_HELP[6])
             quantise(g_last, blocks[5][0], blocks[5][1])
-            lasts[5] = multiply(1, blocks[5][0], blocks[5][1], (0, 1, 2, 3), True)
+            pass_of(1, 1, blocks[5][0], blocks[5][1], lasts[5])
+            lasts[6] = open_block(1, blocks[6][0], blocks[6][1])
             empty_last(4)
             weigh(g_last, blocks[7][0], blocks[7][1], LAST_HELP[7])
             quantise(g_last, blocks[6][0], blocks[6][1])
-            lasts[6] = multiply(1, blocks[6][0], blocks[6][1], (0, 1, 2, 3), True)
+            pass_of(1, 1, blocks[6][0], blocks[6][1], lasts[6])
+            lasts[7] = open_block(1, blocks[7][0], blocks[7][1])
             empty_last(5)
-            weigh(g_last, blocks[8][0], blocks[8][1], LAST_HELP[8])
             quantise(g_last, blocks[7][0], blocks[7][1])
-            lasts[7] = multiply(1, blocks[7][0], blocks[7][1], (0, 1, 2, 3), True)
+            pass_of(1, 1, blocks[7][0], blocks[7][1], lasts[7])
             empty_last(6)
-            quantise(g_last, blocks[8][0], blocks[8][1])
-            lasts[8] = multiply(1, blocks[8][0], blocks[8][1], (0, 1, 2, 3), True)
             empty_last(7)
-            empty_last(8)

@@ -32,8 +32,8 @@ TABLE = WINDOW + N_TILE
 T_BLOCKS = TABLE // P
 REST = TICKS - WINDOW
 WIDER = (1, 2, 3)
-VECTOR_SQUARES = {1: 2048, 2: 2048, 3: 2048, 4: 512, 5: 512, 6: 512, 7: 512, 8: 512, 9: 512, 10: 512, 11: 512}
-GPSIMD_SQUARES = {4: 1024, 8: 1024, 12: 1792}
+VECTOR_SQUARES = {1: 2048, 2: 2048, 3: 2048, 4: 512, 5: 512, 6: 512, 7: 512, 8: 256, 9: 256, 10: 256, 11: 256}
+GPSIMD_SQUARES = {4: 1024, 8: 1024, 12: 2560}
 LAST_WIDTHS = (512, 512, 512, 512, 512, 512, 512, 512)
 LAST_HELP = (160, 160, 160, 160, 160, 160, 160, 160)
 LAST_ENGINES = ("AAAA", "AAAA", "AAAA", "AAAA", "AAAA", "AAAV", "AVAV", "AVAV")
@@ -524,10 +524,10 @@ def tile_flashrecomodel_t_kernel(tc, flashes_pe, flashes_time, flashes_confidenc
             codes(1, 1)
             chunk(1, 3, 320)
             make_tile(10)
-            empty(todos[0], "VVVV")
             codes(1, 2)
-            todos[1] = unit(1)
             square_gpsimd(12)
+            empty(todos[0], "VVVV")
+            todos[1] = unit(1)
             empty(todos[1], "VVVV")
             todos[2] = unit(2)
             empty(todos[2], "VVVV")
@@ -554,7 +554,7 @@ def tile_flashrecomodel_t_kernel(tc, flashes_pe, flashes_time, flashes_confidenc
             todos[7] = unit(7)
             make_tile(15)
             codes(2, 2)
-            chunk(2, 3, 448)
+            chunk(2, 3, 320)
             empty(todos[7], "AAAA")
             codes(2, 3)
 

@@ -32,7 +32,7 @@ TABLE = WINDOW + N_TILE
 T_BLOCKS = TABLE // P
 REST = TICKS - WINDOW
 WIDER = (1, 2, 3)
-VECTOR_SQUARES = {1: 2048, 2: 2048, 3: 2048, 4: 512, 5: 512, 6: 512, 7: 512, 8: 256, 9: 256, 10: 256, 11: 256}
+VECTOR_SQUARES = {1: 2048, 2: 2048, 3: 2048, 4: 256, 5: 256, 6: 256, 7: 256}
 GPSIMD_SQUARES = {4: 1024, 8: 1024, 12: 2560}
 LAST_WIDTHS = (512, 512, 512, 512, 512, 512, 512, 512)
 LAST_HELP = (160, 160, 160, 160, 160, 160, 160, 160)

@@ -32,7 +32,7 @@ TABLE = WINDOW + N_TILE
 T_BLOCKS = TABLE // P
 REST = TICKS - WINDOW
 WIDER = (1, 2, 3)
-VECTOR_SQUARES = {1: 2048, 2: 2048, 3: 2048, 4: 256, 5: 256, 6: 256, 7: 256}
+VECTOR_SQUARES = {1: 2048, 2: 2048, 3: 2048, 4: 512, 5: 512, 6: 512, 7: 512}
 GPSIMD_SQUARES = {4: 1024, 8: 1024, 12: 2560}
 LAST_WIDTHS = (512, 512, 512, 512, 512, 512, 512, 512)
 LAST_HELP = (160, 160, 160, 160, 160, 160, 160, 160)
@@ -56,9 +56,8 @@ def tile_flashrecomodel_t_kernel(tc, flashes_pe, flashes_time, flashes_confidenc
         ticks = const.tile([P, REST], F32)
         negc = const.tile([P, TILES], F32)
         neg_h = const.tile([P, 1], F32)
-        parts = const.tile([P, TILES, W_BANKS + 2], F32)
+        parts = const.tile([P, TILES, W_BANKS + 3], F32)
         sums = const.tile([P, TILES], F32)
-        sums_eps = const.tile([P, TILES], F32)
         recip = const.tile([P, TILES], F32)
         factors_ps = dqpool.tile([P, 2 * TILES], F32, name="factors_ps")
         recip_ps = factors_ps[:, 0:TILES]
@@ -172,8 +171,7 @@ def tile_flashrecomodel_t_kernel(tc, flashes_pe, flashes_time, flashes_confidenc
 
         def invert_group(g):
             four = slice(g * PACK, (g + 1) * PACK)
-            nc.vector.tensor_scalar_add(out=sums_eps[:, four], in0=sums[:, four], scalar1=1e-10)
-            nc.vector.reciprocal(out=recip[:, four], in_=sums_eps[:, four])
+            nc.vector.reciprocal(out=recip[:, four], in_=sums[:, four])
             nc.tensor.matmul(out=recip_ps[:, four], lhsT=ident_f[:], rhs=recip[:, four], start=True, stop=True)
 
         def weigh(g, t0, width, helper):
@@ -186,7 +184,9 @@ def tile_flashrecomodel_t_kernel(tc, flashes_pe, flashes_time, flashes_confidenc
                 nc.gpsimd.tensor_tensor(
                     out=wchs[(g, n)][:, off + mine : off + width, :].rearrange("p (c i) j -> p c j i", i=4),
                     in0=gts[g][:, :, t0 + mine : t0 + width].rearrange("p j (c i) -> p c j i", i=4),
-                    in1=token(recip_ps[:, four]).unsqueeze(1).unsqueeze(3).to_broadcast([P, helper // 4, PACK, 4]),
+                    in1=(token(recip_ps[:, four]) if g >= 2 else recip[:, four]).unsqueeze(1).unsqueeze(3).to_broadcast(
+                        [P, helper // 4, PACK, 4]
+                    ),
                     op=ALU.mult,
                 )
             nc.vector.tensor_tensor(
@@ -342,6 +342,7 @@ def tile_flashrecomodel_t_kernel(tc, flashes_pe, flashes_time, flashes_confidenc
             nc.vector.memset(tick_cols[:].rearrange("p a k -> p (a k)").bitcast(I32), 0)
             nc.vector.memset(flash_cols[:].rearrange("p a k -> p (a k)").bitcast(I32), 0)
             nc.vector.memset(parts[:].rearrange("p a k -> p (a k)"), 0.0)
+            nc.vector.tensor_scalar_add(out=parts[:, :, W_BANKS + 2], in0=parts[:, :, W_BANKS + 2], scalar1=1e-10)
 
             sig2 = prep.tile([P, 1], F32)
             inv2 = prep.tile([P, 1], F32)

@@ -30,13 +30,14 @@ WINDOW = 1536
 W_BANKS = WINDOW // N_TILE
 TABLE = WINDOW + N_TILE
 T_BLOCKS = TABLE // P
+PIECES = 10
 REST = TICKS - WINDOW
+SEED = 512
 WIDER = (1, 2, 3)
-VECTOR_SQUARES = {1: 2048, 2: 2048, 3: 2048, 4: 512, 5: 512, 6: 512, 7: 512}
-GPSIMD_SQUARES = {4: 1024, 8: 1024, 12: 2560}
-LAST_WIDTHS = (512, 512, 512, 512, 512, 512, 512, 512)
-LAST_HELP = (160, 160, 160, 160, 160, 160, 160, 160)
-LAST_ENGINES = ("AAAA", "AAAA", "AAAA", "AAAA", "AAAA", "AAAV", "AVAV", "AVAV")
+VECTOR_TILES = (1, 2, 3, 6, 9, 13, 14)
+STEEPEST = 64.0
+LAST_WIDTHS = (512,) * 8
+LAST_ENGINES = ("AAAA",) * 5 + ("AAAV", "AVAV", "AVAV")
 
 FLOPS = 2 * EVENTS * FLASHES * CHANNELS * TICKS
 
@@ -48,14 +49,18 @@ def tile_flashrecomodel_t_kernel(tc, flashes_pe, flashes_time, flashes_confidenc
         ctx.enter_context(tc.manual_schedule())
         const = ctx.enter_context(tc.tile_pool(name="const", bufs=1))
         gpool = ctx.enter_context(tc.tile_pool(name="gpool", bufs=2))
-        wchpool = ctx.enter_context(tc.tile_pool(name="wchpool", bufs=2))
+        wchpool = ctx.enter_context(tc.tile_pool(name="wchpool", bufs=1))
         c0pool = ctx.enter_context(tc.tile_pool(name="c0pool", bufs=1))
         dqpool = ctx.enter_context(tc.psum_pool(name="dqpool", bufs=1))
         accpool = ctx.enter_context(tc.psum_pool(name="accpool", bufs=4))
 
         ticks = const.tile([P, REST], F32)
         negc = const.tile([P, TILES], F32)
+        neg_2c = const.tile([P, TILES], F32)
         neg_h = const.tile([P, 1], F32)
+        neg_v = const.tile([P, 1], F32)
+        beta = const.tile([P, TILES], F32)
+        eta = const.tile([P, TILES], F32)
         parts = const.tile([P, TILES, W_BANKS + 3], F32)
         sums = const.tile([P, TILES], F32)
         recip = const.tile([P, TILES], F32)
@@ -98,35 +103,16 @@ def tile_flashrecomodel_t_kernel(tc, flashes_pe, flashes_time, flashes_confidenc
             nc.vector.tensor_copy(out=dst, in_=src)
             return dst
 
-        def distance_vector(i):
-            lo = first_rest(i)
-            hi = lo + VECTOR_SQUARES.get(i, 0)
-            if hi > lo:
-                nc.vector.tensor_scalar_add(
-                    out=g_tile(i)[:, lo:hi], in0=ticks[:, lo - WINDOW : hi - WINDOW], scalar1=negc[:, i : i + 1]
-                )
-
         def square_vector(i):
             lo = first_rest(i)
-            hi = lo + VECTOR_SQUARES.get(i, 0)
-            if hi > lo:
-                gt = g_tile(i)[:, lo:hi]
-                nc.vector.tensor_tensor(out=gt, in0=gt, in1=gt, op=ALU.mult)
-
-        def square_gpsimd(i):
-            lo = first_rest(i) + VECTOR_SQUARES.get(i, 0)
-            hi = lo + GPSIMD_SQUARES.get(i, 0)
-            if hi > lo:
-                gt = g_tile(i)[:, lo:hi]
-                nc.gpsimd.tensor_scalar(
-                    out=gt, in0=ticks[:, lo - WINDOW : hi - WINDOW], scalar1=token(negc[:, i : i + 1]), scalar2=1.0,
-                    op0=ALU.add, op1=ALU.mult,
-                )
-                nc.gpsimd.tensor_tensor(out=gt, in0=gt, in1=gt, op=ALU.mult)
+            nc.vector.scalar_tensor_tensor(
+                out=g_tile(i)[:, lo:TICKS], in0=ticks[:, lo - WINDOW : REST], scalar=neg_2c[:, i : i + 1],
+                in1=ticks[:, lo - WINDOW : REST], op0=ALU.add, op1=ALU.mult,
+            )
 
         def square_scalar(i):
-            lo = first_rest(i) + VECTOR_SQUARES.get(i, 0) + GPSIMD_SQUARES.get(i, 0)
-            if lo < TICKS:
+            if i not in VECTOR_TILES:
+                lo = first_rest(i)
                 nc.scalar.activation(
                     out=g_tile(i)[:, lo:TICKS], in_=ticks[:, lo - WINDOW : REST], func=ACT.Square,
                     bias=negc[:, i : i + 1], scale=1.0,
@@ -134,8 +120,10 @@ def tile_flashrecomodel_t_kernel(tc, flashes_pe, flashes_time, flashes_confidenc
 
         def exp_rest(i):
             gt = g_tile(i)[:, first_rest(i) : TICKS]
+            scale, bias = (neg_v, beta) if i in VECTOR_TILES else (neg_h, eta)
             nc.scalar.activation(
-                out=gt, in_=gt, func=ACT.Exp, scale=neg_h[:, 0:1], accum_out=parts[:, i, W_BANKS : W_BANKS + 1],
+                out=gt, in_=gt, func=ACT.Exp, scale=scale[:, 0:1], bias=bias[:, i : i + 1],
+                accum_out=parts[:, i, W_BANKS : W_BANKS + 1],
             )
 
         def square_tensor(i, u):
@@ -156,7 +144,7 @@ def tile_flashrecomodel_t_kernel(tc, flashes_pe, flashes_time, flashes_confidenc
             column = u if u < W_BANKS else W_BANKS + 1
             nc.scalar.activation(
                 out=g_tile(i)[:, u * N_TILE : (u + 1) * N_TILE], in_=dqs[(i, u)][:], func=ACT.Exp, scale=neg_h[:, 0:1],
-                accum_out=parts[:, i, column : column + 1],
+                bias=eta[:, i : i + 1], accum_out=parts[:, i, column : column + 1],
             )
 
         def exp_window(i):
@@ -177,16 +165,15 @@ def tile_flashrecomodel_t_kernel(tc, flashes_pe, flashes_time, flashes_confidenc
         def weigh(g, t0, width, helper):
             n, off = divmod(t0, CHUNK)
             if off == 0:
-                wchs[(g, n)] = wchpool.tile([P, CHUNK, PACK], BF16, name="wch", align_bytes=64)
+                tag = "wch%d" % (n % 2 if g == GROUPS - 1 else 0)
+                wchs[(g, n)] = wchpool.tile([P, CHUNK, PACK], BF16, name=tag, align_bytes=64)
             four = slice(g * PACK, (g + 1) * PACK)
             mine = width - helper
             if helper:
                 nc.gpsimd.tensor_tensor(
                     out=wchs[(g, n)][:, off + mine : off + width, :].rearrange("p (c i) j -> p c j i", i=4),
                     in0=gts[g][:, :, t0 + mine : t0 + width].rearrange("p j (c i) -> p c j i", i=4),
-                    in1=(token(recip_ps[:, four]) if g >= 2 else recip[:, four]).unsqueeze(1).unsqueeze(3).to_broadcast(
-                        [P, helper // 4, PACK, 4]
-                    ),
+                    in1=(token(recip_ps[:, four]) if g == GROUPS - 1 else recip[:, four]).unsqueeze(1).unsqueeze(3).to_broadcast([P, helper // 4, PACK, 4]),
                     op=ALU.mult,
                 )
             nc.vector.tensor_tensor(
@@ -200,9 +187,11 @@ def tile_flashrecomodel_t_kernel(tc, flashes_pe, flashes_time, flashes_confidenc
             n, off = divmod(t0, CHUNK)
             c = g % PASSES
             if off == 0:
-                pool = c0pool if c == 0 else late["c1pool"]
-                w_codes[(c, n)] = pool.tile([P, CHUNK], U32, name="w_codes%d_%d" % (c, n), align_bytes=64)
-                w_scales[(c, n)] = pool.tile([P, CHUNK], U8, name="w_scales%d_%d" % (c, n), align_bytes=64)
+                own = g == 2 and n == N_CHUNKS - 1
+                pool = c0pool if c == 0 and not own else late["c1pool"]
+                which = (g if own else c, n)
+                w_codes[(c, n)] = pool.tile([P, CHUNK], U32, name="w_codes%d_%d" % which, align_bytes=64)
+                w_scales[(c, n)] = pool.tile([P, CHUNK], U8, name="w_scales%d_%d" % which, align_bytes=64)
             nc.vector.quantize_mx(
                 out=w_codes[(c, n)][:, off : off + width].bitcast(FP8X4),
                 scales=w_scales[(c, n)][:, off : off + width],
@@ -218,70 +207,38 @@ def tile_flashrecomodel_t_kernel(tc, flashes_pe, flashes_time, flashes_confidenc
                 return dqpool.tile([P, N_TILE], F32, name="acc_dq", tag="dq%d" % (q - 4))
             return accpool.tile([P, N_TILE], F32, name="acc")
 
-        def multiply(b, t0, width, ms, all_seven):
+        def mx_pass(b, c, m, t0, acc, nw):
             n, off = divmod(t0, CHUNK)
-            todo = []
-            for m in ms:
-                m_cols = slice(m * P, (m + 1) * P)
-                pieces = []
-                for x0 in range(0, width, N_TILE):
-                    nw = min(N_TILE, width - x0)
-                    n_cols = slice(off + x0, off + x0 + nw)
-                    acc = bank(all_seven)
-                    for c in range(PASSES):
-                        nc.tensor.matmul_mx(
-                            out=acc[:, 0:nw],
-                            lhsT=pe_codes[b * PASSES + c][:, m_cols].bitcast(FP8X4),
-                            lhsT_scale=pe_scales[b * PASSES + c][:, m_cols],
-                            rhs=w_codes[(c, n)][:, n_cols].bitcast(FP8X4),
-                            rhs_scale=w_scales[(c, n)][:, n_cols],
-                            start=(c == 0),
-                            stop=(c == PASSES - 1),
-                        )
-                    pieces.append((acc, x0, nw))
-                todo.append((b, m, t0, width, pieces))
-            return todo
-
-        def pass_of(b, c, t0, width, todo):
-            n, off = divmod(t0, CHUNK)
-            for unused_b, m, unused_t, unused_w, pieces in todo:
-                m_cols = slice(m * P, (m + 1) * P)
-                for acc, x0, nw in pieces:
-                    n_cols = slice(off + x0, off + x0 + nw)
-                    nc.tensor.matmul_mx(
-                        out=acc[:, 0:nw],
-                        lhsT=pe_codes[b * PASSES + c][:, m_cols].bitcast(FP8X4),
-                        lhsT_scale=pe_scales[b * PASSES + c][:, m_cols],
-                        rhs=w_codes[(c, n)][:, n_cols].bitcast(FP8X4),
-                        rhs_scale=w_scales[(c, n)][:, n_cols],
-                        start=(c == 0),
-                        stop=(c == PASSES - 1),
-                    )
-
-        def open_block(b, t0, width):
-            todo = []
-            for m in range(CHANNELS // P):
-                todo.append((b, m, t0, width, [(bank(True), 0, width)]))
-            pass_of(b, 0, t0, width, todo)
-            return todo
-
-        def copy_out(items, engines):
-            b, m_first, t0, width, unused = items[0]
-            stage = late["stpool"].tile([P, CHUNK], F32, name="stage")
-            e = 0
-            for a, item in enumerate(items):
-                for acc, x0, nw in item[4]:
-                    dst = stage[:, a * width + x0 : a * width + x0 + nw]
-                    if engines[e % len(engines)] == "V":
-                        nc.vector.tensor_copy(out=dst, in_=acc[:, 0:nw])
-                    else:
-                        nc.scalar.copy(out=dst, in_=acc[:, 0:nw])
-                    e += 1
-            count = len(items)
-            nc.sync.dma_start(
-                out=out[b, m_first * P : (m_first + count) * P, t0 : t0 + width].rearrange("(m p) t -> p m t", p=P),
-                in_=stage[:, 0 : count * width].rearrange("p (m t) -> p m t", m=count),
+            m_cols = slice(m * P, (m + 1) * P)
+            nc.tensor.matmul_mx(
+                out=acc[:, 0:nw],
+                lhsT=pe_codes[b * PASSES + c][:, m_cols].bitcast(FP8X4),
+                lhsT_scale=pe_scales[b * PASSES + c][:, m_cols],
+                rhs=w_codes[(c, n)][:, off : off + nw].bitcast(FP8X4),
+                rhs_scale=w_scales[(c, n)][:, off : off + nw],
+                start=(c == 0),
+                stop=(c == PASSES - 1),
             )
+
+        def unit(v):
+            n = v // 2
+            todo = []
+            for m in (2 * (v % 2), 2 * (v % 2) + 1):
+                accs = []
+                for x in range(CHUNK // N_TILE):
+                    acc = bank(v == 7)
+                    for c in range(PASSES):
+                        mx_pass(0, c, m, n * CHUNK + x * N_TILE, acc, N_TILE)
+                    accs.append(acc)
+                todo.append((m, n, accs))
+            return todo
+
+        def empty(v, engine):
+            for m, n, accs in todos[v]:
+                stage = late["stpool"].tile([P, CHUNK], F32, name="stage")
+                for x, acc in enumerate(accs):
+                    engine(out=stage[:, x * N_TILE : (x + 1) * N_TILE], in_=acc[:])
+                nc.sync.dma_start(out=out[0, m * P : (m + 1) * P, n * CHUNK : (n + 1) * CHUNK], in_=stage[:])
 
         def make_tile(i):
             square_scalar(i)
@@ -293,13 +250,6 @@ def tile_flashrecomodel_t_kernel(tc, flashes_pe, flashes_time, flashes_confidenc
 
         def codes(g, n):
             quantise(g, n * CHUNK, CHUNK)
-
-        def unit(v):
-            return multiply(0, (v // 2) * CHUNK, CHUNK, (2 * (v % 2), 2 * (v % 2) + 1), False)
-
-        def empty(todo, engines):
-            copy_out(todo[0:1], engines[0:2])
-            copy_out(todo[1:2], engines[2:4])
 
         with tc.tile_pool(name="prep", bufs=1) as prep:
             tm_bf = prep.tile([P, GROUPS, PACK], BF16)
@@ -317,53 +267,145 @@ def tile_flashrecomodel_t_kernel(tc, flashes_pe, flashes_time, flashes_confidenc
             for g in range(GROUPS):
                 nc.sync.dma_start(out=pe_raw[:, g].rearrange("p j w -> p (j w)"), in_=pe_view[:, g])
 
-            seed = 128
-            tick_i = prep.tile([P, seed], I32)
-            nc.gpsimd.iota(tick_i[:], pattern=[[1, seed]], base=WINDOW, channel_multiplier=0)
             warm = prep.tile([P, 1], F32)
             nc.gpsimd.memset(warm[:], 0.0)
+            tick_i = prep.tile([P, SEED], I32)
+            nc.gpsimd.iota(tick_i[:], pattern=[[1, SEED]], base=WINDOW, channel_multiplier=0)
             tcol_i = prep.tile([P, T_BLOCKS], I32)
             nc.gpsimd.iota(tcol_i[:], pattern=[[P, T_BLOCKS]], base=0, channel_multiplier=1)
-            tick_cols = prep.tile([P, T_BLOCKS, P], BF16)
-            flash_cols = prep.tile([P, TILES, P], BF16)
             make_identity(nc, ident[:])
 
             warm_out = prep.tile([P, 1], F32)
             nc.scalar.activation(out=warm_out[:], in_=warm[:], func=ACT.Exp)
             nc.scalar.copy(out=ident_f[:], in_=ident[:])
 
-            nc.vector.tensor_copy(out=ticks[:, 0:seed], in_=tick_i[:])
-            have = seed
+            tick_cols = prep.tile([P, T_BLOCKS * PIECES + P], BF16)
+            tick_pieces = tick_cols[:, 0 : T_BLOCKS * PIECES].rearrange("p (a k) -> p a k", k=PIECES)
+            flash_cols = prep.tile([P, TILES, P], BF16)
+            nc.vector.memset(flash_cols[:].rearrange("p a k -> p (a k)").bitcast(I32), 0)
+            nc.vector.memset(tick_cols[:, T_BLOCKS * PIECES :].bitcast(I32), 0)
+
+            def cast(dst, src):
+                return lambda: nc.vector.tensor_copy(out=dst, in_=src)
+
+            def twice(src, count):
+                return src.unsqueeze(2).to_broadcast([P, count, 2])
+
+            def combine(dst, in0, in1, op):
+                return lambda: nc.vector.tensor_tensor(out=dst, in0=in0, in1=in1, op=op)
+
+            def scale(dst, src, factor):
+                return lambda: nc.vector.tensor_scalar_mul(out=dst, in0=src, scalar1=factor)
+
+            def add_product(dst, x, factor, y):
+                return lambda: nc.vector.scalar_tensor_tensor(
+                    out=dst, in0=x, scalar=factor, in1=y, op0=ALU.mult, op1=ALU.add
+                )
+
+            def in_turn(*chains):
+                for step in range(max(len(chain) for chain in chains)):
+                    for chain in chains:
+                        if step < len(chain):
+                            chain[step]()
+
+            tcol = prep.tile([P, T_BLOCKS], F32)
+
+            def doubling(have, more):
+                return lambda: nc.vector.tensor_scalar_add(
+                    out=ticks[:, have : have + more], in0=ticks[:, 0:more], scalar1=float(have)
+                )
+
+            ramp = [cast(ticks[:, 0:SEED], tick_i[:])]
+            have = SEED
             while have < REST:
                 more = min(have, REST - have)
-                nc.vector.tensor_scalar_add(out=ticks[:, have : have + more], in0=ticks[:, 0:more], scalar1=float(have))
+                ramp.append(doubling(have, more))
                 have += more
-
-            nc.vector.memset(tick_cols[:].rearrange("p a k -> p (a k)").bitcast(I32), 0)
-            nc.vector.memset(flash_cols[:].rearrange("p a k -> p (a k)").bitcast(I32), 0)
-            nc.vector.memset(parts[:].rearrange("p a k -> p (a k)"), 0.0)
-            nc.vector.tensor_scalar_add(out=parts[:, :, W_BANKS + 2], in0=parts[:, :, W_BANKS + 2], scalar1=1e-10)
+            in_turn(
+                ramp,
+                [
+                    cast(tcol[:], tcol_i[:]),
+                    lambda: nc.vector.memset(tick_pieces[:, :, 7:10], 1.0),
+                    lambda: nc.vector.memset(flash_cols[:, :, 0:3], 1.0),
+                    lambda: nc.vector.memset(parts[:].rearrange("p a k -> p (a k)"), 0.0),
+                ],
+            )
 
             sig2 = prep.tile([P, 1], F32)
             inv2 = prep.tile([P, 1], F32)
+            t_sq = prep.tile([P, T_BLOCKS], F32)
             nc.vector.tensor_scalar(
                 out=negc[:], in0=tm_bf[:].rearrange("p g j -> p (g j)"), scalar1=-float(TICKS), scalar2=0.0,
                 op0=ALU.mult, op1=ALU.min,
             )
             nc.vector.tensor_tensor(out=sig2[:], in0=sig_bf[:], in1=sig_bf[:], op=ALU.mult)
+            nc.vector.tensor_tensor(out=t_sq[:], in0=tcol[:], in1=tcol[:], op=ALU.mult)
             nc.vector.tensor_scalar_max(out=negc[:], in0=negc[:], scalar1=-float(TICKS - 1))
-            nc.vector.reciprocal(out=inv2[:], in_=sig2[:])
-            tcol = prep.tile([P, T_BLOCKS], F32)
-            nc.vector.tensor_copy(out=tcol[:], in_=tcol_i[:])
-            nc.vector.tensor_scalar_mul(out=neg_h[:], in0=inv2[:], scalar1=-0.5)
-            cf_f = prep.tile([P, TILES], F32)
-            nc.vector.tensor_copy(out=cf_f[:], in_=cf_bf[:].rearrange("p g j -> p (g j)"))
-            nc.tensor.matmul(out=cf_ps, lhsT=ident_f[:], rhs=cf_f[:], start=True, stop=True)
+
+            t_rem1 = prep.tile([P, T_BLOCKS], F32)
+            t_rem2 = prep.tile([P, T_BLOCKS], F32)
+            t_lo = prep.tile([P, T_BLOCKS], F32)
+            a_lo = prep.tile([P, TILES], F32)
+            c_sq = prep.tile([P, TILES], F32)
+            c_rem1 = prep.tile([P, TILES], F32)
+            c_rem2 = prep.tile([P, TILES], F32)
+            h_v = prep.tile([P, 1], F32)
+            h_hi = prep.tile([P, 1], BF16)
+            h_lo = prep.tile([P, 1], F32)
+            rest1 = prep.tile([P, TILES], F32)
+            rest2 = prep.tile([P, TILES], F32)
+            rest3 = prep.tile([P, TILES], F32)
+            exp_eta = prep.tile([P, TILES], F32)
+            in_turn(
+                [
+                    lambda: nc.vector.reciprocal(out=inv2[:], in_=sig2[:]),
+                    lambda: nc.vector.tensor_scalar(
+                        out=h_v[:], in0=inv2[:], scalar1=0.5, scalar2=STEEPEST, op0=ALU.mult, op1=ALU.min
+                    ),
+                    scale(neg_v[:], h_v[:], -1.0),
+                    cast(h_hi[:], h_v[:]),
+                    scale(beta[:], c_sq[:], neg_v[:, 0:1]),
+                    combine(h_lo[:], h_v[:], h_hi[:], ALU.subtract),
+                    add_product(rest1[:], flash_cols[:, :, 7], h_hi[:, 0:1], beta[:]),
+                    scale(neg_h[:], inv2[:], -0.5),
+                    add_product(rest2[:], c_rem1[:], h_hi[:, 0:1], rest1[:]),
+                    add_product(rest3[:], flash_cols[:, :, 7], h_lo[:, 0:1], rest2[:]),
+                    add_product(eta[:], c_rem1[:], h_lo[:, 0:1], rest3[:]),
+                ],
+                [
+                    combine(c_sq[:], negc[:], negc[:], ALU.mult),
+                    cast(flash_cols[:, :, 7], c_sq[:]),
+                    combine(c_rem1[:], c_sq[:], flash_cols[:, :, 7], ALU.subtract),
+                    cast(flash_cols[:, :, 8], c_rem1[:]),
+                    combine(c_rem2[:], c_rem1[:], flash_cols[:, :, 8], ALU.subtract),
+                    cast(flash_cols[:, :, 9], c_rem2[:]),
+                ],
+                [
+                    scale(neg_2c[:], negc[:], 2.0),
+                    cast(flash_cols[:, :, 3:5], twice(neg_2c[:], TILES)),
+                    combine(a_lo[:], neg_2c[:], flash_cols[:, :, 3], ALU.subtract),
+                    cast(flash_cols[:, :, 5:7], twice(a_lo[:], TILES)),
+                ],
+                [
+                    cast(tick_pieces[:, :, 0], t_sq[:]),
+                    combine(t_rem1[:], t_sq[:], tick_pieces[:, :, 0], ALU.subtract),
+                    cast(tick_pieces[:, :, 1], t_rem1[:]),
+                    combine(t_rem2[:], t_rem1[:], tick_pieces[:, :, 1], ALU.subtract),
+                    cast(tick_pieces[:, :, 2], t_rem2[:]),
+                ],
+                [
+                    cast(tick_pieces[:, :, 3:6:2], twice(tcol[:], T_BLOCKS)),
+                    combine(t_lo[:], tcol[:], tick_pieces[:, :, 3], ALU.subtract),
+                    cast(tick_pieces[:, :, 4:7:2], twice(t_lo[:], T_BLOCKS)),
+                ],
+            )
 
             square_scalar(0)
             exp_rest(0)
+            nc.scalar.activation(out=exp_eta[:], in_=eta[:], func=ACT.Exp)
 
             spes = {}
+            cf_f = prep.tile([P, TILES], F32)
 
             def scale_pe(g):
                 spes[g] = prep.tile([P, CHANNELS, PACK], BF16, name="spe%d" % g, align_bytes=64)
@@ -380,69 +422,17 @@ def tile_flashrecomodel_t_kernel(tc, flashes_pe, flashes_time, flashes_confidenc
                     in_=spes[g][:].rearrange("p w j -> p (w j)"),
                 )
 
-            t_sq = prep.tile([P, T_BLOCKS], F32)
-            t_rem1 = prep.tile([P, T_BLOCKS], F32)
-            t_rem2 = prep.tile([P, T_BLOCKS], F32)
-            t_lo = prep.tile([P, T_BLOCKS], F32)
-            a_full = prep.tile([P, TILES], F32)
-            a_lo = prep.tile([P, TILES], F32)
-            c_sq = prep.tile([P, TILES], F32)
-            c_rem1 = prep.tile([P, TILES], F32)
-            c_rem2 = prep.tile([P, TILES], F32)
-
-            def cast(dst, src):
-                return lambda: nc.vector.tensor_copy(out=dst, in_=src)
-
-            def twice(src, count):
-                return src.unsqueeze(2).to_broadcast([P, count, 2])
-
-            def combine(dst, in0, in1, op):
-                return lambda: nc.vector.tensor_tensor(out=dst, in0=in0, in1=in1, op=op)
-
-            chains = [
-                [
-                    combine(t_sq[:], tcol[:], tcol[:], ALU.mult),
-                    cast(tick_cols[:, :, 0], t_sq[:]),
-                    combine(t_rem1[:], t_sq[:], tick_cols[:, :, 0], ALU.subtract),
-                    cast(tick_cols[:, :, 1], t_rem1[:]),
-                    combine(t_rem2[:], t_rem1[:], tick_cols[:, :, 1], ALU.subtract),
-                    cast(tick_cols[:, :, 2], t_rem2[:]),
-                ],
-                [
-                    combine(c_sq[:], negc[:], negc[:], ALU.mult),
-                    cast(flash_cols[:, :, 7], c_sq[:]),
-                    combine(c_rem1[:], c_sq[:], flash_cols[:, :, 7], ALU.subtract),
-                    cast(flash_cols[:, :, 8], c_rem1[:]),
-                    combine(c_rem2[:], c_rem1[:], flash_cols[:, :, 8], ALU.subtract),
-                    cast(flash_cols[:, :, 9], c_rem2[:]),
-                ],
-                [
-                    cast(tick_cols[:, :, 3:6:2], twice(tcol[:], T_BLOCKS)),
-                    combine(t_lo[:], tcol[:], tick_cols[:, :, 3], ALU.subtract),
-                    cast(tick_cols[:, :, 4:7:2], twice(t_lo[:], T_BLOCKS)),
-                    lambda: nc.vector.memset(tick_cols[:, :, 7:10], 1.0),
-                ],
-                [
-                    lambda: nc.vector.tensor_scalar_mul(out=a_full[:], in0=negc[:], scalar1=2.0),
-                    cast(flash_cols[:, :, 3:5], twice(a_full[:], TILES)),
-                    combine(a_lo[:], a_full[:], flash_cols[:, :, 3], ALU.subtract),
-                    cast(flash_cols[:, :, 5:7], twice(a_lo[:], TILES)),
-                    lambda: nc.vector.memset(flash_cols[:, :, 0:3], 1.0),
-                ],
-            ]
-            for step in range(6):
-                for chain in chains:
-                    if step < len(chain):
-                        chain[step]()
-
             tabs = []
             for a in range(4):
                 tabs.append(accpool.tile([P, 8 * P], BF16, name="tab%d" % a, tag="acc"))
             for a in range(T_BLOCKS):
-                nc.tensor.transpose(tabs[a // 8][:, (a % 8) * P : (a % 8 + 1) * P], tick_cols[:, a, :], ident[:])
+                nc.tensor.transpose(
+                    tabs[a // 8][:, (a % 8) * P : (a % 8 + 1) * P], tick_cols[:, a * PIECES : a * PIECES + P], ident[:]
+                )
             for a in range(8):
                 nc.tensor.transpose(tabs[2][:, a * P : (a + 1) * P], flash_cols[:, a, :], ident[:])
-            distance_vector(1)
+            nc.vector.tensor_copy(out=cf_f[:], in_=cf_bf[:].rearrange("p g j -> p (g j)"))
+            nc.tensor.matmul(out=cf_ps, lhsT=ident_f[:], rhs=cf_f[:], start=True, stop=True)
             nc.vector.tensor_copy(out=tick_rows[:, 0 : 8 * P], in_=tabs[0][:])
             square_vector(1)
             exp_rest(1)
@@ -453,18 +443,13 @@ def tile_flashrecomodel_t_kernel(tc, flashes_pe, flashes_time, flashes_confidenc
             for a in range(8):
                 nc.tensor.transpose(tabs[3][:, a * P : (a + 1) * P], flash_cols[:, 8 + a, :], ident[:])
             square_tensor(1, W_BANKS)
-            distance_vector(2)
-            distance_vector(3)
             square_vector(2)
             square_vector(3)
+            nc.vector.tensor_scalar_mul(out=parts[:, :, W_BANKS + 2], in0=exp_eta[:], scalar1=1e-10)
+            nc.vector.tensor_copy(out=flash_rows[1][:], in_=tabs[3][:])
             exp_window(0)
             exp_bank(1, W_BANKS)
             square_tensor(2, W_BANKS)
-            nc.vector.tensor_copy(out=flash_rows[1][:], in_=tabs[3][:])
-            square_gpsimd(4)
-            scale_pe(0)
-            scale_pe(1)
-            quantise_pe(0)
             exp_window(1)
             exp_bank(2, W_BANKS)
             square_tensor(3, W_BANKS)
@@ -473,91 +458,84 @@ def tile_flashrecomodel_t_kernel(tc, flashes_pe, flashes_time, flashes_confidenc
             exp_window(3)
             exp_bank(3, W_BANKS)
             exp_rest(3)
-            distance_vector(4)
-            quantise_pe(1)
-            square_vector(4)
-            distance_vector(5)
-            sum_group(0)
-            square_vector(5)
-            invert_group(0)
-            make_tile(4)
-            chunk(0, 0, 320)
-            chunk(0, 1, 320)
-            codes(0, 0)
-            make_tile(5)
-            distance_vector(6)
-            chunk(0, 2, 320)
+            scale_pe(0)
+            scale_pe(1)
+            quantise_pe(0)
             square_vector(6)
-            codes(0, 1)
-            distance_vector(7)
-            chunk(0, 3, 320)
-            square_vector(7)
-            make_tile(6)
-            square_gpsimd(8)
+            quantise_pe(1)
+            sum_group(0)
+            invert_group(0)
+            chunk(0, 0, 512)
             scale_pe(2)
-            scale_pe(3)
-            codes(0, 2)
+            make_tile(4)
+            codes(0, 0)
             quantise_pe(2)
-            make_tile(7)
-            distance_vector(8)
+            chunk(0, 1, 512)
+            scale_pe(3)
+            make_tile(5)
+            codes(0, 1)
             quantise_pe(3)
-            distance_vector(9)
-            square_vector(8)
-            distance_vector(10)
+            chunk(0, 2, 320)
+            make_tile(6)
+            codes(0, 2)
+            chunk(0, 3, 320)
+            make_tile(7)
+            codes(0, 3)
             square_vector(9)
-            distance_vector(11)
-            square_vector(10)
 
-        with tc.tile_pool(name="c1pool", bufs=1) as c1pool, tc.tile_pool(name="stpool", bufs=4) as stpool:
+        with tc.tile_pool(name="c1pool", bufs=1) as c1pool, tc.tile_pool(name="stpool", bufs=3) as stpool:
             late["c1pool"] = c1pool
             late["stpool"] = stpool
             sum_group(1)
             invert_group(1)
-            codes(0, 3)
-            square_vector(11)
-            make_tile(8)
             chunk(1, 0, 320)
-            chunk(1, 1, 320)
+            make_tile(8)
             codes(1, 0)
             todos[0] = unit(0)
+            chunk(1, 1, 512)
+            empty(0, nc.vector.tensor_copy)
             make_tile(9)
-            chunk(1, 2, 320)
             codes(1, 1)
-            chunk(1, 3, 320)
+            todos[1] = unit(1)
+            chunk(1, 2, 512)
+            empty(1, nc.vector.tensor_copy)
             make_tile(10)
             codes(1, 2)
-            square_gpsimd(12)
-            empty(todos[0], "VVVV")
-            todos[1] = unit(1)
-            empty(todos[1], "VVVV")
             todos[2] = unit(2)
-            empty(todos[2], "VVVV")
+            chunk(1, 3, 512)
+            empty(2, nc.vector.tensor_copy)
             make_tile(11)
+            codes(1, 3)
             todos[3] = unit(3)
-            empty(todos[3], "VVVV")
+            square_vector(13)
+            square_vector(14)
             sum_group(2)
             invert_group(2)
-            codes(1, 3)
-            todos[4] = unit(4)
+            chunk(2, 0, 512)
+            empty(3, nc.vector.tensor_copy)
             make_tile(12)
-            chunk(2, 0, 448)
-            empty(todos[4], "VVVV")
-            todos[5] = unit(5)
-            make_tile(13)
             codes(2, 0)
-            chunk(2, 1, 448)
-            empty(todos[5], "VVVV")
-            todos[6] = unit(6)
-            make_tile(14)
+            todos[4] = unit(4)
+            chunk(2, 1, 512)
+            empty(4, nc.vector.tensor_copy)
+            make_tile(13)
             codes(2, 1)
-            chunk(2, 2, 448)
-            empty(todos[6], "VVVV")
-            todos[7] = unit(7)
-            make_tile(15)
+            todos[5] = unit(5)
+            chunk(2, 2, 512)
+            empty(5, nc.vector.tensor_copy)
+            make_tile(14)
             codes(2, 2)
+            todos[6] = unit(6)
             chunk(2, 3, 320)
-            empty(todos[7], "AAAA")
+            make_tile(15)
+            banks[0] = 4
+            todos[7] = unit(7)
+            banks[0] = 0
+            empty(6, nc.scalar.copy)
+            empty(7, nc.scalar.copy)
             codes(2, 3)
+            sum_group(3)
+            invert_group(3)
 
             g_last = GROUPS - 1
             blocks = []
@@ -566,51 +544,44 @@ def tile_flashrecomodel_t_kernel(tc, flashes_pe, flashes_time, flashes_confidenc
                 blocks.append((begin, width))
                 begin += width
             lasts = {}
+            result = gpool.tile([P, CHANNELS // P, TICKS], F32, name="gg")
+
+            def weigh_last(x):
+                if x < len(blocks):
+                    t0, width = blocks[x]
+                    weigh(g_last, t0, width, width * 5 // 16)
+
+            def pass_last(x, c):
+                t0, width = blocks[x]
+                for m in range(CHANNELS // P):
+                    mx_pass(1, c, m, t0, lasts[x][m], width)
+
+            def open_last(x):
+                if x < len(blocks):
+                    lasts[x] = [bank(True) for m in range(CHANNELS // P)]
+                    pass_last(x, 0)
 
             def empty_last(x):
-                together = CHUNK // blocks[x][1]
-                for a in range(0, len(lasts[x]), together):
-                    copy_out(lasts[x][a : a + together], LAST_ENGINES[x][a:] + LAST_ENGINES[x][:a])
+                t0, width = blocks[x]
+                for m in range(CHANNELS // P):
+                    engine = nc.vector.tensor_copy if LAST_ENGINES[x][m] == "V" else nc.scalar.copy
+                    engine(out=result[:, m, t0 : t0 + width], in_=lasts[x][m][:, 0:width])
+                    if m % 2:
+                        nc.sync.dma_start(
+                            out=out[1, (m - 1) * P : (m + 1) * P, t0 : t0 + width].rearrange("(m p) t -> p m t", p=P),
+                            in_=result[:, m - 1 : m + 1, t0 : t0 + width],
+                        )
 
-            sum_group(3)
-            invert_group(3)
-            lasts[0] = open_block(1, blocks[0][0], blocks[0][1])
-            weigh(g_last, blocks[0][0], blocks[0][1], LAST_HELP[0])
+            open_last(0)
+            weigh_last(0)
             quantise(g_last, blocks[0][0], blocks[0][1])
-            pass_of(1, 1, blocks[0][0], blocks[0][1], lasts[0])
-            lasts[1] = open_block(1, blocks[1][0], blocks[1][1])
-            weigh(g_last, blocks[1][0], blocks[1][1], LAST_HELP[1])
-            weigh(g_last, blocks[2][0], blocks[2][1], LAST_HELP[2])
-            quantise(g_last, blocks[1][0], blocks[1][1])
-            pass_of(1, 1, blocks[1][0], blocks[1][1], lasts[1])
-            lasts[2] = open_block(1, blocks[2][0], blocks[2][1])
-            empty_last(0)
-            weigh(g_last, blocks[3][0], blocks[3][1], LAST_HELP[3])
-            quantise(g_last, blocks[2][0], blocks[2][1])
-            pass_of(1, 1, blocks[2][0], blocks[2][1], lasts[2])
-            lasts[3] = open_block(1, blocks[3][0], blocks[3][1])
-            empty_last(1)
-            weigh(g_last, blocks[4][0], blocks[4][1], LAST_HELP[4])
-            quantise(g_last, blocks[3][0], blocks[3][1])
-            pass_of(1, 1, blocks[3][0], blocks[3][1], lasts[3])
-            lasts[4] = open_block(1, blocks[4][0], blocks[4][1])
-            empty_last(2)
-            weigh(g_last, blocks[5][0], blocks[5][1], LAST_HELP[5])
-            quantise(g_last, blocks[4][0], blocks[4][1])
-            pass_of(1, 1, blocks[4][0], blocks[4][1], lasts[4])
-            lasts[5] = open_block(1, blocks[5][0], blocks[5][1])
-            empty_last(3)
-            weigh(g_last, blocks[6][0], blocks[6][1], LAST_HELP[6])
-            quantise(g_last, blocks[5][0], blocks[5][1])
-            pass_of(1, 1, blocks[5][0], blocks[5][1], lasts[5])
-            lasts[6] = open_block(1, blocks[6][0], blocks[6][1])
-            empty_last(4)
-            weigh(g_last, blocks[7][0], blocks[7][1], LAST_HELP[7])
-            quantise(g_last, blocks[6][0], blocks[6][1])
-            pass_of(1, 1, blocks[6][0], blocks[6][1], lasts[6])
-            lasts[7] = open_block(1, blocks[7][0], blocks[7][1])
-            empty_last(5)
-            quantise(g_last, blocks[7][0], blocks[7][1])
-            pass_of(1, 1, blocks[7][0], blocks[7][1], lasts[7])
-            empty_last(6)
-            empty_last(7)
+            pass_last(0, 1)
+            open_last(1)
+            weigh_last(1)
+            for x in range(1, len(blocks)):
+                weigh_last(x + 1)
+                quantise(g_last, blocks[x][0], blocks[x][1])
+                pass_last(x, 1)
+                open_last(x + 1)
+                empty_last(x - 1)
+            empty_last(len(blocks) - 1)

@@ -34,7 +34,7 @@ PIECES = 10
 REST = TICKS - WINDOW
 SEED = 512
 WIDER = (1, 2, 3)
-VECTOR_TILES = (1, 2, 3, 6, 9, 13, 14)
+VECTOR_TILES = (1, 2, 3, 6, 7, 13, 14)
 STEEPEST = 64.0
 LAST_WIDTHS = (512,) * 8
 LAST_ENGINES = ("AAAA",) * 5 + ("AAAV", "AVAV", "AVAV")
@@ -433,9 +433,9 @@ def tile_flashrecomodel_t_kernel(tc, flashes_pe, flashes_time, flashes_confidenc
                 nc.tensor.transpose(tabs[2][:, a * P : (a + 1) * P], flash_cols[:, a, :], ident[:])
             nc.vector.tensor_copy(out=cf_f[:], in_=cf_bf[:].rearrange("p g j -> p (g j)"))
             nc.tensor.matmul(out=cf_ps, lhsT=ident_f[:], rhs=cf_f[:], start=True, stop=True)
-            nc.vector.tensor_copy(out=tick_rows[:, 0 : 8 * P], in_=tabs[0][:])
             square_vector(1)
             exp_rest(1)
+            nc.vector.tensor_copy(out=tick_rows[:, 0 : 8 * P], in_=tabs[0][:])
             nc.vector.tensor_copy(out=tick_rows[:, 8 * P : TABLE], in_=tabs[1][:])
             nc.vector.tensor_copy(out=flash_rows[0][:], in_=tabs[2][:])
             for u in range(W_BANKS):
@@ -463,46 +463,46 @@ def tile_flashrecomodel_t_kernel(tc, flashes_pe, flashes_time, flashes_confidenc
             quantise_pe(0)
             square_vector(6)
             quantise_pe(1)
+            square_vector(7)
             sum_group(0)
             invert_group(0)
-            chunk(0, 0, 512)
+            chunk(0, 0, 480)
             scale_pe(2)
             make_tile(4)
             codes(0, 0)
             quantise_pe(2)
-            chunk(0, 1, 512)
+            chunk(0, 1, 480)
             scale_pe(3)
             make_tile(5)
             codes(0, 1)
             quantise_pe(3)
-            chunk(0, 2, 320)
+            chunk(0, 2, 304)
             make_tile(6)
             codes(0, 2)
-            chunk(0, 3, 320)
+            chunk(0, 3, 304)
             make_tile(7)
             codes(0, 3)
-            square_vector(9)
 
         with tc.tile_pool(name="c1pool", bufs=1) as c1pool, tc.tile_pool(name="stpool", bufs=3) as stpool:
             late["c1pool"] = c1pool
             late["stpool"] = stpool
             sum_group(1)
             invert_group(1)
-            chunk(1, 0, 320)
+            chunk(1, 0, 304)
             make_tile(8)
             codes(1, 0)
             todos[0] = unit(0)
-            chunk(1, 1, 512)
+            chunk(1, 1, 480)
             empty(0, nc.vector.tensor_copy)
             make_tile(9)
             codes(1, 1)
             todos[1] = unit(1)
-            chunk(1, 2, 512)
+            chunk(1, 2, 480)
             empty(1, nc.vector.tensor_copy)
             make_tile(10)
             codes(1, 2)
             todos[2] = unit(2)
-            chunk(1, 3, 512)
+            chunk(1, 3, 480)
             empty(2, nc.vector.tensor_copy)
             make_tile(11)
             codes(1, 3)
@@ -511,22 +511,22 @@ def tile_flashrecomodel_t_kernel(tc, flashes_pe, flashes_time, flashes_confidenc
             square_vector(14)
             sum_group(2)
             invert_group(2)
-            chunk(2, 0, 512)
+            chunk(2, 0, 480)
             empty(3, nc.vector.tensor_copy)
             make_tile(12)
             codes(2, 0)
             todos[4] = unit(4)
-            chunk(2, 1, 512)
+            chunk(2, 1, 480)
             empty(4, nc.vector.tensor_copy)
             make_tile(13)
             codes(2, 1)
             todos[5] = unit(5)
-            chunk(2, 2, 512)
+            chunk(2, 2, 480)
             empty(5, nc.vector.tensor_copy)
             make_tile(14)
             codes(2, 2)
             todos[6] = unit(6)
-            chunk(2, 3, 320)
+            chunk(2, 3, 304)
             make_tile(15)
             banks[0] = 4
             todos[7] = unit(7)

@@ -177,9 +177,9 @@ def tile_flashrecomodel_t_kernel(tc, flashes_pe, flashes_time, flashes_confidenc
                     op=ALU.mult,
                 )
             nc.vector.tensor_tensor(
-                out=wchs[(g, n)][:, off : off + mine, :].rearrange("p (c i) j -> p c j i", i=4),
-                in0=gts[g][:, :, t0 : t0 + mine].rearrange("p j (c i) -> p c j i", i=4),
-                in1=recip_ps[:, four].unsqueeze(1).unsqueeze(3).to_broadcast([P, mine // 4, PACK, 4]),
+                out=wchs[(g, n)][:, off : off + mine, :].rearrange("p (c i) j -> p c j i", i=2),
+                in0=gts[g][:, :, t0 : t0 + mine].rearrange("p j (c i) -> p c j i", i=2),
+                in1=recip_ps[:, four].unsqueeze(1).unsqueeze(3).to_broadcast([P, mine // 2, PACK, 2]),
                 op=ALU.mult,
             )
 

@@ -410,9 +410,11 @@ def tile_flashrecomodel_t_kernel(tc, flashes_pe, flashes_time, flashes_confidenc
             def scale_pe(g):
                 spes[g] = prep.tile([P, CHANNELS, PACK], BF16, name="spe%d" % g, align_bytes=64)
                 nc.vector.tensor_tensor(
-                    out=spes[g][:],
-                    in0=pe_raw[:, g].rearrange("p j w -> p w j"),
-                    in1=cf_ps[:, g * PACK : (g + 1) * PACK].unsqueeze(1).to_broadcast([P, CHANNELS, PACK]),
+                    out=spes[g][:].rearrange("p (c i) j -> p c j i", i=4),
+                    in0=pe_raw[:, g].rearrange("p j (c i) -> p c j i", i=4),
+                    in1=cf_ps[:, g * PACK : (g + 1) * PACK].unsqueeze(1).unsqueeze(3).to_broadcast(
+                        [P, CHANNELS // 4, PACK, 4]
+                    ),
                     op=ALU.mult,
                 )
 

@@ -171,9 +171,9 @@ def tile_flashrecomodel_t_kernel(tc, flashes_pe, flashes_time, flashes_confidenc
             mine = width - helper
             if helper:
                 nc.gpsimd.tensor_tensor(
-                    out=wchs[(g, n)][:, off + mine : off + width, :].rearrange("p (c i) j -> p c j i", i=4),
-                    in0=gts[g][:, :, t0 + mine : t0 + width].rearrange("p j (c i) -> p c j i", i=4),
-                    in1=(token(recip_ps[:, four]) if g == GROUPS - 1 else recip[:, four]).unsqueeze(1).unsqueeze(3).to_broadcast([P, helper // 4, PACK, 4]),
+                    out=wchs[(g, n)][:, off + mine : off + width, :].rearrange("p (c i) j -> p c j i", i=2),
+                    in0=gts[g][:, :, t0 + mine : t0 + width].rearrange("p j (c i) -> p c j i", i=2),
+                    in1=(token(recip_ps[:, four]) if g == GROUPS - 1 else recip[:, four]).unsqueeze(1).unsqueeze(3).to_broadcast([P, helper // 2, PACK, 2]),
                     op=ALU.mult,
                 )
             nc.vector.tensor_tensor(

@@ -1,5 +1,6 @@
 from contextlib import ExitStack
 
+import concourse.bass as bass
 import concourse.mybir as mybir
 from concourse.masks import make_identity
 
@@ -34,8 +35,17 @@ PIECES = 10
 REST = TICKS - WINDOW
 SEED = 512
 WIDER = (1, 2, 3)
-VECTOR_TILES = (1, 2, 3, 6, 7, 13, 14)
+VECTOR_TILES = (1, 2, 3)
+PHASES = P
+FRACTION_TICKS = PHASES
+FIRST = WINDOW - FRACTION_TICKS
+RAMP = TICKS - FIRST
+COPIES = 8
+LINE = 6656
+LINE_COLS = LINE // P
+TABLE_ROWS = (PHASES * RAMP + COPIES * LINE) // TICKS
 STEEPEST = 64.0
+CHUNK_ORDER = (2, 3, 1, 0)
 LAST_WIDTHS = (512,) * 8
 LAST_ENGINES = ("AAAA",) * 5 + ("AAAV", "AVAV", "AVAV")
 
@@ -48,13 +58,16 @@ def tile_flashrecomodel_t_kernel(tc, flashes_pe, flashes_time, flashes_confidenc
     with ExitStack() as ctx:
         ctx.enter_context(tc.manual_schedule())
         const = ctx.enter_context(tc.tile_pool(name="const", bufs=1))
-        gpool = ctx.enter_context(tc.tile_pool(name="gpool", bufs=2))
+        nearpool = ctx.enter_context(tc.tile_pool(name="nearpool", bufs=2))
+        farpool = ctx.enter_context(tc.tile_pool(name="farpool", bufs=2))
         wchpool = ctx.enter_context(tc.tile_pool(name="wchpool", bufs=1))
         c0pool = ctx.enter_context(tc.tile_pool(name="c0pool", bufs=1))
         dqpool = ctx.enter_context(tc.psum_pool(name="dqpool", bufs=1))
         accpool = ctx.enter_context(tc.psum_pool(name="accpool", bufs=4))
 
-        ticks = const.tile([P, REST], F32)
+        ramp = const.tile([P, RAMP], F32)
+        ticks = ramp[:, FRACTION_TICKS:RAMP]
+        starts = const.tile([P, TILES], I32)
         negc = const.tile([P, TILES], F32)
         neg_2c = const.tile([P, TILES], F32)
         neg_h = const.tile([P, 1], F32)
@@ -79,7 +92,8 @@ def tile_flashrecomodel_t_kernel(tc, flashes_pe, flashes_time, flashes_confidenc
             pe_codes.append(const.tile([P, CHANNELS], U32, name="pe_codes%d" % g, align_bytes=64))
             pe_scales.append(const.tile([P, CHANNELS], U8, name="pe_scales%d" % g, align_bytes=64))
 
-        gts = {}
+        near = {}
+        far = {}
         dqs = {}
         wchs = {}
         w_codes = {}
@@ -87,14 +101,19 @@ def tile_flashrecomodel_t_kernel(tc, flashes_pe, flashes_time, flashes_confidenc
         late = {}
         todos = {}
 
-        def g_tile(i):
-            g, j = divmod(i, PACK)
-            if g not in gts:
-                gts[g] = gpool.tile([P, PACK, TICKS], F32, name="gg")
-            return gts[g][:, j, :]
+        def near_group(g):
+            if g not in near:
+                near[g] = nearpool.tile([P, PACK, WINDOW], F32, name="near")
+            return near[g]
 
-        def first_rest(i):
-            return TABLE if i in WIDER else WINDOW
+        def far_group(g):
+            if g not in far:
+                far[g] = farpool.tile([P, PACK, REST], F32, name="far")
+            return far[g]
+
+        def rest_of(i):
+            lo = N_TILE if i in WIDER else 0
+            return lo, far_group(i // PACK)[:, i % PACK, lo:REST]
 
         def token(src):
             width = src.shape[1]
@@ -104,22 +123,26 @@ def tile_flashrecomodel_t_kernel(tc, flashes_pe, flashes_time, flashes_confidenc
             return dst
 
         def square_vector(i):
-            lo = first_rest(i)
+            lo, gt = rest_of(i)
             nc.vector.scalar_tensor_tensor(
-                out=g_tile(i)[:, lo:TICKS], in0=ticks[:, lo - WINDOW : REST], scalar=neg_2c[:, i : i + 1],
-                in1=ticks[:, lo - WINDOW : REST], op0=ALU.add, op1=ALU.mult,
+                out=gt, in0=ticks[:, lo:REST], scalar=neg_2c[:, i : i + 1], in1=ticks[:, lo:REST], op0=ALU.add,
+                op1=ALU.mult,
             )
 
         def square_scalar(i):
-            if i not in VECTOR_TILES:
-                lo = first_rest(i)
-                nc.scalar.activation(
-                    out=g_tile(i)[:, lo:TICKS], in_=ticks[:, lo - WINDOW : REST], func=ACT.Square,
-                    bias=negc[:, i : i + 1], scale=1.0,
-                )
+            lo, gt = rest_of(i)
+            nc.scalar.activation(out=gt, in_=ticks[:, lo:REST], func=ACT.Square, bias=negc[:, i : i + 1], scale=1.0)
+
+        table = out[0, 0:TABLE_ROWS, :]
+
+        def gather(i):
+            nc.gpsimd.indirect_dma_start(
+                out=rest_of(i)[1], out_offset=None, in_=table,
+                in_offset=bass.IndirectOffsetOnAxis(ap=starts[:, i : i + 1], axis=1),
+            )
 
         def exp_rest(i):
-            gt = g_tile(i)[:, first_rest(i) : TICKS]
+            gt = rest_of(i)[1]
             scale, bias = (neg_v, beta) if i in VECTOR_TILES else (neg_h, eta)
             nc.scalar.activation(
                 out=gt, in_=gt, func=ACT.Exp, scale=scale[:, 0:1], bias=bias[:, i : i + 1],
@@ -141,10 +164,14 @@ def tile_flashrecomodel_t_kernel(tc, flashes_pe, flashes_time, flashes_confidenc
             )
 
         def exp_bank(i, u):
-            column = u if u < W_BANKS else W_BANKS + 1
+            g, j = divmod(i, PACK)
+            if u < W_BANKS:
+                column, dst = u, near_group(g)[:, j, u * N_TILE : (u + 1) * N_TILE]
+            else:
+                column, dst = W_BANKS + 1, far_group(g)[:, j, 0:N_TILE]
             nc.scalar.activation(
-                out=g_tile(i)[:, u * N_TILE : (u + 1) * N_TILE], in_=dqs[(i, u)][:], func=ACT.Exp, scale=neg_h[:, 0:1],
-                bias=eta[:, i : i + 1], accum_out=parts[:, i, column : column + 1],
+                out=dst, in_=dqs[(i, u)][:], func=ACT.Exp, scale=neg_h[:, 0:1], bias=eta[:, i : i + 1],
+                accum_out=parts[:, i, column : column + 1],
             )
 
         def exp_window(i):
@@ -164,22 +191,24 @@ def tile_flashrecomodel_t_kernel(tc, flashes_pe, flashes_time, flashes_confidenc
 
         def weigh(g, t0, width, helper):
             n, off = divmod(t0, CHUNK)
-            if off == 0:
-                tag = "wch%d" % (n % 2 if g == GROUPS - 1 else 0)
-                wchs[(g, n)] = wchpool.tile([P, CHUNK, PACK], BF16, name=tag, align_bytes=64)
+            if (g, n) not in wchs:
+                second = g == GROUPS - 1 and n % 2
+                pool = late["c1pool"] if second else wchpool
+                wchs[(g, n)] = pool.tile([P, CHUNK, PACK], BF16, name="wch%d" % second, align_bytes=64)
             four = slice(g * PACK, (g + 1) * PACK)
             mine = width - helper
+            src, s0 = (near[g], t0) if t0 < WINDOW else (far[g], t0 - WINDOW)
             if helper:
                 nc.gpsimd.tensor_tensor(
-                    out=wchs[(g, n)][:, off + mine : off + width, :].rearrange("p (c i) j -> p c j i", i=2),
-                    in0=gts[g][:, :, t0 + mine : t0 + width].rearrange("p j (c i) -> p c j i", i=2),
-                    in1=(token(recip_ps[:, four]) if g == GROUPS - 1 else recip[:, four]).unsqueeze(1).unsqueeze(3).to_broadcast([P, helper // 2, PACK, 2]),
+                    out=wchs[(g, n)][:, off + mine : off + width, :].rearrange("p (c i) j -> p c j i", i=4),
+                    in0=src[:, :, s0 + mine : s0 + width].rearrange("p j (c i) -> p c j i", i=4),
+                    in1=(token(recip_ps[:, four]) if g == GROUPS - 1 else recip[:, four]).unsqueeze(1).unsqueeze(3).to_broadcast([P, helper // 4, PACK, 4]),
                     op=ALU.mult,
                 )
             nc.vector.tensor_tensor(
-                out=wchs[(g, n)][:, off : off + mine, :].rearrange("p (c i) j -> p c j i", i=2),
-                in0=gts[g][:, :, t0 : t0 + mine].rearrange("p j (c i) -> p c j i", i=2),
-                in1=recip_ps[:, four].unsqueeze(1).unsqueeze(3).to_broadcast([P, mine // 2, PACK, 2]),
+                out=wchs[(g, n)][:, off : off + mine, :].rearrange("p (c i) j -> p c j i", i=4),
+                in0=src[:, :, s0 : s0 + mine].rearrange("p j (c i) -> p c j i", i=4),
+                in1=recip_ps[:, four].unsqueeze(1).unsqueeze(3).to_broadcast([P, mine // 4, PACK, 4]),
                 op=ALU.mult,
             )
 
@@ -187,11 +216,9 @@ def tile_flashrecomodel_t_kernel(tc, flashes_pe, flashes_time, flashes_confidenc
             n, off = divmod(t0, CHUNK)
             c = g % PASSES
             if off == 0:
-                own = g == 2 and n == N_CHUNKS - 1
-                pool = c0pool if c == 0 and not own else late["c1pool"]
-                which = (g if own else c, n)
-                w_codes[(c, n)] = pool.tile([P, CHUNK], U32, name="w_codes%d_%d" % which, align_bytes=64)
-                w_scales[(c, n)] = pool.tile([P, CHUNK], U8, name="w_scales%d_%d" % which, align_bytes=64)
+                pool = c0pool if c == 0 else late["c1pool"]
+                w_codes[(c, n)] = pool.tile([P, CHUNK], U32, name="w_codes%d_%d" % (c, n), align_bytes=64)
+                w_scales[(c, n)] = pool.tile([P, CHUNK], U8, name="w_scales%d_%d" % (c, n), align_bytes=64)
             nc.vector.quantize_mx(
                 out=w_codes[(c, n)][:, off : off + width].bitcast(FP8X4),
                 scales=w_scales[(c, n)][:, off : off + width],
@@ -221,12 +248,12 @@ def tile_flashrecomodel_t_kernel(tc, flashes_pe, flashes_time, flashes_confidenc
             )
 
         def unit(v):
-            n = v // 2
+            n = CHUNK_ORDER[v // 2]
             todo = []
             for m in (2 * (v % 2), 2 * (v % 2) + 1):
                 accs = []
                 for x in range(CHUNK // N_TILE):
-                    acc = bank(v == 7)
+                    acc = bank(False)
                     for c in range(PASSES):
                         mx_pass(0, c, m, n * CHUNK + x * N_TILE, acc, N_TILE)
                     accs.append(acc)
@@ -238,12 +265,7 @@ def tile_flashrecomodel_t_kernel(tc, flashes_pe, flashes_time, flashes_confidenc
                 stage = late["stpool"].tile([P, CHUNK], F32, name="stage")
                 for x, acc in enumerate(accs):
                     engine(out=stage[:, x * N_TILE : (x + 1) * N_TILE], in_=acc[:])
-                nc.sync.dma_start(out=out[0, m * P : (m + 1) * P, n * CHUNK : (n + 1) * CHUNK], in_=stage[:])
-
-        def make_tile(i):
-            square_scalar(i)
-            exp_window(i)
-            exp_rest(i)
+                nc.sync.dma_start(out=out[1, m * P : (m + 1) * P, n * CHUNK : (n + 1) * CHUNK], in_=stage[:])
 
         def chunk(g, n, helper):
             weigh(g, n * CHUNK, CHUNK, helper)
@@ -251,29 +273,45 @@ def tile_flashrecomodel_t_kernel(tc, flashes_pe, flashes_time, flashes_confidenc
         def codes(g, n):
             quantise(g, n * CHUNK, CHUNK)
 
+        rawpool = ctx.enter_context(tc.tile_pool(name="rawpool", bufs=1))
+        raw_last = rawpool.tile([P, PASSES, PACK, CHANNELS], BF16)
+        spes = {}
+
         with tc.tile_pool(name="prep", bufs=1) as prep:
-            tm_bf = prep.tile([P, GROUPS, PACK], BF16)
-            nc.sync.dma_start(
-                out=tm_bf[:], in_=flashes_time.rearrange("b (c p j) o -> p (b c) (j o)", p=P, j=PACK)
-            )
+            per_event = TILES // EVENTS
+            tm_bf = prep.tile([P, EVENTS, 2 * per_event], BF16)
+            for b in range(EVENTS):
+                nc.sync.dma_start(
+                    out=tm_bf[:, b, 0:per_event].rearrange("p (c j) -> p c j", j=PACK),
+                    in_=flashes_time[EVENTS - 1 - b].rearrange("(c p j) o -> p c (j o)", p=P, j=PACK),
+                )
             sig_bf = prep.tile([P, 1], BF16)
             nc.sync.dma_start(out=sig_bf[:], in_=sigma.partition_broadcast(P))
-            cf_bf = prep.tile([P, GROUPS, PACK], BF16)
-            nc.sync.dma_start(
-                out=cf_bf[:], in_=flashes_confidence.rearrange("b (c p j) o -> p (b c) (j o)", p=P, j=PACK)
-            )
-            pe_raw = prep.tile([P, GROUPS, PACK, CHANNELS], BF16)
-            pe_view = flashes_pe.rearrange("b (c p j) w -> p (b c) (j w)", p=P, j=PACK)
+            cf_bf = prep.tile([P, EVENTS, 2 * per_event], BF16)
+            for b in range(EVENTS):
+                nc.sync.dma_start(
+                    out=cf_bf[:, b, 0:per_event].rearrange("p (c j) -> p c j", j=PACK),
+                    in_=flashes_confidence[EVENTS - 1 - b].rearrange("(c p j) o -> p c (j o)", p=P, j=PACK),
+                )
+            raw_first = prep.tile([P, PASSES, PACK, CHANNELS], BF16)
             for g in range(GROUPS):
-                nc.sync.dma_start(out=pe_raw[:, g].rearrange("p j w -> p (j w)"), in_=pe_view[:, g])
+                b, c = EVENTS - 1 - g // PASSES, g % PASSES
+                nc.sync.dma_start(
+                    out=(raw_first if g < PASSES else raw_last)[:, c].rearrange("p j w -> p (j w)"),
+                    in_=flashes_pe[b, c * K_PASS : (c + 1) * K_PASS, :].rearrange("(p j) w -> p (j w)", j=PACK),
+                )
 
             warm = prep.tile([P, 1], F32)
             nc.gpsimd.memset(warm[:], 0.0)
             tick_i = prep.tile([P, SEED], I32)
-            nc.gpsimd.iota(tick_i[:], pattern=[[1, SEED]], base=WINDOW, channel_multiplier=0)
+            nc.gpsimd.iota(tick_i[:], pattern=[[1, SEED]], base=FIRST, channel_multiplier=0)
             tcol_i = prep.tile([P, T_BLOCKS], I32)
             nc.gpsimd.iota(tcol_i[:], pattern=[[P, T_BLOCKS]], base=0, channel_multiplier=1)
             make_identity(nc, ident[:])
+            line_i = prep.tile([P, LINE_COLS], I32)
+            nc.gpsimd.iota(line_i[:], pattern=[[1, LINE_COLS]], base=WINDOW + 1 - TICKS, channel_multiplier=LINE_COLS)
+            part_i = prep.tile([P, 1], I32)
+            nc.gpsimd.iota(part_i[:], pattern=[[1, 1]], base=0, channel_multiplier=1)
 
             warm_out = prep.tile([P, 1], F32)
             nc.scalar.activation(out=warm_out[:], in_=warm[:], func=ACT.Exp)
@@ -312,17 +350,17 @@ def tile_flashrecomodel_t_kernel(tc, flashes_pe, flashes_time, flashes_confidenc
 
             def doubling(have, more):
                 return lambda: nc.vector.tensor_scalar_add(
-                    out=ticks[:, have : have + more], in0=ticks[:, 0:more], scalar1=float(have)
+                    out=ramp[:, have : have + more], in0=ramp[:, 0:more], scalar1=float(have)
                 )
 
-            ramp = [cast(ticks[:, 0:SEED], tick_i[:])]
+            growth = [cast(ramp[:, 0:SEED], tick_i[:])]
             have = SEED
-            while have < REST:
-                more = min(have, REST - have)
-                ramp.append(doubling(have, more))
+            while have < RAMP:
+                more = min(have, RAMP - have)
+                growth.append(doubling(have, more))
                 have += more
             in_turn(
-                ramp,
+                growth,
                 [
                     cast(tcol[:], tcol_i[:]),
                     lambda: nc.vector.memset(tick_pieces[:, :, 7:10], 1.0),
@@ -335,12 +373,12 @@ def tile_flashrecomodel_t_kernel(tc, flashes_pe, flashes_time, flashes_confidenc
             inv2 = prep.tile([P, 1], F32)
             t_sq = prep.tile([P, T_BLOCKS], F32)
             nc.vector.tensor_scalar(
-                out=negc[:], in0=tm_bf[:].rearrange("p g j -> p (g j)"), scalar1=-float(TICKS), scalar2=0.0,
-                op0=ALU.mult, op1=ALU.min,
+                out=negc[:].rearrange("p (b i) -> p b i", b=EVENTS), in0=tm_bf[:, :, 0:per_event],
+                scalar1=-float(TICKS), scalar2=0.0, op0=ALU.mult, op1=ALU.min,
             )
-            nc.vector.tensor_tensor(out=sig2[:], in0=sig_bf[:], in1=sig_bf[:], op=ALU.mult)
             nc.vector.tensor_tensor(out=t_sq[:], in0=tcol[:], in1=tcol[:], op=ALU.mult)
             nc.vector.tensor_scalar_max(out=negc[:], in0=negc[:], scalar1=-float(TICKS - 1))
+            nc.vector.tensor_tensor(out=sig2[:], in0=sig_bf[:], in1=sig_bf[:], op=ALU.mult)
 
             t_rem1 = prep.tile([P, T_BLOCKS], F32)
             t_rem2 = prep.tile([P, T_BLOCKS], F32)
@@ -404,14 +442,14 @@ def tile_flashrecomodel_t_kernel(tc, flashes_pe, flashes_time, flashes_confidenc
             exp_rest(0)
             nc.scalar.activation(out=exp_eta[:], in_=eta[:], func=ACT.Exp)
 
-            spes = {}
             cf_f = prep.tile([P, TILES], F32)
 
             def scale_pe(g):
-                spes[g] = prep.tile([P, CHANNELS, PACK], BF16, name="spe%d" % g, align_bytes=64)
+                spes[g] = rawpool.tile([P, CHANNELS, PACK], BF16, name="spe", align_bytes=64)
+                raw = (raw_first if g < PASSES else raw_last)[:, g % PASSES]
                 nc.vector.tensor_tensor(
                     out=spes[g][:].rearrange("p (c i) j -> p c j i", i=4),
-                    in0=pe_raw[:, g].rearrange("p j (c i) -> p c j i", i=4),
+                    in0=raw.rearrange("p j (c i) -> p c j i", i=4),
                     in1=cf_ps[:, g * PACK : (g + 1) * PACK].unsqueeze(1).unsqueeze(3).to_broadcast(
                         [P, CHANNELS // 4, PACK, 4]
                     ),
@@ -433,8 +471,75 @@ def tile_flashrecomodel_t_kernel(tc, flashes_pe, flashes_time, flashes_confidenc
                 )
             for a in range(8):
                 nc.tensor.transpose(tabs[2][:, a * P : (a + 1) * P], flash_cols[:, a, :], ident[:])
-            nc.vector.tensor_copy(out=cf_f[:], in_=cf_bf[:].rearrange("p g j -> p (g j)"))
+            nc.vector.tensor_copy(
+                out=cf_f[:].rearrange("p (b i) -> p b i", b=EVENTS), in_=cf_bf[:, :, 0:per_event]
+            )
             nc.tensor.matmul(out=cf_ps, lhsT=ident_f[:], rhs=cf_f[:], start=True, stop=True)
+            part = prep.tile([P, 1], F32)
+            minus_phase = prep.tile([P, 1], F32)
+            copy_i = prep.tile([P, 1], I32)
+            copy_start = prep.tile([P, 1], F32)
+            line = prep.tile([P, LINE_COLS], F32)
+            line_sq = prep.tile([P, LINE_COLS], F32)
+            m_f = prep.tile([P, TILES], F32)
+            m_i = prep.tile([P, TILES], I32)
+            phase_i = prep.tile([P, TILES], I32)
+            whole_i = prep.tile([P, TILES], I32)
+            phase_f = prep.tile([P, TILES], F32)
+            whole_f = prep.tile([P, TILES], F32)
+            on_phase = prep.tile([P, TILES], F32)
+            on_line = prep.tile([P, TILES], F32)
+            gap = prep.tile([P, TILES], F32)
+            starts_f = prep.tile([P, TILES], F32)
+            flat = table.rearrange("a b -> (a b)")
+
+            def fractions():
+                phases = far_group(1)[:].rearrange("p j t -> p (j t)")[:, 0:RAMP]
+                nc.vector.tensor_scalar_add(out=phases, in0=ramp[:], scalar1=minus_phase[:, 0:1])
+                nc.vector.tensor_tensor(out=line_sq[:], in0=line[:], in1=line[:], op=ALU.mult)
+                nc.vector.tensor_tensor(out=phases, in0=phases, in1=phases, op=ALU.mult)
+                nc.sync.dma_start(
+                    out=flat[PHASES * RAMP :].rearrange("(q p k) -> p q k", q=COPIES, p=P),
+                    in_=line_sq[:].unsqueeze(1).to_broadcast([P, COPIES, LINE_COLS]),
+                )
+                nc.sync.dma_start(out=flat[0 : PHASES * RAMP].rearrange("(p u) -> p u", p=P), in_=phases)
+
+            def find_starts():
+                in_turn(
+                    [
+                        scale(m_f[:], negc[:], -float(PHASES)),
+                        cast(m_i[:], m_f[:]),
+                        lambda: nc.vector.tensor_single_scalar(phase_i[:], m_i[:], PHASES - 1, op=ALU.bitwise_and),
+                        lambda: nc.vector.tensor_single_scalar(whole_i[:], m_i[:], 7, op=ALU.arith_shift_right),
+                        cast(phase_f[:], phase_i[:]),
+                        lambda: nc.vector.tensor_scalar_add(
+                            out=whole_f[:], in0=whole_i[:], scalar1=-float(FRACTION_TICKS)
+                        ),
+                        lambda: nc.vector.scalar_tensor_tensor(
+                            out=on_phase[:], in0=phase_f[:], scalar=float(RAMP), in1=whole_f[:], op0=ALU.mult,
+                            op1=ALU.subtract,
+                        ),
+                        combine(gap[:], on_line[:], on_phase[:], ALU.subtract),
+                        lambda: nc.vector.scalar_tensor_tensor(
+                            out=gap[:], in0=negc[:], scalar=-float(FRACTION_TICKS), in1=gap[:], op0=ALU.is_le,
+                            op1=ALU.mult,
+                        ),
+                        combine(starts_f[:], on_phase[:], gap[:], ALU.add),
+                        cast(starts[:], starts_f[:]),
+                    ],
+                    [
+                        cast(part[:], part_i[:]),
+                        lambda: nc.vector.tensor_single_scalar(copy_i[:], part_i[:], COPIES - 1, op=ALU.bitwise_and),
+                        scale(minus_phase[:], part[:], -1.0 / PHASES),
+                        lambda: nc.vector.tensor_scalar(
+                            out=copy_start[:], in0=copy_i[:], scalar1=float(LINE),
+                            scalar2=float(PHASES * RAMP + TICKS - 1), op0=ALU.mult, op1=ALU.add,
+                        ),
+                        cast(line[:], line_i[:]),
+                        lambda: nc.vector.tensor_scalar_add(out=on_line[:], in0=negc[:], scalar1=copy_start[:, 0:1]),
+                    ],
+                )
+
             square_vector(1)
             exp_rest(1)
             nc.vector.tensor_copy(out=tick_rows[:, 0 : 8 * P], in_=tabs[0][:])
@@ -445,7 +550,13 @@ def tile_flashrecomodel_t_kernel(tc, flashes_pe, flashes_time, flashes_confidenc
             for a in range(8):
                 nc.tensor.transpose(tabs[3][:, a * P : (a + 1) * P], flash_cols[:, 8 + a, :], ident[:])
             square_tensor(1, W_BANKS)
+            find_starts()
+            fractions()
             square_vector(2)
+            gather(4)
+            gather(5)
+            gather(6)
+            gather(7)
             square_vector(3)
             nc.vector.tensor_scalar_mul(out=parts[:, :, W_BANKS + 2], in0=exp_eta[:], scalar1=1e-10)
             nc.vector.tensor_copy(out=flash_rows[1][:], in_=tabs[3][:])
@@ -461,81 +572,98 @@ def tile_flashrecomodel_t_kernel(tc, flashes_pe, flashes_time, flashes_confidenc
             exp_bank(3, W_BANKS)
             exp_rest(3)
             scale_pe(0)
-            scale_pe(1)
             quantise_pe(0)
-            square_vector(6)
-            quantise_pe(1)
-            square_vector(7)
             sum_group(0)
             invert_group(0)
-            chunk(0, 0, 480)
-            scale_pe(2)
-            make_tile(4)
-            codes(0, 0)
-            quantise_pe(2)
-            chunk(0, 1, 480)
-            scale_pe(3)
-            make_tile(5)
-            codes(0, 1)
-            quantise_pe(3)
-            chunk(0, 2, 304)
-            make_tile(6)
+            chunk(0, 2, 480)
+            scale_pe(1)
+            exp_window(4)
+            exp_window(5)
+            exp_rest(4)
             codes(0, 2)
             chunk(0, 3, 304)
-            make_tile(7)
+            quantise_pe(1)
+            exp_window(6)
+            exp_rest(5)
             codes(0, 3)
+            weigh(0, WINDOW, 2 * CHUNK - WINDOW, 152)
+            weigh(0, CHUNK, WINDOW - CHUNK, 152)
+            exp_window(7)
+            exp_rest(6)
+            codes(0, 1)
+            gather(8)
+            chunk(0, 0, 304)
+            exp_rest(7)
+            codes(0, 0)
+            gather(9)
 
         with tc.tile_pool(name="c1pool", bufs=1) as c1pool, tc.tile_pool(name="stpool", bufs=3) as stpool:
             late["c1pool"] = c1pool
             late["stpool"] = stpool
             sum_group(1)
             invert_group(1)
-            chunk(1, 0, 304)
-            make_tile(8)
-            codes(1, 0)
-            todos[0] = unit(0)
-            chunk(1, 1, 480)
-            empty(0, nc.vector.tensor_copy)
-            make_tile(9)
-            codes(1, 1)
-            todos[1] = unit(1)
-            chunk(1, 2, 480)
-            empty(1, nc.vector.tensor_copy)
-            make_tile(10)
+            chunk(1, 2, 304)
+            exp_window(8)
+            exp_window(9)
             codes(1, 2)
-            todos[2] = unit(2)
+            gather(10)
+            todos[0] = unit(0)
             chunk(1, 3, 480)
-            empty(2, nc.vector.tensor_copy)
-            make_tile(11)
+            empty(0, nc.vector.tensor_copy)
+            exp_window(10)
+            exp_rest(8)
             codes(1, 3)
+            gather(11)
+            todos[1] = unit(1)
+            weigh(1, WINDOW, 2 * CHUNK - WINDOW, 240)
+            weigh(1, CHUNK, WINDOW - CHUNK, 240)
+            empty(1, nc.vector.tensor_copy)
+            exp_window(11)
+            exp_rest(9)
+            codes(1, 1)
+            todos[2] = unit(2)
+            gather(12)
+            chunk(1, 0, 480)
+            scale_pe(2)
+            exp_rest(10)
+            empty(2, nc.scalar.copy)
+            quantise_pe(2)
+            codes(1, 0)
             todos[3] = unit(3)
-            square_vector(13)
-            square_vector(14)
+            gather(13)
+            exp_rest(11)
             sum_group(2)
             invert_group(2)
-            chunk(2, 0, 480)
-            empty(3, nc.vector.tensor_copy)
-            make_tile(12)
-            codes(2, 0)
-            todos[4] = unit(4)
-            chunk(2, 1, 480)
-            empty(4, nc.vector.tensor_copy)
-            make_tile(13)
-            codes(2, 1)
-            todos[5] = unit(5)
-            chunk(2, 2, 480)
-            empty(5, nc.vector.tensor_copy)
-            make_tile(14)
+            chunk(2, 2, 304)
+            empty(3, nc.scalar.copy)
+            exp_window(12)
+            exp_window(13)
             codes(2, 2)
-            todos[6] = unit(6)
-            chunk(2, 3, 304)
-            make_tile(15)
-            banks[0] = 4
-            todos[7] = unit(7)
-            banks[0] = 0
-            empty(6, nc.scalar.copy)
-            empty(7, nc.scalar.copy)
+            todos[4] = unit(4)
+            gather(14)
+            chunk(2, 3, 480)
+            empty(4, nc.vector.tensor_copy)
+            exp_rest(12)
+            exp_window(14)
             codes(2, 3)
+            todos[5] = unit(5)
+            gather(15)
+            weigh(2, WINDOW, 2 * CHUNK - WINDOW, 240)
+            weigh(2, CHUNK, WINDOW - CHUNK, 240)
+            scale_pe(3)
+            exp_rest(13)
+            exp_window(15)
+            empty(5, nc.scalar.copy)
+            quantise_pe(3)
+            codes(2, 1)
+            todos[6] = unit(6)
+            chunk(2, 0, 304)
+            exp_rest(14)
+            empty(6, nc.scalar.copy)
+            exp_rest(15)
+            todos[7] = unit(7)
+            empty(7, nc.scalar.copy)
+            codes(2, 0)
             sum_group(3)
             invert_group(3)
 
@@ -546,7 +674,8 @@ def tile_flashrecomodel_t_kernel(tc, flashes_pe, flashes_time, flashes_confidenc
                 blocks.append((begin, width))
                 begin += width
             lasts = {}
-            result = gpool.tile([P, CHANNELS // P, TICKS], F32, name="gg")
+            early = nearpool.tile([P, CHANNELS // P, WINDOW], F32, name="near")
+            later = farpool.tile([P, CHANNELS // P, REST], F32, name="far")
 
             def weigh_last(x):
                 if x < len(blocks):
@@ -565,13 +694,14 @@ def tile_flashrecomodel_t_kernel(tc, flashes_pe, flashes_time, flashes_confidenc
 
             def empty_last(x):
                 t0, width = blocks[x]
+                result, s0 = (early, t0) if t0 < WINDOW else (later, t0 - WINDOW)
                 for m in range(CHANNELS // P):
                     engine = nc.vector.tensor_copy if LAST_ENGINES[x][m] == "V" else nc.scalar.copy
-                    engine(out=result[:, m, t0 : t0 + width], in_=lasts[x][m][:, 0:width])
+                    engine(out=result[:, m, s0 : s0 + width], in_=lasts[x][m][:, 0:width])
                     if m % 2:
                         nc.sync.dma_start(
-                            out=out[1, (m - 1) * P : (m + 1) * P, t0 : t0 + width].rearrange("(m p) t -> p m t", p=P),
-                            in_=result[:, m - 1 : m + 1, t0 : t0 + width],
+                            out=out[0, (m - 1) * P : (m + 1) * P, t0 : t0 + width].rearrange("(m p) t -> p m t", p=P),
+                            in_=result[:, m - 1 : m + 1, s0 : s0 + width],
                         )
 
             open_last(0)

@@ -36,14 +36,18 @@ REST = TICKS - WINDOW
 SEED = 512
 WIDER = (1, 2, 3)
 VECTOR_TILES = (1, 2, 3)
-PHASES = P
-FRACTION_TICKS = PHASES
+PHASE_BITS = 5
+PHASES = 2**PHASE_BITS
+SEGMENTS = P // PHASES
+FRACTION_TICKS = 128
 FIRST = WINDOW - FRACTION_TICKS
 RAMP = TICKS - FIRST
 COPIES = 8
+SEGMENT = RAMP // SEGMENTS
 LINE = 6656
 LINE_COLS = LINE // P
-TABLE_ROWS = (PHASES * RAMP + COPIES * LINE) // TICKS
+TABLE_SIZE = PHASES * RAMP + COPIES * LINE
+TABLE_ROWS = -(-TABLE_SIZE // TICKS)
 STEEPEST = 64.0
 CHUNK_ORDER = (2, 3, 1, 0)
 LAST_WIDTHS = (512,) * 8
@@ -477,6 +481,8 @@ def tile_flashrecomodel_t_kernel(tc, flashes_pe, flashes_time, flashes_confidenc
             nc.tensor.matmul(out=cf_ps, lhsT=ident_f[:], rhs=cf_f[:], start=True, stop=True)
             part = prep.tile([P, 1], F32)
             minus_phase = prep.tile([P, 1], F32)
+            segment_i = prep.tile([P, 1], I32)
+            segment_f = prep.tile([P, 1], F32)
             copy_i = prep.tile([P, 1], I32)
             copy_start = prep.tile([P, 1], F32)
             line = prep.tile([P, LINE_COLS], F32)
@@ -494,15 +500,17 @@ def tile_flashrecomodel_t_kernel(tc, flashes_pe, flashes_time, flashes_confidenc
             flat = table.rearrange("a b -> (a b)")
 
             def fractions():
-                phases = far_group(1)[:].rearrange("p j t -> p (j t)")[:, 0:RAMP]
-                nc.vector.tensor_scalar_add(out=phases, in0=ramp[:], scalar1=minus_phase[:, 0:1])
+                phases = far_group(1)[:, 0, 0:SEGMENT]
+                nc.vector.tensor_scalar_add(out=phases, in0=ramp[:, 0:SEGMENT], scalar1=minus_phase[:, 0:1])
                 nc.vector.tensor_tensor(out=line_sq[:], in0=line[:], in1=line[:], op=ALU.mult)
                 nc.vector.tensor_tensor(out=phases, in0=phases, in1=phases, op=ALU.mult)
                 nc.sync.dma_start(
                     out=flat[PHASES * RAMP :].rearrange("(q p k) -> p q k", q=COPIES, p=P),
                     in_=line_sq[:].unsqueeze(1).to_broadcast([P, COPIES, LINE_COLS]),
                 )
-                nc.sync.dma_start(out=flat[0 : PHASES * RAMP].rearrange("(p u) -> p u", p=P), in_=phases)
+                by_segment = flat[0 : PHASES * RAMP].rearrange("(f h k) -> h f k", h=SEGMENTS, k=SEGMENT)
+                for s in range(SEGMENTS):
+                    nc.sync.dma_start(out=by_segment[s], in_=phases[s * PHASES : (s + 1) * PHASES, :])
 
             def find_starts():
                 in_turn(
@@ -510,7 +518,7 @@ def tile_flashrecomodel_t_kernel(tc, flashes_pe, flashes_time, flashes_confidenc
                         scale(m_f[:], negc[:], -float(PHASES)),
                         cast(m_i[:], m_f[:]),
                         lambda: nc.vector.tensor_single_scalar(phase_i[:], m_i[:], PHASES - 1, op=ALU.bitwise_and),
-                        lambda: nc.vector.tensor_single_scalar(whole_i[:], m_i[:], 7, op=ALU.arith_shift_right),
+                        lambda: nc.vector.tensor_single_scalar(whole_i[:], m_i[:], PHASE_BITS, op=ALU.arith_shift_right),
                         cast(phase_f[:], phase_i[:]),
                         lambda: nc.vector.tensor_scalar_add(
                             out=whole_f[:], in0=whole_i[:], scalar1=-float(FRACTION_TICKS)
@@ -530,13 +538,22 @@ def tile_flashrecomodel_t_kernel(tc, flashes_pe, flashes_time, flashes_confidenc
                     [
                         cast(part[:], part_i[:]),
                         lambda: nc.vector.tensor_single_scalar(copy_i[:], part_i[:], COPIES - 1, op=ALU.bitwise_and),
-                        scale(minus_phase[:], part[:], -1.0 / PHASES),
+                        lambda: nc.vector.tensor_single_scalar(
+                            segment_i[:], part_i[:], PHASE_BITS, op=ALU.arith_shift_right
+                        ),
                         lambda: nc.vector.tensor_scalar(
                             out=copy_start[:], in0=copy_i[:], scalar1=float(LINE),
                             scalar2=float(PHASES * RAMP + TICKS - 1), op0=ALU.mult, op1=ALU.add,
                         ),
-                        cast(line[:], line_i[:]),
+                        lambda: nc.vector.tensor_scalar_mul(
+                            out=segment_f[:], in0=segment_i[:], scalar1=float(SEGMENT + 1)
+                        ),
                         lambda: nc.vector.tensor_scalar_add(out=on_line[:], in0=negc[:], scalar1=copy_start[:, 0:1]),
+                        cast(line[:], line_i[:]),
+                        lambda: nc.vector.scalar_tensor_tensor(
+                            out=minus_phase[:], in0=part[:], scalar=-1.0 / PHASES, in1=segment_f[:], op0=ALU.mult,
+                            op1=ALU.add,
+                        ),
                     ],
                 )
 
@@ -573,26 +590,26 @@ def tile_flashrecomodel_t_kernel(tc, flashes_pe, flashes_time, flashes_confidenc
             exp_rest(3)
             scale_pe(0)
             quantise_pe(0)
+            scale_pe(1)
             sum_group(0)
             invert_group(0)
-            chunk(0, 2, 480)
-            scale_pe(1)
+            chunk(0, 2, 256)
+            quantise_pe(1)
             exp_window(4)
             exp_window(5)
             exp_rest(4)
             codes(0, 2)
-            chunk(0, 3, 304)
-            quantise_pe(1)
+            chunk(0, 3, 256)
             exp_window(6)
             exp_rest(5)
             codes(0, 3)
-            weigh(0, WINDOW, 2 * CHUNK - WINDOW, 152)
-            weigh(0, CHUNK, WINDOW - CHUNK, 152)
+            weigh(0, WINDOW, 2 * CHUNK - WINDOW, 128)
+            weigh(0, CHUNK, WINDOW - CHUNK, 128)
             exp_window(7)
             exp_rest(6)
             codes(0, 1)
             gather(8)
-            chunk(0, 0, 304)
+            chunk(0, 0, 256)
             exp_rest(7)
             codes(0, 0)
             gather(9)
@@ -602,28 +619,28 @@ def tile_flashrecomodel_t_kernel(tc, flashes_pe, flashes_time, flashes_confidenc
             late["stpool"] = stpool
             sum_group(1)
             invert_group(1)
-            chunk(1, 2, 304)
+            chunk(1, 2, 256)
             exp_window(8)
             exp_window(9)
             codes(1, 2)
             gather(10)
             todos[0] = unit(0)
-            chunk(1, 3, 480)
+            chunk(1, 3, 432)
             empty(0, nc.vector.tensor_copy)
             exp_window(10)
             exp_rest(8)
             codes(1, 3)
             gather(11)
             todos[1] = unit(1)
-            weigh(1, WINDOW, 2 * CHUNK - WINDOW, 240)
-            weigh(1, CHUNK, WINDOW - CHUNK, 240)
+            weigh(1, WINDOW, 2 * CHUNK - WINDOW, 208)
+            weigh(1, CHUNK, WINDOW - CHUNK, 208)
             empty(1, nc.vector.tensor_copy)
             exp_window(11)
             exp_rest(9)
             codes(1, 1)
             todos[2] = unit(2)
             gather(12)
-            chunk(1, 0, 480)
+            chunk(1, 0, 432)
             scale_pe(2)
             exp_rest(10)
             empty(2, nc.scalar.copy)
@@ -634,22 +651,22 @@ def tile_flashrecomodel_t_kernel(tc, flashes_pe, flashes_time, flashes_confidenc
             exp_rest(11)
             sum_group(2)
             invert_group(2)
-            chunk(2, 2, 304)
+            chunk(2, 2, 256)
             empty(3, nc.scalar.copy)
             exp_window(12)
             exp_window(13)
             codes(2, 2)
             todos[4] = unit(4)
             gather(14)
-            chunk(2, 3, 480)
+            chunk(2, 3, 432)
             empty(4, nc.vector.tensor_copy)
             exp_rest(12)
             exp_window(14)
             codes(2, 3)
             todos[5] = unit(5)
             gather(15)
-            weigh(2, WINDOW, 2 * CHUNK - WINDOW, 240)
-            weigh(2, CHUNK, WINDOW - CHUNK, 240)
+            weigh(2, WINDOW, 2 * CHUNK - WINDOW, 208)
+            weigh(2, CHUNK, WINDOW - CHUNK, 208)
             scale_pe(3)
             exp_rest(13)
             exp_window(15)
@@ -657,7 +674,7 @@ def tile_flashrecomodel_t_kernel(tc, flashes_pe, flashes_time, flashes_confidenc
             quantise_pe(3)
             codes(2, 1)
             todos[6] = unit(6)
-            chunk(2, 0, 304)
+            chunk(2, 0, 256)
             exp_rest(14)
             empty(6, nc.scalar.copy)
             exp_rest(15)

@@ -265,11 +265,13 @@ def tile_flashrecomodel_t_kernel(tc, flashes_pe, flashes_time, flashes_confidenc
             return todo
 
         def empty(v, engine):
-            for m, n, accs in todos[v]:
-                stage = late["stpool"].tile([P, CHUNK], F32, name="stage")
+            if v % 2:
+                pair = late["c1pool"].tile([P, 2, CHUNK], F32, name="pair", tag="wch1", align_bytes=64)
+            for a, (m, n, accs) in enumerate(todos[v]):
+                stage = pair[:, a, :] if v % 2 else late["stpool"].tile([P, CHUNK], F32, name="stage")[:]
                 for x, acc in enumerate(accs):
                     engine(out=stage[:, x * N_TILE : (x + 1) * N_TILE], in_=acc[:])
-                nc.sync.dma_start(out=out[1, m * P : (m + 1) * P, n * CHUNK : (n + 1) * CHUNK], in_=stage[:])
+                nc.sync.dma_start(out=out[1, m * P : (m + 1) * P, n * CHUNK : (n + 1) * CHUNK], in_=stage)
 
         def chunk(g, n, helper):
             weigh(g, n * CHUNK, CHUNK, helper)
@@ -570,7 +572,6 @@ def tile_flashrecomodel_t_kernel(tc, flashes_pe, flashes_time, flashes_confidenc
             find_starts()
             fractions()
             square_vector(2)
-            gather(4)
             gather(5)
             gather(6)
             gather(7)
@@ -596,6 +597,7 @@ def tile_flashrecomodel_t_kernel(tc, flashes_pe, flashes_time, flashes_confidenc
             chunk(0, 2, 256)
             quantise_pe(1)
             exp_window(4)
+            square_scalar(4)
             exp_window(5)
             exp_rest(4)
             codes(0, 2)
@@ -603,16 +605,16 @@ def tile_flashrecomodel_t_kernel(tc, flashes_pe, flashes_time, flashes_confidenc
             exp_window(6)
             exp_rest(5)
             codes(0, 3)
-            weigh(0, WINDOW, 2 * CHUNK - WINDOW, 128)
-            weigh(0, CHUNK, WINDOW - CHUNK, 128)
+            weigh(0, WINDOW, 2 * CHUNK - WINDOW, 256)
+            gather(8)
+            weigh(0, CHUNK, WINDOW - CHUNK, 0)
             exp_window(7)
             exp_rest(6)
             codes(0, 1)
-            gather(8)
             chunk(0, 0, 256)
+            gather(9)
             exp_rest(7)
             codes(0, 0)
-            gather(9)
 
         with tc.tile_pool(name="c1pool", bufs=1) as c1pool, tc.tile_pool(name="stpool", bufs=3) as stpool:
             late["c1pool"] = c1pool
@@ -620,51 +622,51 @@ def tile_flashrecomodel_t_kernel(tc, flashes_pe, flashes_time, flashes_confidenc
             sum_group(1)
             invert_group(1)
             chunk(1, 2, 256)
+            gather(10)
             exp_window(8)
             exp_window(9)
             codes(1, 2)
-            gather(10)
             todos[0] = unit(0)
             chunk(1, 3, 432)
+            gather(11)
             empty(0, nc.vector.tensor_copy)
             exp_window(10)
             exp_rest(8)
             codes(1, 3)
-            gather(11)
             todos[1] = unit(1)
-            weigh(1, WINDOW, 2 * CHUNK - WINDOW, 208)
-            weigh(1, CHUNK, WINDOW - CHUNK, 208)
-            empty(1, nc.vector.tensor_copy)
+            weigh(1, WINDOW, 2 * CHUNK - WINDOW, 256)
+            gather(12)
+            weigh(1, CHUNK, WINDOW - CHUNK, 0)
             exp_window(11)
             exp_rest(9)
+            empty(1, nc.scalar.copy)
             codes(1, 1)
             todos[2] = unit(2)
-            gather(12)
             chunk(1, 0, 432)
+            gather(13)
             scale_pe(2)
             exp_rest(10)
             empty(2, nc.scalar.copy)
             quantise_pe(2)
             codes(1, 0)
             todos[3] = unit(3)
-            gather(13)
             exp_rest(11)
             sum_group(2)
             invert_group(2)
             chunk(2, 2, 256)
+            gather(14)
             empty(3, nc.scalar.copy)
             exp_window(12)
             exp_window(13)
             codes(2, 2)
             todos[4] = unit(4)
-            gather(14)
             chunk(2, 3, 432)
+            gather(15)
             empty(4, nc.vector.tensor_copy)
             exp_rest(12)
             exp_window(14)
             codes(2, 3)
             todos[5] = unit(5)
-            gather(15)
             weigh(2, WINDOW, 2 * CHUNK - WINDOW, 208)
             weigh(2, CHUNK, WINDOW - CHUNK, 208)
             scale_pe(3)

@@ -49,8 +49,8 @@ LINE_COLS = LINE // P
 TABLE_SIZE = PHASES * RAMP + COPIES * LINE
 TABLE_ROWS = -(-TABLE_SIZE // TICKS)
 STEEPEST = 64.0
+PAIRED = (1, 3, 5)
 CHUNK_ORDER = (2, 3, 1, 0)
-LAST_WIDTHS = (512,) * 8
 LAST_ENGINES = ("AAAA",) * 5 + ("AAAV", "AVAV", "AVAV")
 
 FLOPS = 2 * EVENTS * FLASHES * CHANNELS * TICKS
@@ -196,7 +196,7 @@ def tile_flashrecomodel_t_kernel(tc, flashes_pe, flashes_time, flashes_confidenc
         def weigh(g, t0, width, helper):
             n, off = divmod(t0, CHUNK)
             if (g, n) not in wchs:
-                second = g == GROUPS - 1 and n % 2
+                second = g == GROUPS - 1 and CHUNK_ORDER.index(n) % 2
                 pool = late["c1pool"] if second else wchpool
                 wchs[(g, n)] = pool.tile([P, CHUNK, PACK], BF16, name="wch%d" % second, align_bytes=64)
             four = slice(g * PACK, (g + 1) * PACK)
@@ -220,12 +220,16 @@ def tile_flashrecomodel_t_kernel(tc, flashes_pe, flashes_time, flashes_confidenc
             n, off = divmod(t0, CHUNK)
             c = g % PASSES
             if off == 0:
-                pool = c0pool if c == 0 else late["c1pool"]
-                w_codes[(c, n)] = pool.tile([P, CHUNK], U32, name="w_codes%d_%d" % (c, n), align_bytes=64)
-                w_scales[(c, n)] = pool.tile([P, CHUNK], U8, name="w_scales%d_%d" % (c, n), align_bytes=64)
+                if (g, n) == (GROUPS - PASSES, CHUNK_ORDER[-1]):
+                    w_codes[(g, n)] = rawpool.tile([P, CHUNK], U32, name="w_codes_own", tag="raw_last", align_bytes=64)
+                    w_scales[(g, n)] = rawpool.tile([P, CHUNK], U8, name="w_scales_own", tag="spe", align_bytes=64)
+                else:
+                    pool = c0pool if c == 0 else late["c1pool"]
+                    w_codes[(g, n)] = pool.tile([P, CHUNK], U32, name="w_codes%d_%d" % (c, n), align_bytes=64)
+                    w_scales[(g, n)] = pool.tile([P, CHUNK], U8, name="w_scales%d_%d" % (c, n), align_bytes=64)
             nc.vector.quantize_mx(
-                out=w_codes[(c, n)][:, off : off + width].bitcast(FP8X4),
-                scales=w_scales[(c, n)][:, off : off + width],
+                out=w_codes[(g, n)][:, off : off + width].bitcast(FP8X4),
+                scales=w_scales[(g, n)][:, off : off + width],
                 in_=wchs[(g, n)][:, off : off + width, :].rearrange("p t j -> p (t j)"),
             )
 
@@ -245,8 +249,8 @@ def tile_flashrecomodel_t_kernel(tc, flashes_pe, flashes_time, flashes_confidenc
                 out=acc[:, 0:nw],
                 lhsT=pe_codes[b * PASSES + c][:, m_cols].bitcast(FP8X4),
                 lhsT_scale=pe_scales[b * PASSES + c][:, m_cols],
-                rhs=w_codes[(c, n)][:, off : off + nw].bitcast(FP8X4),
-                rhs_scale=w_scales[(c, n)][:, off : off + nw],
+                rhs=w_codes[(b * PASSES + c, n)][:, off : off + nw].bitcast(FP8X4),
+                rhs_scale=w_scales[(b * PASSES + c, n)][:, off : off + nw],
                 start=(c == 0),
                 stop=(c == PASSES - 1),
             )
@@ -257,7 +261,7 @@ def tile_flashrecomodel_t_kernel(tc, flashes_pe, flashes_time, flashes_confidenc
             for m in (2 * (v % 2), 2 * (v % 2) + 1):
                 accs = []
                 for x in range(CHUNK // N_TILE):
-                    acc = bank(False)
+                    acc = bank(v == 7)
                     for c in range(PASSES):
                         mx_pass(0, c, m, n * CHUNK + x * N_TILE, acc, N_TILE)
                     accs.append(acc)
@@ -265,10 +269,10 @@ def tile_flashrecomodel_t_kernel(tc, flashes_pe, flashes_time, flashes_confidenc
             return todo
 
         def empty(v, engine):
-            if v % 2:
+            if v in PAIRED:
                 pair = late["c1pool"].tile([P, 2, CHUNK], F32, name="pair", tag="wch1", align_bytes=64)
             for a, (m, n, accs) in enumerate(todos[v]):
-                stage = pair[:, a, :] if v % 2 else late["stpool"].tile([P, CHUNK], F32, name="stage")[:]
+                stage = pair[:, a, :] if v in PAIRED else late["stpool"].tile([P, CHUNK], F32, name="stage")[:]
                 for x, acc in enumerate(accs):
                     engine(out=stage[:, x * N_TILE : (x + 1) * N_TILE], in_=acc[:])
                 nc.sync.dma_start(out=out[1, m * P : (m + 1) * P, n * CHUNK : (n + 1) * CHUNK], in_=stage)
@@ -280,7 +284,7 @@ def tile_flashrecomodel_t_kernel(tc, flashes_pe, flashes_time, flashes_confidenc
             quantise(g, n * CHUNK, CHUNK)
 
         rawpool = ctx.enter_context(tc.tile_pool(name="rawpool", bufs=1))
-        raw_last = rawpool.tile([P, PASSES, PACK, CHANNELS], BF16)
+        raw_last = rawpool.tile([P, PASSES, PACK, CHANNELS], BF16, name="raw_last", align_bytes=64)
         spes = {}
 
         with tc.tile_pool(name="prep", bufs=1) as prep:
@@ -638,8 +642,8 @@ def tile_flashrecomodel_t_kernel(tc, flashes_pe, flashes_time, flashes_confidenc
             gather(12)
             weigh(1, CHUNK, WINDOW - CHUNK, 0)
             exp_window(11)
-            exp_rest(9)
             empty(1, nc.scalar.copy)
+            exp_rest(9)
             codes(1, 1)
             todos[2] = unit(2)
             chunk(1, 0, 432)
@@ -678,20 +682,18 @@ def tile_flashrecomodel_t_kernel(tc, flashes_pe, flashes_time, flashes_confidenc
             todos[6] = unit(6)
             chunk(2, 0, 256)
             exp_rest(14)
-            empty(6, nc.scalar.copy)
             exp_rest(15)
+            banks[0] = 4
             todos[7] = unit(7)
+            banks[0] = 0
+            empty(6, nc.scalar.copy)
             empty(7, nc.scalar.copy)
             codes(2, 0)
             sum_group(3)
             invert_group(3)
 
             g_last = GROUPS - 1
-            blocks = []
-            begin = 0
-            for width in LAST_WIDTHS:
-                blocks.append((begin, width))
-                begin += width
+            blocks = [(n * CHUNK + begin, N_TILE) for n in CHUNK_ORDER for begin in (0, N_TILE)]
             lasts = {}
             early = nearpool.tile([P, CHANNELS // P, WINDOW], F32, name="near")
             later = farpool.tile([P, CHANNELS // P, REST], F32, name="far")

from contextlib import ExitStack

import concourse.bass as bass
import concourse.mybir as mybir
from concourse.masks import make_identity

F32 = mybir.dt.float32
BF16 = mybir.dt.bfloat16
U32 = mybir.dt.uint32
U8 = mybir.dt.uint8
I32 = mybir.dt.int32
FP8X4 = mybir.dt.float8_e4m3fn_x4
ACT = mybir.ActivationFunctionType
ALU = mybir.AluOpType
AX = mybir.AxisListType

P = 128
PACK = 4
EVENTS = 2
FLASHES = 1024
CHANNELS = 512
TICKS = 4096
K_PASS = P * PACK
PASSES = FLASHES // K_PASS
GROUPS = EVENTS * PASSES
TILES = GROUPS * PACK
CHUNK = 1024
N_CHUNKS = TICKS // CHUNK
N_TILE = 512
WINDOW = 1536
W_BANKS = WINDOW // N_TILE
TABLE = WINDOW + N_TILE
T_BLOCKS = TABLE // P
PIECES = 10
REST = TICKS - WINDOW
SEED = 512
WIDER = (1, 2, 3)
VECTOR_TILES = (1, 2, 3)
PHASE_BITS = 5
PHASES = 2**PHASE_BITS
SEGMENTS = P // PHASES
FRACTION_TICKS = 128
FIRST = WINDOW - FRACTION_TICKS
RAMP = TICKS - FIRST
COPIES = 8
SEGMENT = RAMP // SEGMENTS
LINE = 6656
LINE_COLS = LINE // P
TABLE_SIZE = PHASES * RAMP + COPIES * LINE
TABLE_ROWS = -(-TABLE_SIZE // TICKS)
STEEPEST = 64.0
PAIRED = (1, 3, 5)
CHUNK_ORDER = (2, 3, 1, 0)
LAST_ENGINES = ("AAAA",) * 5 + ("AAAV", "AVAV", "AVAV")

FLOPS = 2 * EVENTS * FLASHES * CHANNELS * TICKS


def tile_flashrecomodel_t_kernel(tc, flashes_pe, flashes_time, flashes_confidence, num_ticks, sigma, out):
    nc = tc.nc
    assert num_ticks == TICKS
    with ExitStack() as ctx:
        ctx.enter_context(tc.manual_schedule())
        const = ctx.enter_context(tc.tile_pool(name="const", bufs=1))
        nearpool = ctx.enter_context(tc.tile_pool(name="nearpool", bufs=2))
        farpool = ctx.enter_context(tc.tile_pool(name="farpool", bufs=2))
        wchpool = ctx.enter_context(tc.tile_pool(name="wchpool", bufs=1))
        c0pool = ctx.enter_context(tc.tile_pool(name="c0pool", bufs=1))
        dqpool = ctx.enter_context(tc.psum_pool(name="dqpool", bufs=1))
        accpool = ctx.enter_context(tc.psum_pool(name="accpool", bufs=4))

        ramp = const.tile([P, RAMP], F32)
        ticks = ramp[:, FRACTION_TICKS:RAMP]
        starts = const.tile([P, TILES], I32)
        negc = const.tile([P, TILES], F32)
        neg_2c = const.tile([P, TILES], F32)
        neg_h = const.tile([P, 1], F32)
        neg_v = const.tile([P, 1], F32)
        beta = const.tile([P, TILES], F32)
        eta = const.tile([P, TILES], F32)
        parts = const.tile([P, TILES, W_BANKS + 3], F32)
        sums = const.tile([P, TILES], F32)
        recip = const.tile([P, TILES], F32)
        factors_ps = dqpool.tile([P, 2 * TILES], F32, name="factors_ps")
        recip_ps = factors_ps[:, 0:TILES]
        cf_ps = factors_ps[:, TILES : 2 * TILES]
        ident = const.tile([P, P], BF16)
        ident_f = const.tile([P, P], F32)
        tokens = const.tile([P, 32 * PACK], F32)
        tokens_used = [0]
        tick_rows = const.tile([P, TABLE], BF16)
        flash_rows = [const.tile([P, 8 * P], BF16, name="flash_rows%d" % a) for a in range(2)]
        pe_codes = []
        pe_scales = []
        for g in range(GROUPS):
            pe_codes.append(const.tile([P, CHANNELS], U32, name="pe_codes%d" % g, align_bytes=64))
            pe_scales.append(const.tile([P, CHANNELS], U8, name="pe_scales%d" % g, align_bytes=64))

        near = {}
        far = {}
        dqs = {}
        wchs = {}
        w_codes = {}
        w_scales = {}
        late = {}
        todos = {}

        def near_group(g):
            if g not in near:
                near[g] = nearpool.tile([P, PACK, WINDOW], F32, name="near")
            return near[g]

        def far_group(g):
            if g not in far:
                far[g] = farpool.tile([P, PACK, REST], F32, name="far")
            return far[g]

        def rest_of(i):
            lo = N_TILE if i in WIDER else 0
            return lo, far_group(i // PACK)[:, i % PACK, lo:REST]

        def token(src):
            width = src.shape[1]
            dst = tokens[:, tokens_used[0] * PACK : tokens_used[0] * PACK + width]
            tokens_used[0] += 1
            nc.vector.tensor_copy(out=dst, in_=src)
            return dst

        def square_vector(i):
            lo, gt = rest_of(i)
            nc.vector.scalar_tensor_tensor(
                out=gt, in0=ticks[:, lo:REST], scalar=neg_2c[:, i : i + 1], in1=ticks[:, lo:REST], op0=ALU.add,
                op1=ALU.mult,
            )

        def square_scalar(i):
            lo, gt = rest_of(i)
            nc.scalar.activation(out=gt, in_=ticks[:, lo:REST], func=ACT.Square, bias=negc[:, i : i + 1], scale=1.0)

        table = out[0, 0:TABLE_ROWS, :]

        def gather(i):
            nc.gpsimd.indirect_dma_start(
                out=rest_of(i)[1], out_offset=None, in_=table,
                in_offset=bass.IndirectOffsetOnAxis(ap=starts[:, i : i + 1], axis=1),
            )

        def exp_rest(i):
            gt = rest_of(i)[1]
            scale, bias = (neg_v, beta) if i in VECTOR_TILES else (neg_h, eta)
            nc.scalar.activation(
                out=gt, in_=gt, func=ACT.Exp, scale=scale[:, 0:1], bias=bias[:, i : i + 1],
                accum_out=parts[:, i, W_BANKS : W_BANKS + 1],
            )

        def square_tensor(i, u):
            if u < W_BANKS:
                dq = dqpool.tile([P, N_TILE], F32, name="dq%d" % u)
            else:
                dq = accpool.tile([P, N_TILE], F32, name="dq_wider", tag="acc")
            dqs[(i, u)] = dq
            nc.tensor.matmul(
                out=dq[:],
                lhsT=flash_rows[i // 8][:, (i % 8) * P : (i % 8 + 1) * P],
                rhs=tick_rows[:, u * N_TILE : (u + 1) * N_TILE],
                start=True,
                stop=True,
            )

        def exp_bank(i, u):
            g, j = divmod(i, PACK)
            if u < W_BANKS:
                column, dst = u, near_group(g)[:, j, u * N_TILE : (u + 1) * N_TILE]
            else:
                column, dst = W_BANKS + 1, far_group(g)[:, j, 0:N_TILE]
            nc.scalar.activation(
                out=dst, in_=dqs[(i, u)][:], func=ACT.Exp, scale=neg_h[:, 0:1], bias=eta[:, i : i + 1],
                accum_out=parts[:, i, column : column + 1],
            )

        def exp_window(i):
            for u in range(W_BANKS):
                exp_bank(i, u)
                if i + 1 < TILES:
                    square_tensor(i + 1, u)

        def sum_group(g):
            four = slice(g * PACK, (g + 1) * PACK)
            nc.vector.reduce_sum(out=sums[:, four], in_=parts[:, four, :], axis=AX.X)

        def invert_group(g):
            four = slice(g * PACK, (g + 1) * PACK)
            nc.vector.reciprocal(out=recip[:, four], in_=sums[:, four])
            nc.tensor.matmul(out=recip_ps[:, four], lhsT=ident_f[:], rhs=recip[:, four], start=True, stop=True)

        def weigh(g, t0, width, helper):
            n, off = divmod(t0, CHUNK)
            if (g, n) not in wchs:
                second = g == GROUPS - 1 and CHUNK_ORDER.index(n) % 2
                pool = late["c1pool"] if second else wchpool
                wchs[(g, n)] = pool.tile([P, CHUNK, PACK], BF16, name="wch%d" % second, align_bytes=64)
            four = slice(g * PACK, (g + 1) * PACK)
            mine = width - helper
            src, s0 = (near[g], t0) if t0 < WINDOW else (far[g], t0 - WINDOW)
            if helper:
                nc.gpsimd.tensor_tensor(
                    out=wchs[(g, n)][:, off + mine : off + width, :].rearrange("p (c i) j -> p c j i", i=4),
                    in0=src[:, :, s0 + mine : s0 + width].rearrange("p j (c i) -> p c j i", i=4),
                    in1=(token(recip_ps[:, four]) if g == GROUPS - 1 else recip[:, four]).unsqueeze(1).unsqueeze(3).to_broadcast([P, helper // 4, PACK, 4]),
                    op=ALU.mult,
                )
            nc.vector.tensor_tensor(
                out=wchs[(g, n)][:, off : off + mine, :].rearrange("p (c i) j -> p c j i", i=4),
                in0=src[:, :, s0 : s0 + mine].rearrange("p j (c i) -> p c j i", i=4),
                in1=recip_ps[:, four].unsqueeze(1).unsqueeze(3).to_broadcast([P, mine // 4, PACK, 4]),
                op=ALU.mult,
            )

        def quantise(g, t0, width):
            n, off = divmod(t0, CHUNK)
            c = g % PASSES
            if off == 0:
                if (g, n) == (GROUPS - PASSES, CHUNK_ORDER[-1]):
                    w_codes[(g, n)] = rawpool.tile([P, CHUNK], U32, name="w_codes_own", tag="raw_last", align_bytes=64)
                    w_scales[(g, n)] = rawpool.tile([P, CHUNK], U8, name="w_scales_own", tag="spe", align_bytes=64)
                else:
                    pool = c0pool if c == 0 else late["c1pool"]
                    w_codes[(g, n)] = pool.tile([P, CHUNK], U32, name="w_codes%d_%d" % (c, n), align_bytes=64)
                    w_scales[(g, n)] = pool.tile([P, CHUNK], U8, name="w_scales%d_%d" % (c, n), align_bytes=64)
            nc.vector.quantize_mx(
                out=w_codes[(g, n)][:, off : off + width].bitcast(FP8X4),
                scales=w_scales[(g, n)][:, off : off + width],
                in_=wchs[(g, n)][:, off : off + width, :].rearrange("p t j -> p (t j)"),
            )

        banks = [0]

        def bank(all_seven):
            q = banks[0] % 7
            banks[0] += 1
            if all_seven and q >= 4:
                return dqpool.tile([P, N_TILE], F32, name="acc_dq", tag="dq%d" % (q - 4))
            return accpool.tile([P, N_TILE], F32, name="acc")

        def mx_pass(b, c, m, t0, acc, nw):
            n, off = divmod(t0, CHUNK)
            m_cols = slice(m * P, (m + 1) * P)
            nc.tensor.matmul_mx(
                out=acc[:, 0:nw],
                lhsT=pe_codes[b * PASSES + c][:, m_cols].bitcast(FP8X4),
                lhsT_scale=pe_scales[b * PASSES + c][:, m_cols],
                rhs=w_codes[(b * PASSES + c, n)][:, off : off + nw].bitcast(FP8X4),
                rhs_scale=w_scales[(b * PASSES + c, n)][:, off : off + nw],
                start=(c == 0),
                stop=(c == PASSES - 1),
            )

        def unit(v):
            n = CHUNK_ORDER[v // 2]
            todo = []
            for m in (2 * (v % 2), 2 * (v % 2) + 1):
                accs = []
                for x in range(CHUNK // N_TILE):
                    acc = bank(v == 7)
                    for c in range(PASSES):
                        mx_pass(0, c, m, n * CHUNK + x * N_TILE, acc, N_TILE)
                    accs.append(acc)
                todo.append((m, n, accs))
            return todo

        def empty(v, engine):
            if v in PAIRED:
                pair = late["c1pool"].tile([P, 2, CHUNK], F32, name="pair", tag="wch1", align_bytes=64)
            for a, (m, n, accs) in enumerate(todos[v]):
                stage = pair[:, a, :] if v in PAIRED else late["stpool"].tile([P, CHUNK], F32, name="stage")[:]
                for x, acc in enumerate(accs):
                    engine(out=stage[:, x * N_TILE : (x + 1) * N_TILE], in_=acc[:])
                nc.sync.dma_start(out=out[1, m * P : (m + 1) * P, n * CHUNK : (n + 1) * CHUNK], in_=stage)

        def chunk(g, n, helper):
            weigh(g, n * CHUNK, CHUNK, helper)

        def codes(g, n):
            quantise(g, n * CHUNK, CHUNK)

        rawpool = ctx.enter_context(tc.tile_pool(name="rawpool", bufs=1))
        raw_last = rawpool.tile([P, PASSES, PACK, CHANNELS], BF16, name="raw_last", align_bytes=64)
        spes = {}

        with tc.tile_pool(name="prep", bufs=1) as prep:
            per_event = TILES // EVENTS
            tm_bf = prep.tile([P, EVENTS, 2 * per_event], BF16)
            for b in range(EVENTS):
                nc.sync.dma_start(
                    out=tm_bf[:, b, 0:per_event].rearrange("p (c j) -> p c j", j=PACK),
                    in_=flashes_time[EVENTS - 1 - b].rearrange("(c p j) o -> p c (j o)", p=P, j=PACK),
                )
            sig_bf = prep.tile([P, 1], BF16)
            nc.sync.dma_start(out=sig_bf[:], in_=sigma.partition_broadcast(P))
            cf_bf = prep.tile([P, EVENTS, 2 * per_event], BF16)
            for b in range(EVENTS):
                nc.sync.dma_start(
                    out=cf_bf[:, b, 0:per_event].rearrange("p (c j) -> p c j", j=PACK),
                    in_=flashes_confidence[EVENTS - 1 - b].rearrange("(c p j) o -> p c (j o)", p=P, j=PACK),
                )
            raw_first = prep.tile([P, PASSES, PACK, CHANNELS], BF16)
            for g in range(GROUPS):
                b, c = EVENTS - 1 - g // PASSES, g % PASSES
                nc.sync.dma_start(
                    out=(raw_first if g < PASSES else raw_last)[:, c].rearrange("p j w -> p (j w)"),
                    in_=flashes_pe[b, c * K_PASS : (c + 1) * K_PASS, :].rearrange("(p j) w -> p (j w)", j=PACK),
                )

            warm = prep.tile([P, 1], F32)
            nc.gpsimd.memset(warm[:], 0.0)
            tick_i = prep.tile([P, SEED], I32)
            nc.gpsimd.iota(tick_i[:], pattern=[[1, SEED]], base=FIRST, channel_multiplier=0)
            tcol_i = prep.tile([P, T_BLOCKS], I32)
            nc.gpsimd.iota(tcol_i[:], pattern=[[P, T_BLOCKS]], base=0, channel_multiplier=1)
            make_identity(nc, ident[:])
            line_i = prep.tile([P, LINE_COLS], I32)
            nc.gpsimd.iota(line_i[:], pattern=[[1, LINE_COLS]], base=WINDOW + 1 - TICKS, channel_multiplier=LINE_COLS)
            part_i = prep.tile([P, 1], I32)
            nc.gpsimd.iota(part_i[:], pattern=[[1, 1]], base=0, channel_multiplier=1)

            warm_out = prep.tile([P, 1], F32)
            nc.scalar.activation(out=warm_out[:], in_=warm[:], func=ACT.Exp)
            nc.scalar.copy(out=ident_f[:], in_=ident[:])

            tick_cols = prep.tile([P, T_BLOCKS * PIECES + P], BF16)
            tick_pieces = tick_cols[:, 0 : T_BLOCKS * PIECES].rearrange("p (a k) -> p a k", k=PIECES)
            flash_cols = prep.tile([P, TILES, P], BF16)
            nc.vector.memset(flash_cols[:].rearrange("p a k -> p (a k)").bitcast(I32), 0)
            nc.vector.memset(tick_cols[:, T_BLOCKS * PIECES :].bitcast(I32), 0)

            def cast(dst, src):
                return lambda: nc.vector.tensor_copy(out=dst, in_=src)

            def twice(src, count):
                return src.unsqueeze(2).to_broadcast([P, count, 2])

            def combine(dst, in0, in1, op):
                return lambda: nc.vector.tensor_tensor(out=dst, in0=in0, in1=in1, op=op)

            def scale(dst, src, factor):
                return lambda: nc.vector.tensor_scalar_mul(out=dst, in0=src, scalar1=factor)

            def add_product(dst, x, factor, y):
                return lambda: nc.vector.scalar_tensor_tensor(
                    out=dst, in0=x, scalar=factor, in1=y, op0=ALU.mult, op1=ALU.add
                )

            def in_turn(*chains):
                for step in range(max(len(chain) for chain in chains)):
                    for chain in chains:
                        if step < len(chain):
                            chain[step]()

            tcol = prep.tile([P, T_BLOCKS], F32)

            def doubling(have, more):
                return lambda: nc.vector.tensor_scalar_add(
                    out=ramp[:, have : have + more], in0=ramp[:, 0:more], scalar1=float(have)
                )

            growth = [cast(ramp[:, 0:SEED], tick_i[:])]
            have = SEED
            while have < RAMP:
                more = min(have, RAMP - have)
                growth.append(doubling(have, more))
                have += more
            in_turn(
                growth,
                [
                    cast(tcol[:], tcol_i[:]),
                    lambda: nc.vector.memset(tick_pieces[:, :, 7:10], 1.0),
                    lambda: nc.vector.memset(flash_cols[:, :, 0:3], 1.0),
                    lambda: nc.vector.memset(parts[:].rearrange("p a k -> p (a k)"), 0.0),
                ],
            )

            sig2 = prep.tile([P, 1], F32)
            inv2 = prep.tile([P, 1], F32)
            t_sq = prep.tile([P, T_BLOCKS], F32)
            nc.vector.tensor_scalar(
                out=negc[:].rearrange("p (b i) -> p b i", b=EVENTS), in0=tm_bf[:, :, 0:per_event],
                scalar1=-float(TICKS), scalar2=0.0, op0=ALU.mult, op1=ALU.min,
            )
            nc.vector.tensor_tensor(out=t_sq[:], in0=tcol[:], in1=tcol[:], op=ALU.mult)
            nc.vector.tensor_scalar_max(out=negc[:], in0=negc[:], scalar1=-float(TICKS - 1))
            nc.vector.tensor_tensor(out=sig2[:], in0=sig_bf[:], in1=sig_bf[:], op=ALU.mult)

            t_rem1 = prep.tile([P, T_BLOCKS], F32)
            t_rem2 = prep.tile([P, T_BLOCKS], F32)
            t_lo = prep.tile([P, T_BLOCKS], F32)
            a_lo = prep.tile([P, TILES], F32)
            c_sq = prep.tile([P, TILES], F32)
            c_rem1 = prep.tile([P, TILES], F32)
            c_rem2 = prep.tile([P, TILES], F32)
            h_v = prep.tile([P, 1], F32)
            h_hi = prep.tile([P, 1], BF16)
            h_lo = prep.tile([P, 1], F32)
            rest1 = prep.tile([P, TILES], F32)
            rest2 = prep.tile([P, TILES], F32)
            rest3 = prep.tile([P, TILES], F32)
            exp_eta = prep.tile([P, TILES], F32)
            in_turn(
                [
                    lambda: nc.vector.reciprocal(out=inv2[:], in_=sig2[:]),
                    lambda: nc.vector.tensor_scalar(
                        out=h_v[:], in0=inv2[:], scalar1=0.5, scalar2=STEEPEST, op0=ALU.mult, op1=ALU.min
                    ),
                    scale(neg_v[:], h_v[:], -1.0),
                    cast(h_hi[:], h_v[:]),
                    scale(beta[:], c_sq[:], neg_v[:, 0:1]),
                    combine(h_lo[:], h_v[:], h_hi[:], ALU.subtract),
                    add_product(rest1[:], flash_cols[:, :, 7], h_hi[:, 0:1], beta[:]),
                    scale(neg_h[:], inv2[:], -0.5),
                    add_product(rest2[:], c_rem1[:], h_hi[:, 0:1], rest1[:]),
                    add_product(rest3[:], flash_cols[:, :, 7], h_lo[:, 0:1], rest2[:]),
                    add_product(eta[:], c_rem1[:], h_lo[:, 0:1], rest3[:]),
                ],
                [
                    combine(c_sq[:], negc[:], negc[:], ALU.mult),
                    cast(flash_cols[:, :, 7], c_sq[:]),
                    combine(c_rem1[:], c_sq[:], flash_cols[:, :, 7], ALU.subtract),
                    cast(flash_cols[:, :, 8], c_rem1[:]),
                    combine(c_rem2[:], c_rem1[:], flash_cols[:, :, 8], ALU.subtract),
                    cast(flash_cols[:, :, 9], c_rem2[:]),
                ],
                [
                    scale(neg_2c[:], negc[:], 2.0),
                    cast(flash_cols[:, :, 3:5], twice(neg_2c[:], TILES)),
                    combine(a_lo[:], neg_2c[:], flash_cols[:, :, 3], ALU.subtract),
                    cast(flash_cols[:, :, 5:7], twice(a_lo[:], TILES)),
                ],
                [
                    cast(tick_pieces[:, :, 0], t_sq[:]),
                    combine(t_rem1[:], t_sq[:], tick_pieces[:, :, 0], ALU.subtract),
                    cast(tick_pieces[:, :, 1], t_rem1[:]),
                    combine(t_rem2[:], t_rem1[:], tick_pieces[:, :, 1], ALU.subtract),
                    cast(tick_pieces[:, :, 2], t_rem2[:]),
                ],
                [
                    cast(tick_pieces[:, :, 3:6:2], twice(tcol[:], T_BLOCKS)),
                    combine(t_lo[:], tcol[:], tick_pieces[:, :, 3], ALU.subtract),
                    cast(tick_pieces[:, :, 4:7:2], twice(t_lo[:], T_BLOCKS)),
                ],
            )

            square_scalar(0)
            exp_rest(0)
            nc.scalar.activation(out=exp_eta[:], in_=eta[:], func=ACT.Exp)

            cf_f = prep.tile([P, TILES], F32)

            def scale_pe(g):
                spes[g] = rawpool.tile([P, CHANNELS, PACK], BF16, name="spe", align_bytes=64)
                raw = (raw_first if g < PASSES else raw_last)[:, g % PASSES]
                nc.vector.tensor_tensor(
                    out=spes[g][:].rearrange("p (c i) j -> p c j i", i=4),
                    in0=raw.rearrange("p j (c i) -> p c j i", i=4),
                    in1=cf_ps[:, g * PACK : (g + 1) * PACK].unsqueeze(1).unsqueeze(3).to_broadcast(
                        [P, CHANNELS // 4, PACK, 4]
                    ),
                    op=ALU.mult,
                )

            def quantise_pe(g):
                nc.vector.quantize_mx(
                    out=pe_codes[g][:].bitcast(FP8X4), scales=pe_scales[g][:],
                    in_=spes[g][:].rearrange("p w j -> p (w j)"),
                )

            tabs = []
            for a in range(4):
                tabs.append(accpool.tile([P, 8 * P], BF16, name="tab%d" % a, tag="acc"))
            for a in range(T_BLOCKS):
                nc.tensor.transpose(
                    tabs[a // 8][:, (a % 8) * P : (a % 8 + 1) * P], tick_cols[:, a * PIECES : a * PIECES + P], ident[:]
                )
            for a in range(8):
                nc.tensor.transpose(tabs[2][:, a * P : (a + 1) * P], flash_cols[:, a, :], ident[:])
            nc.vector.tensor_copy(
                out=cf_f[:].rearrange("p (b i) -> p b i", b=EVENTS), in_=cf_bf[:, :, 0:per_event]
            )
            nc.tensor.matmul(out=cf_ps, lhsT=ident_f[:], rhs=cf_f[:], start=True, stop=True)
            part = prep.tile([P, 1], F32)
            minus_phase = prep.tile([P, 1], F32)
            segment_i = prep.tile([P, 1], I32)
            segment_f = prep.tile([P, 1], F32)
            copy_i = prep.tile([P, 1], I32)
            copy_start = prep.tile([P, 1], F32)
            line = prep.tile([P, LINE_COLS], F32)
            line_sq = prep.tile([P, LINE_COLS], F32)
            m_f = prep.tile([P, TILES], F32)
            m_i = prep.tile([P, TILES], I32)
            phase_i = prep.tile([P, TILES], I32)
            whole_i = prep.tile([P, TILES], I32)
            phase_f = prep.tile([P, TILES], F32)
            whole_f = prep.tile([P, TILES], F32)
            on_phase = prep.tile([P, TILES], F32)
            on_line = prep.tile([P, TILES], F32)
            gap = prep.tile([P, TILES], F32)
            starts_f = prep.tile([P, TILES], F32)
            flat = table.rearrange("a b -> (a b)")

            def fractions():
                phases = far_group(1)[:, 0, 0:SEGMENT]
                nc.vector.tensor_scalar_add(out=phases, in0=ramp[:, 0:SEGMENT], scalar1=minus_phase[:, 0:1])
                nc.vector.tensor_tensor(out=line_sq[:], in0=line[:], in1=line[:], op=ALU.mult)
                nc.vector.tensor_tensor(out=phases, in0=phases, in1=phases, op=ALU.mult)
                nc.sync.dma_start(
                    out=flat[PHASES * RAMP :].rearrange("(q p k) -> p q k", q=COPIES, p=P),
                    in_=line_sq[:].unsqueeze(1).to_broadcast([P, COPIES, LINE_COLS]),
                )
                by_segment = flat[0 : PHASES * RAMP].rearrange("(f h k) -> h f k", h=SEGMENTS, k=SEGMENT)
                for s in range(SEGMENTS):
                    nc.sync.dma_start(out=by_segment[s], in_=phases[s * PHASES : (s + 1) * PHASES, :])

            def find_starts():
                in_turn(
                    [
                        scale(m_f[:], negc[:], -float(PHASES)),
                        cast(m_i[:], m_f[:]),
                        lambda: nc.vector.tensor_single_scalar(phase_i[:], m_i[:], PHASES - 1, op=ALU.bitwise_and),
                        lambda: nc.vector.tensor_single_scalar(whole_i[:], m_i[:], PHASE_BITS, op=ALU.arith_shift_right),
                        cast(phase_f[:], phase_i[:]),
                        lambda: nc.vector.tensor_scalar_add(
                            out=whole_f[:], in0=whole_i[:], scalar1=-float(FRACTION_TICKS)
                        ),
                        lambda: nc.vector.scalar_tensor_tensor(
                            out=on_phase[:], in0=phase_f[:], scalar=float(RAMP), in1=whole_f[:], op0=ALU.mult,
                            op1=ALU.subtract,
                        ),
                        combine(gap[:], on_line[:], on_phase[:], ALU.subtract),
                        lambda: nc.vector.scalar_tensor_tensor(
                            out=gap[:], in0=negc[:], scalar=-float(FRACTION_TICKS), in1=gap[:], op0=ALU.is_le,
                            op1=ALU.mult,
                        ),
                        combine(starts_f[:], on_phase[:], gap[:], ALU.add),
                        cast(starts[:], starts_f[:]),
                    ],
                    [
                        cast(part[:], part_i[:]),
                        lambda: nc.vector.tensor_single_scalar(copy_i[:], part_i[:], COPIES - 1, op=ALU.bitwise_and),
                        lambda: nc.vector.tensor_single_scalar(
                            segment_i[:], part_i[:], PHASE_BITS, op=ALU.arith_shift_right
                        ),
                        lambda: nc.vector.tensor_scalar(
                            out=copy_start[:], in0=copy_i[:], scalar1=float(LINE),
                            scalar2=float(PHASES * RAMP + TICKS - 1), op0=ALU.mult, op1=ALU.add,
                        ),
                        lambda: nc.vector.tensor_scalar_mul(
                            out=segment_f[:], in0=segment_i[:], scalar1=float(SEGMENT + 1)
                        ),
                        lambda: nc.vector.tensor_scalar_add(out=on_line[:], in0=negc[:], scalar1=copy_start[:, 0:1]),
                        cast(line[:], line_i[:]),
                        lambda: nc.vector.scalar_tensor_tensor(
                            out=minus_phase[:], in0=part[:], scalar=-1.0 / PHASES, in1=segment_f[:], op0=ALU.mult,
                            op1=ALU.add,
                        ),
                    ],
                )

            square_vector(1)
            exp_rest(1)
            nc.vector.tensor_copy(out=tick_rows[:, 0 : 8 * P], in_=tabs[0][:])
            nc.vector.tensor_copy(out=tick_rows[:, 8 * P : TABLE], in_=tabs[1][:])
            nc.vector.tensor_copy(out=flash_rows[0][:], in_=tabs[2][:])
            for u in range(W_BANKS):
                square_tensor(0, u)
            for a in range(8):
                nc.tensor.transpose(tabs[3][:, a * P : (a + 1) * P], flash_cols[:, 8 + a, :], ident[:])
            square_tensor(1, W_BANKS)
            find_starts()
            fractions()
            square_vector(2)
            gather(5)
            gather(6)
            gather(7)
            square_vector(3)
            nc.vector.tensor_scalar_mul(out=parts[:, :, W_BANKS + 2], in0=exp_eta[:], scalar1=1e-10)
            nc.vector.tensor_copy(out=flash_rows[1][:], in_=tabs[3][:])
            exp_window(0)
            exp_bank(1, W_BANKS)
            square_tensor(2, W_BANKS)
            exp_window(1)
            exp_bank(2, W_BANKS)
            square_tensor(3, W_BANKS)
            exp_window(2)
            exp_rest(2)
            exp_window(3)
            exp_bank(3, W_BANKS)
            exp_rest(3)
            scale_pe(0)
            quantise_pe(0)
            scale_pe(1)
            sum_group(0)
            invert_group(0)
            chunk(0, 2, 256)
            quantise_pe(1)
            exp_window(4)
            square_scalar(4)
            exp_window(5)
            exp_rest(4)
            codes(0, 2)
            chunk(0, 3, 256)
            exp_window(6)
            exp_rest(5)
            codes(0, 3)
            weigh(0, WINDOW, 2 * CHUNK - WINDOW, 256)
            gather(8)
            weigh(0, CHUNK, WINDOW - CHUNK, 0)
            exp_window(7)
            exp_rest(6)
            codes(0, 1)
            chunk(0, 0, 256)
            gather(9)
            exp_rest(7)
            codes(0, 0)

        with tc.tile_pool(name="c1pool", bufs=1) as c1pool, tc.tile_pool(name="stpool", bufs=3) as stpool:
            late["c1pool"] = c1pool
            late["stpool"] = stpool
            sum_group(1)
            invert_group(1)
            chunk(1, 2, 256)
            gather(10)
            exp_window(8)
            exp_window(9)
            codes(1, 2)
            todos[0] = unit(0)
            chunk(1, 3, 432)
            gather(11)
            empty(0, nc.vector.tensor_copy)
            exp_window(10)
            exp_rest(8)
            codes(1, 3)
            todos[1] = unit(1)
            weigh(1, WINDOW, 2 * CHUNK - WINDOW, 256)
            gather(12)
            weigh(1, CHUNK, WINDOW - CHUNK, 0)
            exp_window(11)
            empty(1, nc.scalar.copy)
            exp_rest(9)
            codes(1, 1)
            todos[2] = unit(2)
            chunk(1, 0, 432)
            gather(13)
            scale_pe(2)
            exp_rest(10)
            empty(2, nc.scalar.copy)
            quantise_pe(2)
            codes(1, 0)
            todos[3] = unit(3)
            exp_rest(11)
            sum_group(2)
            invert_group(2)
            chunk(2, 2, 256)
            gather(14)
            empty(3, nc.scalar.copy)
            exp_window(12)
            exp_window(13)
            codes(2, 2)
            todos[4] = unit(4)
            chunk(2, 3, 432)
            gather(15)
            empty(4, nc.vector.tensor_copy)
            exp_rest(12)
            exp_window(14)
            codes(2, 3)
            todos[5] = unit(5)
            weigh(2, WINDOW, 2 * CHUNK - WINDOW, 208)
            weigh(2, CHUNK, WINDOW - CHUNK, 208)
            scale_pe(3)
            exp_rest(13)
            exp_window(15)
            empty(5, nc.scalar.copy)
            quantise_pe(3)
            codes(2, 1)
            todos[6] = unit(6)
            chunk(2, 0, 256)
            exp_rest(14)
            exp_rest(15)
            banks[0] = 4
            todos[7] = unit(7)
            banks[0] = 0
            empty(6, nc.scalar.copy)
            empty(7, nc.scalar.copy)
            codes(2, 0)
            sum_group(3)
            invert_group(3)

            g_last = GROUPS - 1
            blocks = [(n * CHUNK + begin, N_TILE) for n in CHUNK_ORDER for begin in (0, N_TILE)]
            lasts = {}
            early = nearpool.tile([P, CHANNELS // P, WINDOW], F32, name="near")
            later = farpool.tile([P, CHANNELS // P, REST], F32, name="far")

            def weigh_last(x):
                if x < len(blocks):
                    t0, width = blocks[x]
                    weigh(g_last, t0, width, width * 5 // 16)

            def pass_last(x, c):
                t0, width = blocks[x]
                for m in range(CHANNELS // P):
                    mx_pass(1, c, m, t0, lasts[x][m], width)

            def open_last(x):
                if x < len(blocks):
                    lasts[x] = [bank(True) for m in range(CHANNELS // P)]
                    pass_last(x, 0)

            def empty_last(x):
                t0, width = blocks[x]
                result, s0 = (early, t0) if t0 < WINDOW else (later, t0 - WINDOW)
                for m in range(CHANNELS // P):
                    engine = nc.vector.tensor_copy if LAST_ENGINES[x][m] == "V" else nc.scalar.copy
                    engine(out=result[:, m, s0 : s0 + width], in_=lasts[x][m][:, 0:width])
                    if m % 2:
                        nc.sync.dma_start(
                            out=out[0, (m - 1) * P : (m + 1) * P, t0 : t0 + width].rearrange("(m p) t -> p m t", p=P),
                            in_=result[:, m - 1 : m + 1, s0 : s0 + width],
                        )

            open_last(0)
            weigh_last(0)
            quantise(g_last, blocks[0][0], blocks[0][1])
            pass_last(0, 1)
            open_last(1)
            weigh_last(1)
            for x in range(1, len(blocks)):
                weigh_last(x + 1)
                quantise(g_last, blocks[x][0], blocks[x][1])
                pass_last(x, 1)
                open_last(x + 1)
                empty_last(x - 1)
            empty_last(len(blocks) - 1)
